import numpy as np
import ml_dtypes


def mxq(x, axis, fmt="e4m3"):
    dtype, down = {"e4m3": (ml_dtypes.float8_e4m3fn, 7), "e5m2": (ml_dtypes.float8_e5m2, 14)}[fmt]
    v = np.moveaxis(np.asarray(x, np.float32).astype(ml_dtypes.bfloat16).astype(np.float64), axis, -1)
    blocks = v.reshape(v.shape[:-1] + (-1, 32))
    amax = np.abs(blocks).max(-1, keepdims=True)
    byte = np.maximum(np.where(amax > 0, np.frexp(amax)[1] - 1 + 127, 0) - down, 1)
    scale = np.exp2(byte - 127.0)
    codes = (blocks / scale).astype(np.float32).astype(dtype).astype(np.float64)
    return np.moveaxis((codes * scale).reshape(v.shape), -1, axis)


WIDE = False


def mx_kscale(k):
    if not WIDE:
        return np.ones(k)
    levels = np.array([10, -10, 5, -5, 0])
    a = np.random.permutation(np.resize(levels, k // 512 * 4)).reshape(k // 512, 4)
    idx = np.arange(k)
    return np.exp2(a[idx // 512, idx % 128 // 32])


BF16 = ml_dtypes.bfloat16


def bf(x):
    return np.asarray(x, np.float32).astype(BF16)


def f64(x):
    return np.asarray(x).astype(np.float64)


E2M1 = np.array([0.0, 0.5, 1.0, 1.5, 2.0, 3.0, 4.0, 6.0, -0.0, -0.5, -1.0, -1.5, -2.0, -3.0, -4.0, -6.0])


def pack_weight(w, fmt):
    k, n = w.shape
    w = f64(bf(w)).reshape(k // 32, 32, n)
    amax = np.abs(w).max(1)
    if fmt == "e4m3":
        byte = np.frexp(amax)[1] - 1 + 127 - 7
    else:
        mant, ex = np.frexp(amax / 6.0)
        byte = np.where(mant > 0.5, ex, ex - 1) + 127
    byte = np.clip(np.where(amax > 0, byte, 1), 1, 254)
    scaled = (w * np.exp2(127.0 - byte)[:, None, :]).reshape(k, n).astype(np.float32)
    by_word = np.ascontiguousarray(scaled.reshape(k // 512, 128, 4, n).transpose(0, 1, 3, 2))
    if fmt == "e4m3":
        words = by_word.astype(ml_dtypes.float8_e4m3fn).view(np.uint8)
    else:
        c = by_word.astype(ml_dtypes.float4_e2m1fn).view(np.uint8) & 0xF
        words = c[..., 0::2] | (c[..., 1::2] << 4)
    return np.ascontiguousarray(words), np.ascontiguousarray(byte.astype(np.uint8).reshape(k // 512, 16, n))


def unpack_weight(words, scales, fmt):
    g, p, n, _ = words.shape
    if fmt == "e4m3":
        vals = np.ascontiguousarray(words).view(ml_dtypes.float8_e4m3fn).astype(np.float64)
    else:
        nib = np.empty((g, p, n, 4), np.uint8)
        nib[..., 0::2] = words & 0xF
        nib[..., 1::2] = words >> 4
        vals = E2M1[nib]
    vals = vals * np.repeat(np.exp2(scales.astype(np.float64) - 127.0), 8, axis=1)[..., None]
    return vals.transpose(0, 1, 3, 2).reshape(g * 512, n)


B, Tq, Tk, C = 2, 512, 512, 1024
C2 = 2 * C
VAR_EPS = 1e-6
LN_EPS = 1e-5
FMT = "e4m3"


def layernorm(x, g, b):
    m = x.mean(-1, keepdims=True)
    v = ((x - m) ** 2).mean(-1, keepdims=True)
    return (x - m) / np.sqrt(v + LN_EPS) * g + b


def softplus(v):
    return np.log(1.0 + np.exp(v))


def setup_inputs():
    s = mx_kscale(C)
    w = 1.0 / np.sqrt(C)
    context = bf(np.random.standard_normal((B, Tk, C)) * s)
    eps_noise = bf(np.random.standard_normal((B, Tk, C)))
    Wk_words, Wk_scales = pack_weight(np.ascontiguousarray((np.random.standard_normal((C2, C)) * w / s).T), FMT)
    bk = bf(np.random.standard_normal(C2) * 0.2)
    Wv_words, Wv_scales = pack_weight(np.ascontiguousarray((np.random.standard_normal((C2, C)) * w / s).T), FMT)
    bv = bf(np.random.standard_normal(C2) * 0.2)
    return {"context": context,
            "eps_noise": eps_noise,
            "Wk_words": Wk_words,
            "Wk_scales": Wk_scales,
            "bk": bk,
            "Wv_words": Wv_words,
            "Wv_scales": Wv_scales,
            "bv": bv,
            "ln_k_g": bf(1.0 + 0.1 * np.random.standard_normal(C)),
            "ln_k_b": bf(np.random.standard_normal(C) * 0.2),
            "ln_v_g": bf(1.0 + 0.1 * np.random.standard_normal(C)),
            "ln_v_b": bf(np.random.standard_normal(C) * 0.2)}


def reference(context, eps_noise, Wk_words, Wk_scales, bk, Wv_words, Wv_scales, bv, ln_k_g, ln_k_b, ln_v_g, ln_v_b):
    cq = mxq(f64(context), 2, "e4m3")
    k_out = (cq @ unpack_weight(Wk_words, Wk_scales, FMT)) + f64(bk)
    k_mu = layernorm(k_out[..., :C], f64(ln_k_g), f64(ln_k_b))
    k_var = softplus(k_out[..., C:]) + VAR_EPS
    v_out = (cq @ unpack_weight(Wv_words, Wv_scales, FMT)) + f64(bv)
    v_mu = layernorm(v_out[..., :C], f64(ln_v_g), f64(ln_v_b))
    v_var = softplus(v_out[..., C:]) + VAR_EPS
    v_sample = v_mu + np.sqrt(v_var) * f64(eps_noise)
    return k_mu, k_var, v_sample

@@ -1,0 +1,345 @@
+from contextlib import ExitStack
+
+import concourse.mybir as mybir
+from concourse.masks import make_identity
+
+F32 = mybir.dt.float32
+BF16 = mybir.dt.bfloat16
+I32 = mybir.dt.int32
+U32 = mybir.dt.uint32
+U8 = mybir.dt.uint8
+FP8X4 = mybir.dt.float8_e4m3fn_x4
+ALU = mybir.AluOpType
+ACT = mybir.ActivationFunctionType
+AXIS = mybir.AxisListType
+
+P = 128
+PACK = 4
+K_PASS = P * PACK
+TOKENS = 1024
+C = 1024
+PASSES = C // K_PASS
+TILES = TOKENS // P
+BANK = 512
+HALVES = C // BANK
+GROUP = 4
+ROUNDS = TILES // GROUP
+PREP_AHEAD = 3
+VAR_EPS = 1e-6
+LN_EPS = 1e-5
+LINEAR_FROM = 20.0
+
+FLOPS = 2 * TOKENS * C * 4 * C
+
+KEY = 0
+VALUE = 1
+MEAN = 0
+VARIANCE = C
+
+
+def tile_probcrossattention_pa_kernel(
+    tc,
+    context,
+    eps_noise,
+    Wk_words,
+    Wk_scales,
+    bk,
+    Wv_words,
+    Wv_scales,
+    bv,
+    ln_k_g,
+    ln_k_b,
+    ln_v_g,
+    ln_v_b,
+    out_0,
+    out_1,
+    out_2,
+):
+    nc = tc.nc
+    context_rows = context.flatten_outer_dims().rearrange("(i p) c -> p i c", p=P)
+    noise_rows = eps_noise.flatten_outer_dims().rearrange("(i p) c -> p i c", p=P)
+    k_mu_rows = out_0.flatten_outer_dims()
+    k_var_rows = out_1.flatten_outer_dims()
+    v_sample_rows = out_2.flatten_outer_dims()
+    words_in = (Wk_words, Wv_words)
+    scales_in = (Wk_scales, Wv_scales)
+
+    with ExitStack() as stack:
+        keep = stack.enter_context(tc.tile_pool(name="keep", bufs=1))
+        work = stack.enter_context(tc.tile_pool(name="work", bufs=2))
+        psum = stack.enter_context(tc.psum_pool(name="psum", bufs=1))
+
+        context_raw = keep.tile([P, TILES, C], BF16)
+        noise = keep.tile([P, TILES, C], BF16)
+        context_codes = keep.tile([P, TILES, PASSES, P], U32, align_bytes=64)
+        context_scales = keep.tile([P, TILES, PASSES, P], U8, align_bytes=64)
+        weight_codes = keep.tile([P, 2, PASSES, 2 * C], U32, align_bytes=64)
+        weight_scales = keep.tile([P, 2 * C], U8, align_bytes=64)
+        bias_all = keep.tile([P, 2, 2 * C], BF16)
+        gain_k = keep.tile([P, C], BF16)
+        shift_k = keep.tile([P, C], BF16)
+        gain_v_sbuf = keep.tile([P, C], BF16)
+        shift_v_sbuf = keep.tile([P, C], BF16)
+        identity_f32 = keep.tile([P, P], F32)
+        identity_bf16 = keep.tile([P, P], BF16)
+        var_eps = keep.tile([P, 1], F32)
+        exp_var_eps = keep.tile([P, 1], F32)
+        minus_half = keep.tile([P, 2], F32)
+        gain_v = psum.tile([P, C], BF16)
+        shift_v = psum.tile([P, C], BF16)
+
+        nc.vector.memset(weight_scales[:].bitcast(I32), 0)
+        nc.vector.memset(var_eps[:], VAR_EPS)
+        nc.vector.memset(minus_half[:], -0.5)
+        make_identity(nc, identity_f32[:])
+        make_identity(nc, identity_bf16[:])
+
+        def load_context(i):
+            nc.sync.dma_start(out=context_raw[:, i, :], in_=context_rows[:, i, :])
+
+        def load_weight_section(weight, first_column):
+            for g in range(PASSES):
+                packed = words_in[weight][g].rearrange("p n t -> p (n t)")
+                nc.sync.dma_start(
+                    out=weight_codes[:, weight, g, first_column : first_column + C].bitcast(I32),
+                    in_=packed[:, PACK * first_column : PACK * (first_column + C)].bitcast(I32),
+                )
+
+        for i in range(PREP_AHEAD):
+            load_context(i)
+        for quadrant in range(4):
+            for weight in (KEY, VALUE):
+                first_row = 32 * quadrant + 8 * weight
+                nc.sync.dma_start(
+                    out=weight_scales[first_row : first_row + 8, :].bitcast(I32),
+                    in_=scales_in[weight][:, 4 * quadrant : 4 * quadrant + 4, :].bitcast(I32),
+                )
+        load_weight_section(KEY, VARIANCE)
+        load_weight_section(VALUE, VARIANCE)
+        load_weight_section(KEY, MEAN)
+        load_weight_section(VALUE, MEAN)
+        for i in range(PREP_AHEAD, TILES):
+            load_context(i)
+        for i in range(TILES):
+            nc.sync.dma_start(out=noise[:, i, :], in_=noise_rows[:, i, :])
+
+        nc.scalar.dma_start(out=bias_all[:, KEY, :], in_=bk.partition_broadcast(P))
+        nc.scalar.dma_start(out=bias_all[:, VALUE, :], in_=bv.partition_broadcast(P))
+        nc.scalar.dma_start(out=gain_k[:], in_=ln_k_g.partition_broadcast(P))
+        nc.scalar.dma_start(out=shift_k[:], in_=ln_k_b.partition_broadcast(P))
+        nc.scalar.dma_start(out=gain_v_sbuf[:], in_=ln_v_g.partition_broadcast(P))
+        nc.scalar.dma_start(out=shift_v_sbuf[:], in_=ln_v_b.partition_broadcast(P))
+        nc.scalar.activation(out=exp_var_eps[:], in_=var_eps[:], func=ACT.Exp)
+
+        mean_in_k = {}
+        mean_in_v = {}
+        var_in = {}
+        var_out = {}
+        minus_mean = {}
+        square_sum = {}
+        inv_std = {}
+        minus_mean_inv_std = {}
+
+        def quantise_context(i):
+            words = context_raw[:, i, :].bitcast(F32)
+            turned = psum.tile([P, PASSES * 2, P], F32)
+            for g in range(PASSES):
+                for u in range(2):
+                    nc.tensor.transpose(
+                        turned[:, 2 * g + u, :],
+                        words[:, 256 * g + u : 256 * (g + 1) : 2],
+                        identity_f32[:],
+                    )
+            grouped = work.tile([P, PASSES * P * PACK], BF16, align_bytes=64)
+            nc.scalar.copy(
+                out=grouped[:].bitcast(F32).rearrange("p (g r u) -> p g r u", g=PASSES, u=2),
+                in_=turned[:].rearrange("p (g u) r -> p g r u", u=2),
+            )
+            nc.vector.quantize_mx(
+                out=context_codes[:, i, :, :].rearrange("p g r -> p (g r)").bitcast(FP8X4),
+                scales=context_scales[:, i, :, :].rearrange("p g r -> p (g r)"),
+                in_=grouped[:],
+            )
+
+        def product(i, weight, first_column):
+            columns = slice(first_column, first_column + BANK)
+            bank = psum.tile([P, BANK], F32, bufs=5)
+            for g in range(PASSES):
+                plane_row = 4 * (PASSES * weight + g)
+                nc.tensor.matmul_mx(
+                    out=bank[:],
+                    lhsT=context_codes[:, i, g, :].bitcast(FP8X4),
+                    lhsT_scale=context_scales[:, i, g, :],
+                    rhs=weight_codes[:, weight, g, columns].bitcast(FP8X4),
+                    rhs_scale=weight_scales[plane_row:P, columns],
+                    start=(g == 0),
+                    stop=(g == PASSES - 1),
+                )
+            return bank
+
+        def project(i):
+            v = work.tile([P, 2, C], F32, bufs=GROUP + 1)
+            for weight in (KEY, VALUE):
+                for h in range(HALVES):
+                    bank = product(i, weight, VARIANCE + h * BANK)
+                    nc.vector.tensor_tensor(
+                        out=v[:, weight, h * BANK : (h + 1) * BANK],
+                        in0=bank[:],
+                        in1=bias_all[:, weight, VARIANCE + h * BANK : VARIANCE + (h + 1) * BANK],
+                        op=ALU.add,
+                    )
+            x_k = work.tile([P, C], F32, bufs=4)
+            x_v = work.tile([P, C], F32, bufs=GROUP + 2)
+            sums = work.tile([P, 2, HALVES], F32, bufs=3)
+            for weight, x in ((KEY, x_k), (VALUE, x_v)):
+                for h in range(HALVES):
+                    bank = product(i, weight, MEAN + h * BANK)
+                    nc.vector.scalar_tensor_tensor(
+                        out=x[:, h * BANK : (h + 1) * BANK],
+                        in0=bank[:],
+                        scalar=1.0,
+                        in1=bias_all[:, weight, MEAN + h * BANK : MEAN + (h + 1) * BANK],
+                        op0=ALU.mult,
+                        op1=ALU.add,
+                        accum_out=sums[:, weight, h : h + 1],
+                    )
+            total = work.tile([P, 2], F32, bufs=3)
+            nc.vector.tensor_reduce(out=total[:], in_=sums[:], axis=AXIS.X, op=ALU.add)
+            neg_mean = work.tile([P, 2], F32, bufs=GROUP + 3)
+            nc.vector.tensor_scalar_mul(out=neg_mean[:], in0=total[:], scalar1=-1.0 / C)
+            var_in[i] = v
+            mean_in_k[i] = x_k
+            mean_in_v[i] = x_v
+            minus_mean[i] = neg_mean
+
+        def exponential(i):
+            e = work.tile([P, 2, C], F32, bufs=GROUP + 1)
+            nc.scalar.activation(out=e[:], in_=var_in[i][:], func=ACT.Exp, bias=var_eps[:])
+            var_out[i] = e
+
+        def squares(i):
+            ssq = work.tile([P, 2], F32, bufs=GROUP + 3)
+            for weight, x in ((KEY, mean_in_k[i]), (VALUE, mean_in_v[i])):
+                unread = work.tile([P, C], BF16, bufs=2)
+                nc.scalar.activation(
+                    out=unread[:],
+                    in_=x[:],
+                    func=ACT.Square,
+                    bias=minus_mean[i][:, weight : weight + 1],
+                    accum_out=ssq[:, weight : weight + 1],
+                )
+            square_sum[i] = ssq
+
+        def inverse_std(i):
+            variance = work.tile([P, 2], F32, bufs=3)
+            nc.gpsimd.tensor_scalar(
+                out=variance[:],
+                in0=square_sum[i][:],
+                scalar1=1.0 / C,
+                scalar2=LN_EPS,
+                op0=ALU.mult,
+                op1=ALU.add,
+            )
+            rstd = work.tile([P, 2], F32, bufs=GROUP + 3)
+            nc.gpsimd.tensor_tensor(out=rstd[:], in0=variance[:], in1=minus_half[:], op=ALU.pow)
+            shift = work.tile([P, 1], F32, bufs=GROUP + 3)
+            nc.gpsimd.tensor_tensor(
+                out=shift[:], in0=minus_mean[i][:, KEY : KEY + 1], in1=rstd[:, KEY : KEY + 1], op=ALU.mult
+            )
+            inv_std[i] = rstd
+            minus_mean_inv_std[i] = shift
+
+        def finish_k_mu(i):
+            x = mean_in_k[i]
+            nc.scalar.activation(
+                out=x[:],
+                in_=x[:],
+                func=ACT.Identity,
+                scale=inv_std[i][:, KEY : KEY + 1],
+                bias=minus_mean_inv_std[i][:],
+            )
+            nc.gpsimd.tensor_tensor(out=x[:], in0=x[:], in1=gain_k[:], op=ALU.mult)
+            nc.gpsimd.tensor_tensor(out=x[:], in0=x[:], in1=shift_k[:], op=ALU.add)
+            nc.sync.dma_start(out=k_mu_rows[i * P : (i + 1) * P, :], in_=x[:])
+
+        def finish_v_mu(i):
+            x = mean_in_v[i]
+            nc.vector.scalar_tensor_tensor(
+                out=x[:],
+                in0=x[:],
+                scalar=minus_mean[i][:, VALUE : VALUE + 1],
+                in1=gain_v[:],
+                op0=ALU.add,
+                op1=ALU.mult,
+            )
+            nc.vector.scalar_tensor_tensor(
+                out=x[:],
+                in0=x[:],
+                scalar=inv_std[i][:, VALUE : VALUE + 1],
+                in1=shift_v[:],
+                op0=ALU.mult,
+                op1=ALU.add,
+            )
+
+        def logarithm(i):
+            e = var_out[i]
+            nc.scalar.activation(out=e[:], in_=e[:], func=ACT.Ln, bias=exp_var_eps[:])
+
+        def linear_tail(i):
+            e = var_out[i]
+            nc.vector.scalar_tensor_tensor(
+                out=e[:],
+                in0=e[:],
+                scalar=LINEAR_FROM,
+                in1=var_in[i][:],
+                op0=ALU.min,
+                op1=ALU.max,
+            )
+            nc.sync.dma_start(out=k_var_rows[i * P : (i + 1) * P, :], in_=e[:, KEY, :])
+
+        def square_root(i):
+            e = var_out[i]
+            nc.scalar.activation(out=e[:, VALUE, :], in_=e[:, VALUE, :], func=ACT.Sqrt)
+
+        def scale_noise(i, engine):
+            e = var_out[i]
+            engine.tensor_tensor(out=e[:, VALUE, :], in0=e[:, VALUE, :], in1=noise[:, i, :], op=ALU.mult)
+
+        def add_noise(i):
+            x = mean_in_v[i]
+            nc.vector.tensor_tensor(out=x[:], in0=x[:], in1=var_out[i][:, VALUE, :], op=ALU.add)
+            nc.sync.dma_start(out=v_sample_rows[i * P : (i + 1) * P, :], in_=x[:])
+
+        for i in range(PREP_AHEAD):
+            quantise_context(i)
+        project(0)
+        for h in range(HALVES):
+            half = slice(h * BANK, (h + 1) * BANK)
+            nc.tensor.matmul(out=gain_v[:, half], lhsT=identity_bf16[:], rhs=gain_v_sbuf[:, half], start=True, stop=True)
+            nc.tensor.matmul(out=shift_v[:, half], lhsT=identity_bf16[:], rhs=shift_v_sbuf[:, half], start=True, stop=True)
+
+        for r in range(ROUNDS):
+            first = r * GROUP
+            last_round = r == ROUNDS - 1
+            for i in range(first, first + GROUP):
+                if r > 0:
+                    add_noise(i - GROUP)
+                if i + 1 < TILES:
+                    project(i + 1)
+                exponential(i)
+                squares(i)
+                inverse_std(i)
+                if i > first:
+                    finish_k_mu(i - 1)
+                if i + PREP_AHEAD < TILES:
+                    quantise_context(i + PREP_AHEAD)
+            finish_k_mu(first + GROUP - 1)
+            for i in range(first, first + GROUP):
+                logarithm(i)
+                finish_v_mu(i)
+                linear_tail(i)
+            for i in range(first, first + GROUP):
+                square_root(i)
+                scale_noise(i, nc.vector if last_round else nc.gpsimd)
+                if last_round:
+                    add_noise(i)

@@ -35,6 +35,12 @@ KEY = 0
 VALUE = 1
 MEAN = 0
 VARIANCE = C
+BK_ROW = 0
+BV_ROW = 4
+GAIN_K_ROW = 0
+SHIFT_K_ROW = 2
+GAIN_V_ROW = 4
+SHIFT_V_ROW = 6
 
 
 def tile_probcrossattention_pa_kernel(
@@ -78,8 +84,8 @@ def tile_probcrossattention_pa_kernel(
         bias_all = keep.tile([P, 2, 2 * C], BF16)
         gain_k = keep.tile([P, C], BF16)
         shift_k = keep.tile([P, C], BF16)
-        gain_v_sbuf = keep.tile([P, C], BF16)
-        shift_v_sbuf = keep.tile([P, C], BF16)
+        bias_rows = keep.tile([P, BANK], BF16)
+        norm_rows = keep.tile([P, BANK], BF16)
         identity_f32 = keep.tile([P, P], F32)
         identity_bf16 = keep.tile([P, P], BF16)
         var_eps = keep.tile([P, 1], F32)
@@ -88,6 +94,8 @@ def tile_probcrossattention_pa_kernel(
         gain_v = psum.tile([P, C], BF16)
         shift_v = psum.tile([P, C], BF16)
 
+        nc.vector.memset(bias_rows[:].bitcast(I32), 0)
+        nc.vector.memset(norm_rows[:].bitcast(I32), 0)
         nc.vector.memset(weight_scales[:].bitcast(I32), 0)
         nc.vector.memset(var_eps[:], VAR_EPS)
         nc.vector.memset(minus_half[:], -0.5)
@@ -105,30 +113,38 @@ def tile_probcrossattention_pa_kernel(
                     in_=packed[:, PACK * first_column : PACK * (first_column + C)].bitcast(I32),
                 )
 
-        for i in range(PREP_AHEAD):
-            load_context(i)
-        for quadrant in range(4):
-            for weight in (KEY, VALUE):
+        def load_weight_scales(weight):
+            for quadrant in range(4):
                 first_row = 32 * quadrant + 8 * weight
                 nc.sync.dma_start(
                     out=weight_scales[first_row : first_row + 8, :].bitcast(I32),
                     in_=scales_in[weight][:, 4 * quadrant : 4 * quadrant + 4, :].bitcast(I32),
                 )
+
+        def load_vector(vector, rows_tile, first_row):
+            rows = vector.rearrange("(j n) -> j n", n=BANK)
+            nc.sync.dma_start(out=rows_tile[first_row : first_row + rows.shape[0], :], in_=rows)
+
+        load_context(0)
+        load_vector(bk, bias_rows, BK_ROW)
+        load_vector(bv, bias_rows, BV_ROW)
+        load_weight_scales(KEY)
         load_weight_section(KEY, VARIANCE)
+        load_weight_scales(VALUE)
         load_weight_section(VALUE, VARIANCE)
+        load_context(1)
+        load_context(2)
         load_weight_section(KEY, MEAN)
         load_weight_section(VALUE, MEAN)
+        load_vector(ln_k_g, norm_rows, GAIN_K_ROW)
+        load_vector(ln_k_b, norm_rows, SHIFT_K_ROW)
+        load_vector(ln_v_g, norm_rows, GAIN_V_ROW)
+        load_vector(ln_v_b, norm_rows, SHIFT_V_ROW)
         for i in range(PREP_AHEAD, TILES):
             load_context(i)
         for i in range(TILES):
             nc.sync.dma_start(out=noise[:, i, :], in_=noise_rows[:, i, :])
 
-        nc.scalar.dma_start(out=bias_all[:, KEY, :], in_=bk.partition_broadcast(P))
-        nc.scalar.dma_start(out=bias_all[:, VALUE, :], in_=bv.partition_broadcast(P))
-        nc.scalar.dma_start(out=gain_k[:], in_=ln_k_g.partition_broadcast(P))
-        nc.scalar.dma_start(out=shift_k[:], in_=ln_k_b.partition_broadcast(P))
-        nc.scalar.dma_start(out=gain_v_sbuf[:], in_=ln_v_g.partition_broadcast(P))
-        nc.scalar.dma_start(out=shift_v_sbuf[:], in_=ln_v_b.partition_broadcast(P))
         nc.scalar.activation(out=exp_var_eps[:], in_=var_eps[:], func=ACT.Exp)
 
         mean_in_k = {}
@@ -139,6 +155,22 @@ def tile_probcrossattention_pa_kernel(
         square_sum = {}
         inv_std = {}
         minus_mean_inv_std = {}
+
+        def spread(rows_tile, first_row, target):
+            for h in range(HALVES):
+                j = first_row + h
+                nc.tensor.matmul(
+                    out=target[:, h * BANK : (h + 1) * BANK],
+                    lhsT=identity_bf16[:, j : j + 1].to_broadcast([P, P]),
+                    rhs=rows_tile[:],
+                    start=True,
+                    stop=True,
+                )
+
+        def spread_to_sbuf(rows_tile, first_row, target, engine_copy):
+            bank = psum.tile([P, C], BF16, tag="bank", bufs=5)
+            spread(rows_tile, first_row, bank)
+            engine_copy(out=target, in_=bank[:])
 
         def quantise_context(i):
             words = context_raw[:, i, :].bitcast(F32)
@@ -163,7 +195,7 @@ def tile_probcrossattention_pa_kernel(
 
         def product(i, weight, first_column):
             columns = slice(first_column, first_column + BANK)
-            bank = psum.tile([P, BANK], F32, bufs=5)
+            bank = psum.tile([P, BANK], F32, tag="bank", bufs=5)
             for g in range(PASSES):
                 plane_row = 4 * (PASSES * weight + g)
                 nc.tensor.matmul_mx(
@@ -310,13 +342,18 @@ def tile_probcrossattention_pa_kernel(
             nc.vector.tensor_tensor(out=x[:], in0=x[:], in1=var_out[i][:, VALUE, :], op=ALU.add)
             nc.sync.dma_start(out=v_sample_rows[i * P : (i + 1) * P, :], in_=x[:])
 
-        for i in range(PREP_AHEAD):
+        quantise_context(0)
+        spread_to_sbuf(bias_rows, BK_ROW + HALVES, bias_all[:, KEY, VARIANCE:], nc.vector.tensor_copy)
+        spread_to_sbuf(bias_rows, BV_ROW + HALVES, bias_all[:, VALUE, VARIANCE:], nc.vector.tensor_copy)
+        spread_to_sbuf(bias_rows, BK_ROW, bias_all[:, KEY, :VARIANCE], nc.vector.tensor_copy)
+        spread_to_sbuf(bias_rows, BV_ROW, bias_all[:, VALUE, :VARIANCE], nc.vector.tensor_copy)
+        for i in range(1, PREP_AHEAD):
             quantise_context(i)
         project(0)
-        for h in range(HALVES):
-            half = slice(h * BANK, (h + 1) * BANK)
-            nc.tensor.matmul(out=gain_v[:, half], lhsT=identity_bf16[:], rhs=gain_v_sbuf[:, half], start=True, stop=True)
-            nc.tensor.matmul(out=shift_v[:, half], lhsT=identity_bf16[:], rhs=shift_v_sbuf[:, half], start=True, stop=True)
+        spread_to_sbuf(norm_rows, GAIN_K_ROW, gain_k[:], nc.scalar.copy)
+        spread_to_sbuf(norm_rows, SHIFT_K_ROW, shift_k[:], nc.scalar.copy)
+        spread(norm_rows, GAIN_V_ROW, gain_v)
+        spread(norm_rows, SHIFT_V_ROW, shift_v)
 
         for r in range(ROUNDS):
             first = r * GROUP

@@ -27,6 +27,7 @@ ROUNDS = TILES // GROUP
 PREP_AHEAD = 3
 VAR_EPS = 1e-6
 LN_EPS = 1e-5
+GPSIMD_PIECE = 256
 LINEAR_FROM = 20.0
 
 FLOPS = 2 * TOKENS * C * 4 * C
@@ -290,8 +291,12 @@ def tile_probcrossattention_pa_kernel(
                 scale=inv_std[i][:, KEY : KEY + 1],
                 bias=minus_mean_inv_std[i][:],
             )
-            nc.gpsimd.tensor_tensor(out=x[:], in0=x[:], in1=gain_k[:], op=ALU.mult)
-            nc.gpsimd.tensor_tensor(out=x[:], in0=x[:], in1=shift_k[:], op=ALU.add)
+            for first_column in range(0, C, GPSIMD_PIECE):
+                piece = slice(first_column, first_column + GPSIMD_PIECE)
+                nc.gpsimd.tensor_tensor(out=x[:, piece], in0=x[:, piece], in1=gain_k[:, piece], op=ALU.mult)
+            for first_column in range(0, C, GPSIMD_PIECE):
+                piece = slice(first_column, first_column + GPSIMD_PIECE)
+                nc.gpsimd.tensor_tensor(out=x[:, piece], in0=x[:, piece], in1=shift_k[:, piece], op=ALU.add)
             nc.sync.dma_start(out=k_mu_rows[i * P : (i + 1) * P, :], in_=x[:])
 
         def finish_v_mu(i):
@@ -335,7 +340,9 @@ def tile_probcrossattention_pa_kernel(
 
         def scale_noise(i, engine):
             e = var_out[i]
-            engine.tensor_tensor(out=e[:, VALUE, :], in0=e[:, VALUE, :], in1=noise[:, i, :], op=ALU.mult)
+            for first_column in range(0, C, GPSIMD_PIECE):
+                piece = slice(first_column, first_column + GPSIMD_PIECE)
+                engine.tensor_tensor(out=e[:, VALUE, piece], in0=e[:, VALUE, piece], in1=noise[:, i, piece], op=ALU.mult)
 
         def add_noise(i):
             x = mean_in_v[i]

@@ -27,7 +27,6 @@ ROUNDS = TILES // GROUP
 PREP_AHEAD = 3
 VAR_EPS = 1e-6
 LN_EPS = 1e-5
-GPSIMD_PIECE = 256
 LINEAR_FROM = 20.0
 
 FLOPS = 2 * TOKENS * C * 4 * C
@@ -155,7 +154,6 @@ def tile_probcrossattention_pa_kernel(
         minus_mean = {}
         square_sum = {}
         inv_std = {}
-        minus_mean_inv_std = {}
 
         def spread(rows_tile, first_row, target):
             for h in range(HALVES):
@@ -275,28 +273,26 @@ def tile_probcrossattention_pa_kernel(
             )
             rstd = work.tile([P, 2], F32, bufs=GROUP + 3)
             nc.gpsimd.tensor_tensor(out=rstd[:], in0=variance[:], in1=minus_half[:], op=ALU.pow)
-            shift = work.tile([P, 1], F32, bufs=GROUP + 3)
-            nc.gpsimd.tensor_tensor(
-                out=shift[:], in0=minus_mean[i][:, KEY : KEY + 1], in1=rstd[:, KEY : KEY + 1], op=ALU.mult
-            )
             inv_std[i] = rstd
-            minus_mean_inv_std[i] = shift
 
         def finish_k_mu(i):
             x = mean_in_k[i]
-            nc.scalar.activation(
+            nc.vector.scalar_tensor_tensor(
                 out=x[:],
-                in_=x[:],
-                func=ACT.Identity,
-                scale=inv_std[i][:, KEY : KEY + 1],
-                bias=minus_mean_inv_std[i][:],
+                in0=x[:],
+                scalar=minus_mean[i][:, KEY : KEY + 1],
+                in1=gain_k[:],
+                op0=ALU.add,
+                op1=ALU.mult,
             )
-            for first_column in range(0, C, GPSIMD_PIECE):
-                piece = slice(first_column, first_column + GPSIMD_PIECE)
-                nc.gpsimd.tensor_tensor(out=x[:, piece], in0=x[:, piece], in1=gain_k[:, piece], op=ALU.mult)
-            for first_column in range(0, C, GPSIMD_PIECE):
-                piece = slice(first_column, first_column + GPSIMD_PIECE)
-                nc.gpsimd.tensor_tensor(out=x[:, piece], in0=x[:, piece], in1=shift_k[:, piece], op=ALU.add)
+            nc.vector.scalar_tensor_tensor(
+                out=x[:],
+                in0=x[:],
+                scalar=inv_std[i][:, KEY : KEY + 1],
+                in1=shift_k[:],
+                op0=ALU.mult,
+                op1=ALU.add,
+            )
             nc.sync.dma_start(out=k_mu_rows[i * P : (i + 1) * P, :], in_=x[:])
 
         def finish_v_mu(i):
@@ -340,9 +336,7 @@ def tile_probcrossattention_pa_kernel(
 
         def scale_noise(i, engine):
             e = var_out[i]
-            for first_column in range(0, C, GPSIMD_PIECE):
-                piece = slice(first_column, first_column + GPSIMD_PIECE)
-                engine.tensor_tensor(out=e[:, VALUE, piece], in0=e[:, VALUE, piece], in1=noise[:, i, piece], op=ALU.mult)
+            engine.tensor_tensor(out=e[:, VALUE, :], in0=e[:, VALUE, :], in1=noise[:, i, :], op=ALU.mult)
 
         def add_noise(i):
             x = mean_in_v[i]
@@ -384,6 +378,6 @@ def tile_probcrossattention_pa_kernel(
                 linear_tail(i)
             for i in range(first, first + GROUP):
                 square_root(i)
-                scale_noise(i, nc.vector if last_round else nc.gpsimd)
+                scale_noise(i, nc.vector)
                 if last_round:
                     add_noise(i)

@@ -11,7 +11,6 @@ U8 = mybir.dt.uint8
 FP8X4 = mybir.dt.float8_e4m3fn_x4
 ALU = mybir.AluOpType
 ACT = mybir.ActivationFunctionType
-AXIS = mybir.AxisListType
 
 P = 128
 PACK = 4
@@ -22,12 +21,12 @@ PASSES = C // K_PASS
 TILES = TOKENS // P
 BANK = 512
 HALVES = C // BANK
-GROUP = 4
-ROUNDS = TILES // GROUP
-PREP_AHEAD = 3
+CHUNKS = TOKENS // BANK
+CHUNK_TILES = BANK // P
+CHANNEL_TILES = C // P
 VAR_EPS = 1e-6
 LN_EPS = 1e-5
-LINEAR_FROM = 20.0
+LN_FLOOR = 2.0 ** -60
 
 FLOPS = 2 * TOKENS * C * 4 * C
 
@@ -35,12 +34,6 @@ KEY = 0
 VALUE = 1
 MEAN = 0
 VARIANCE = C
-BK_ROW = 0
-BV_ROW = 4
-GAIN_K_ROW = 0
-SHIFT_K_ROW = 2
-GAIN_V_ROW = 4
-SHIFT_V_ROW = 6
 
 
 def tile_probcrossattention_pa_kernel(
@@ -69,38 +62,48 @@ def tile_probcrossattention_pa_kernel(
     v_sample_rows = out_2.flatten_outer_dims()
     words_in = (Wk_words, Wv_words)
     scales_in = (Wk_scales, Wv_scales)
+    bias_in = (bk, bv)
 
     with ExitStack() as stack:
         keep = stack.enter_context(tc.tile_pool(name="keep", bufs=1))
         work = stack.enter_context(tc.tile_pool(name="work", bufs=2))
         psum = stack.enter_context(tc.psum_pool(name="psum", bufs=1))
+        stack.enter_context(tc.manual_schedule())
 
         context_raw = keep.tile([P, TILES, C], BF16)
         noise = keep.tile([P, TILES, C], BF16)
-        context_codes = keep.tile([P, TILES, PASSES, P], U32, align_bytes=64)
-        context_scales = keep.tile([P, TILES, PASSES, P], U8, align_bytes=64)
+        context_codes = keep.tile([P, PASSES, TOKENS], U32, align_bytes=64)
+        context_scales = keep.tile([P, PASSES, TOKENS], U8, align_bytes=64)
         weight_codes = keep.tile([P, 2, PASSES, 2 * C], U32, align_bytes=64)
         weight_scales = keep.tile([P, 2 * C], U8, align_bytes=64)
-        bias_all = keep.tile([P, 2, 2 * C], BF16)
+        bias_mean = keep.tile([P, 2, C], BF16)
         gain_k = keep.tile([P, C], BF16)
         shift_k = keep.tile([P, C], BF16)
         bias_rows = keep.tile([P, BANK], BF16)
         norm_rows = keep.tile([P, BANK], BF16)
+        var_bias_rows = keep.tile([P, P], BF16)
+        neg_var_bias = keep.tile([P, 2 * CHANNEL_TILES], F32)
         identity_f32 = keep.tile([P, P], F32)
         identity_bf16 = keep.tile([P, P], BF16)
         var_eps = keep.tile([P, 1], F32)
-        exp_var_eps = keep.tile([P, 1], F32)
-        minus_half = keep.tile([P, 2], F32)
+        ln_floor = keep.tile([P, 1], F32)
+        minus_half = keep.tile([P, 1], F32)
+        warm = keep.tile([P, 1], F32)
+        v_mu = keep.tile([P, TILES, C], F32)
+        sigma = keep.tile([P, TILES, C], F32)
         gain_v = psum.tile([P, C], BF16)
         shift_v = psum.tile([P, C], BF16)
 
+        nc.vector.memset(var_bias_rows[:].bitcast(I32), 0)
         nc.vector.memset(bias_rows[:].bitcast(I32), 0)
-        nc.vector.memset(norm_rows[:].bitcast(I32), 0)
         nc.vector.memset(weight_scales[:].bitcast(I32), 0)
+        nc.vector.memset(norm_rows[:].bitcast(I32), 0)
         nc.vector.memset(var_eps[:], VAR_EPS)
+        nc.vector.memset(ln_floor[:], LN_FLOOR)
         nc.vector.memset(minus_half[:], -0.5)
         make_identity(nc, identity_f32[:])
         make_identity(nc, identity_bf16[:])
+        nc.scalar.activation(out=warm[:], in_=minus_half[:], func=ACT.Sigmoid)
 
         def load_context(i):
             nc.sync.dma_start(out=context_raw[:, i, :], in_=context_rows[:, i, :])
@@ -121,39 +124,46 @@ def tile_probcrossattention_pa_kernel(
                     in_=scales_in[weight][:, 4 * quadrant : 4 * quadrant + 4, :].bitcast(I32),
                 )
 
-        def load_vector(vector, rows_tile, first_row):
-            rows = vector.rearrange("(j n) -> j n", n=BANK)
-            nc.sync.dma_start(out=rows_tile[first_row : first_row + rows.shape[0], :], in_=rows)
+        def load_rows(vector, first, count, width, rows_tile, first_row):
+            rows = vector[first : first + count * width].rearrange("(j n) -> j n", n=width)
+            nc.sync.dma_start(out=rows_tile[first_row : first_row + count, :], in_=rows)
 
-        load_context(0)
-        load_vector(bk, bias_rows, BK_ROW)
-        load_vector(bv, bias_rows, BV_ROW)
+        for i in range(CHUNK_TILES):
+            load_context(i)
+        for weight in (KEY, VALUE):
+            load_rows(bias_in[weight], MEAN, HALVES, BANK, bias_rows, HALVES * weight)
+            load_rows(bias_in[weight], VARIANCE, CHANNEL_TILES, P, var_bias_rows, CHANNEL_TILES * weight)
         load_weight_scales(KEY)
-        load_weight_section(KEY, VARIANCE)
         load_weight_scales(VALUE)
-        load_weight_section(VALUE, VARIANCE)
-        load_context(1)
-        load_context(2)
-        load_weight_section(KEY, MEAN)
         load_weight_section(VALUE, MEAN)
-        load_vector(ln_k_g, norm_rows, GAIN_K_ROW)
-        load_vector(ln_k_b, norm_rows, SHIFT_K_ROW)
-        load_vector(ln_v_g, norm_rows, GAIN_V_ROW)
-        load_vector(ln_v_b, norm_rows, SHIFT_V_ROW)
-        for i in range(PREP_AHEAD, TILES):
+        load_weight_section(VALUE, VARIANCE)
+        for j, vector in enumerate((ln_k_g, ln_k_b, ln_v_g, ln_v_b)):
+            load_rows(vector, 0, HALVES, BANK, norm_rows, HALVES * j)
+        load_weight_section(KEY, MEAN)
+        for i in range(CHUNK_TILES, TILES):
             load_context(i)
         for i in range(TILES):
             nc.sync.dma_start(out=noise[:, i, :], in_=noise_rows[:, i, :])
+        load_weight_section(KEY, VARIANCE)
 
-        nc.scalar.activation(out=exp_var_eps[:], in_=var_eps[:], func=ACT.Exp)
-
-        mean_in_k = {}
-        mean_in_v = {}
-        var_in = {}
-        var_out = {}
+        negated = {}
+        turned = {}
+        grouped = {}
+        k_mu = {}
         minus_mean = {}
-        square_sum = {}
         inv_std = {}
+        square_sum = {}
+        half_sums = {}
+        log_sigmoid = {}
+        k_var = {}
+
+        def for_scalar(shape, dtype):
+            bank_for_scalar = psum.tile(shape, dtype, tag="bank_for_scalar", bufs=3)
+            return bank_for_scalar
+
+        def for_vector(shape, dtype):
+            bank_for_vector = psum.tile(shape, dtype, tag="bank_for_vector", bufs=3)
+            return bank_for_vector
 
         def spread(rows_tile, first_row, target):
             for h in range(HALVES):
@@ -166,218 +176,375 @@ def tile_probcrossattention_pa_kernel(
                     stop=True,
                 )
 
-        def spread_to_sbuf(rows_tile, first_row, target, engine_copy):
-            bank = psum.tile([P, C], BF16, tag="bank", bufs=5)
+        def spread_by_vector(rows_tile, first_row, target):
+            bank = for_vector([P, C], BF16)
             spread(rows_tile, first_row, bank)
-            engine_copy(out=target, in_=bank[:])
+            nc.vector.tensor_copy(out=target, in_=bank[:])
 
-        def quantise_context(i):
-            words = context_raw[:, i, :].bitcast(F32)
-            turned = psum.tile([P, PASSES * 2, P], F32)
+        def spread_by_scalar(rows_tile, first_row, target):
+            bank = for_scalar([P, C], BF16)
+            spread(rows_tile, first_row, bank)
+            nc.scalar.copy(out=target, in_=bank[:])
+
+        def turn_var_bias():
+            bank = for_vector([P, C], BF16)
+            nc.tensor.transpose(bank[:, :P], var_bias_rows[:], identity_bf16[:])
+            nc.vector.tensor_scalar_mul(
+                out=neg_var_bias[:], in0=bank[:, : 2 * CHANNEL_TILES], scalar1=-1.0
+            )
+
+        def negate_context(i):
+            minus = work.tile([P, C], BF16, tag="minus", bufs=3)
+            nc.vector.tensor_scalar_mul(out=minus[:], in0=context_raw[:, i, :], scalar1=-1.0)
+            negated[i] = minus
+
+        def turn_context(i):
+            words = negated[i][:].bitcast(F32)
+            bank = for_scalar([P, PASSES * 2, P], F32)
             for g in range(PASSES):
                 for u in range(2):
                     nc.tensor.transpose(
-                        turned[:, 2 * g + u, :],
+                        bank[:, 2 * g + u, :],
                         words[:, 256 * g + u : 256 * (g + 1) : 2],
                         identity_f32[:],
                     )
-            grouped = work.tile([P, PASSES * P * PACK], BF16, align_bytes=64)
-            nc.scalar.copy(
-                out=grouped[:].bitcast(F32).rearrange("p (g r u) -> p g r u", g=PASSES, u=2),
-                in_=turned[:].rearrange("p (g u) r -> p g r u", u=2),
-            )
-            nc.vector.quantize_mx(
-                out=context_codes[:, i, :, :].rearrange("p g r -> p (g r)").bitcast(FP8X4),
-                scales=context_scales[:, i, :, :].rearrange("p g r -> p (g r)"),
-                in_=grouped[:],
-            )
+            turned[i] = bank
 
-        def product(i, weight, first_column):
-            columns = slice(first_column, first_column + BANK)
-            bank = psum.tile([P, BANK], F32, tag="bank", bufs=5)
+        def group_context(i):
+            side_by_side = work.tile([P, PASSES * P * PACK], BF16, tag="side_by_side", bufs=3, align_bytes=64)
+            nc.scalar.copy(
+                out=side_by_side[:].bitcast(F32).rearrange("p (g r u) -> p g r u", g=PASSES, u=2),
+                in_=turned[i][:].rearrange("p (g u) r -> p g r u", u=2),
+            )
+            grouped[i] = side_by_side
+
+        def quantise_context(i):
+            tokens = slice(i * P, (i + 1) * P)
             for g in range(PASSES):
-                plane_row = 4 * (PASSES * weight + g)
+                nc.vector.quantize_mx(
+                    out=context_codes[:, g, tokens].bitcast(FP8X4),
+                    scales=context_scales[:, g, tokens],
+                    in_=grouped[i][:, g * K_PASS : (g + 1) * K_PASS],
+                )
+
+        def plane(weight, g, columns):
+            return weight_scales[4 * (PASSES * weight + g) : P, columns]
+
+        def tokens_by_channels(bank, i, weight, first_column):
+            tokens = slice(i * P, (i + 1) * P)
+            columns = slice(first_column, first_column + BANK)
+            for g in range(PASSES):
                 nc.tensor.matmul_mx(
                     out=bank[:],
-                    lhsT=context_codes[:, i, g, :].bitcast(FP8X4),
-                    lhsT_scale=context_scales[:, i, g, :],
+                    lhsT=context_codes[:, g, tokens].bitcast(FP8X4),
+                    lhsT_scale=context_scales[:, g, tokens],
                     rhs=weight_codes[:, weight, g, columns].bitcast(FP8X4),
-                    rhs_scale=weight_scales[plane_row:P, columns],
+                    rhs_scale=plane(weight, g, columns),
                     start=(g == 0),
                     stop=(g == PASSES - 1),
                 )
-            return bank
 
-        def project(i):
-            v = work.tile([P, 2, C], F32, bufs=GROUP + 1)
-            for weight in (KEY, VALUE):
-                for h in range(HALVES):
-                    bank = product(i, weight, VARIANCE + h * BANK)
-                    nc.vector.tensor_tensor(
-                        out=v[:, weight, h * BANK : (h + 1) * BANK],
-                        in0=bank[:],
-                        in1=bias_all[:, weight, VARIANCE + h * BANK : VARIANCE + (h + 1) * BANK],
-                        op=ALU.add,
-                    )
-            x_k = work.tile([P, C], F32, bufs=4)
-            x_v = work.tile([P, C], F32, bufs=GROUP + 2)
-            sums = work.tile([P, 2, HALVES], F32, bufs=3)
-            for weight, x in ((KEY, x_k), (VALUE, x_v)):
-                for h in range(HALVES):
-                    bank = product(i, weight, MEAN + h * BANK)
-                    nc.vector.scalar_tensor_tensor(
-                        out=x[:, h * BANK : (h + 1) * BANK],
-                        in0=bank[:],
-                        scalar=1.0,
-                        in1=bias_all[:, weight, MEAN + h * BANK : MEAN + (h + 1) * BANK],
-                        op0=ALU.mult,
-                        op1=ALU.add,
-                        accum_out=sums[:, weight, h : h + 1],
-                    )
-            total = work.tile([P, 2], F32, bufs=3)
-            nc.vector.tensor_reduce(out=total[:], in_=sums[:], axis=AXIS.X, op=ALU.add)
-            neg_mean = work.tile([P, 2], F32, bufs=GROUP + 3)
-            nc.vector.tensor_scalar_mul(out=neg_mean[:], in0=total[:], scalar1=-1.0 / C)
-            var_in[i] = v
-            mean_in_k[i] = x_k
-            mean_in_v[i] = x_v
-            minus_mean[i] = neg_mean
-
-        def exponential(i):
-            e = work.tile([P, 2, C], F32, bufs=GROUP + 1)
-            nc.scalar.activation(out=e[:], in_=var_in[i][:], func=ACT.Exp, bias=var_eps[:])
-            var_out[i] = e
-
-        def squares(i):
-            ssq = work.tile([P, 2], F32, bufs=GROUP + 3)
-            for weight, x in ((KEY, mean_in_k[i]), (VALUE, mean_in_v[i])):
-                unread = work.tile([P, C], BF16, bufs=2)
-                nc.scalar.activation(
-                    out=unread[:],
-                    in_=x[:],
-                    func=ACT.Square,
-                    bias=minus_mean[i][:, weight : weight + 1],
-                    accum_out=ssq[:, weight : weight + 1],
+        def channels_by_tokens(bank, weight, chunk, j):
+            tokens = slice(chunk * BANK, (chunk + 1) * BANK)
+            columns = slice(VARIANCE + j * P, VARIANCE + (j + 1) * P)
+            for g in range(PASSES):
+                nc.tensor.matmul_mx(
+                    out=bank[:],
+                    lhsT=weight_codes[:, weight, g, columns].bitcast(FP8X4),
+                    lhsT_scale=plane(weight, g, columns),
+                    rhs=context_codes[:, g, tokens].bitcast(FP8X4),
+                    rhs_scale=context_scales[:, g, tokens],
+                    start=(g == 0),
+                    stop=(g == PASSES - 1),
                 )
-            square_sum[i] = ssq
 
-        def inverse_std(i):
-            variance = work.tile([P, 2], F32, bufs=3)
+        def mean_input(i, weight):
+            if weight == KEY:
+                if i not in k_mu:
+                    k_mu_tile = work.tile([P, C], F32, tag="k_mu_tile", bufs=4)
+                    k_mu[i] = k_mu_tile
+                return k_mu[i][:]
+            return v_mu[:, i, :]
+
+        def project_mean(i, weight, h):
+            x = mean_input(i, weight)
+            if h == 0:
+                sums = work.tile([P, HALVES], F32, tag="sums", bufs=4)
+                half_sums[i, weight] = sums
+            bank = for_vector([P, BANK], F32)
+            tokens_by_channels(bank, i, weight, MEAN + h * BANK)
+            nc.vector.scalar_tensor_tensor(
+                out=x[:, h * BANK : (h + 1) * BANK],
+                in0=bank[:],
+                scalar=-1.0,
+                in1=bias_mean[:, weight, h * BANK : (h + 1) * BANK],
+                op0=ALU.mult,
+                op1=ALU.add,
+                accum_out=half_sums[i, weight][:, h : h + 1],
+            )
+            if h == HALVES - 1:
+                neg_mean = work.tile([P, 1], F32, tag="neg_mean", bufs=8)
+                nc.vector.tensor_scalar(
+                    out=neg_mean[:],
+                    in0=half_sums[i, weight][:, 0:1],
+                    scalar1=half_sums[i, weight][:, 1:2],
+                    scalar2=-1.0 / C,
+                    op0=ALU.add,
+                    op1=ALU.mult,
+                )
+                minus_mean[i, weight] = neg_mean
+
+        def squares(i, weight):
+            ssq = work.tile([P, 1], F32, tag="ssq", bufs=4)
+            unread = work.tile([P, C], BF16, tag="unread", bufs=1)
+            nc.scalar.activation(
+                out=unread[:],
+                in_=mean_input(i, weight),
+                func=ACT.Square,
+                bias=minus_mean[i, weight][:],
+                accum_out=ssq[:],
+            )
+            variance = work.tile([P, 1], F32, tag="variance", bufs=4)
             nc.gpsimd.tensor_scalar(
                 out=variance[:],
-                in0=square_sum[i][:],
+                in0=ssq[:],
                 scalar1=1.0 / C,
                 scalar2=LN_EPS,
                 op0=ALU.mult,
                 op1=ALU.add,
             )
-            rstd = work.tile([P, 2], F32, bufs=GROUP + 3)
+            rstd = work.tile([P, 1], F32, tag="rstd", bufs=8)
             nc.gpsimd.tensor_tensor(out=rstd[:], in0=variance[:], in1=minus_half[:], op=ALU.pow)
-            inv_std[i] = rstd
+            inv_std[i, weight] = rstd
 
-        def finish_k_mu(i):
-            x = mean_in_k[i]
+        def normalise(i, weight):
+            x = mean_input(i, weight)
+            gain, shift = ((gain_k, shift_k), (gain_v, shift_v))[weight]
             nc.vector.scalar_tensor_tensor(
-                out=x[:],
-                in0=x[:],
-                scalar=minus_mean[i][:, KEY : KEY + 1],
-                in1=gain_k[:],
+                out=x,
+                in0=x,
+                scalar=minus_mean[i, weight][:],
+                in1=gain[:],
                 op0=ALU.add,
                 op1=ALU.mult,
             )
             nc.vector.scalar_tensor_tensor(
-                out=x[:],
-                in0=x[:],
-                scalar=inv_std[i][:, KEY : KEY + 1],
-                in1=shift_k[:],
+                out=x,
+                in0=x,
+                scalar=inv_std[i, weight][:],
+                in1=shift[:],
                 op0=ALU.mult,
                 op1=ALU.add,
             )
-            nc.sync.dma_start(out=k_mu_rows[i * P : (i + 1) * P, :], in_=x[:])
+            if weight == KEY:
+                nc.sync.dma_start(out=k_mu_rows[i * P : (i + 1) * P, :], in_=x)
 
-        def finish_v_mu(i):
-            x = mean_in_v[i]
+        def bias_column(weight, j):
+            column = CHANNEL_TILES * weight + j
+            return neg_var_bias[:, column : column + 1]
+
+        def sigmoid(weight, chunk, j):
+            if j == 0:
+                logs = work.tile([P, CHANNEL_TILES, BANK], F32, tag="logs", bufs=2)
+                log_sigmoid[weight, chunk] = logs
+            bank = for_scalar([P, BANK], F32)
+            channels_by_tokens(bank, weight, chunk, j)
+            nc.scalar.activation(
+                out=log_sigmoid[weight, chunk][:, j, :],
+                in_=bank[:],
+                func=ACT.Sigmoid,
+                bias=bias_column(weight, j),
+            )
+
+        def logarithm(weight, chunk, half):
+            part = log_sigmoid[weight, chunk][:, half * CHUNK_TILES : (half + 1) * CHUNK_TILES, :]
+            nc.scalar.activation(out=part, in_=part, func=ACT.Ln, bias=ln_floor[:])
+
+        def linear_tail(weight, chunk, j):
+            part = log_sigmoid[weight, chunk][:, j, :]
+            bank = for_vector([P, BANK], F32)
+            channels_by_tokens(bank, weight, chunk, j)
             nc.vector.scalar_tensor_tensor(
-                out=x[:],
-                in0=x[:],
-                scalar=minus_mean[i][:, VALUE : VALUE + 1],
-                in1=gain_v[:],
+                out=part,
+                in0=bank[:],
+                scalar=bias_column(weight, j),
+                in1=part,
                 op0=ALU.add,
-                op1=ALU.mult,
-            )
-            nc.vector.scalar_tensor_tensor(
-                out=x[:],
-                in0=x[:],
-                scalar=inv_std[i][:, VALUE : VALUE + 1],
-                in1=shift_v[:],
-                op0=ALU.mult,
-                op1=ALU.add,
+                op1=ALU.min,
             )
 
-        def logarithm(i):
-            e = var_out[i]
-            nc.scalar.activation(out=e[:], in_=e[:], func=ACT.Ln, bias=exp_var_eps[:])
+        def turn_back(bank, weight, chunk, half, a):
+            for q in range(CHUNK_TILES):
+                nc.tensor.transpose(
+                    bank[:, q * P : (q + 1) * P],
+                    log_sigmoid[weight, chunk][:, half * CHUNK_TILES + q, a * P : (a + 1) * P],
+                    identity_f32[:],
+                )
 
-        def linear_tail(i):
-            e = var_out[i]
-            nc.vector.scalar_tensor_tensor(
-                out=e[:],
-                in0=e[:],
-                scalar=LINEAR_FROM,
-                in1=var_in[i][:],
-                op0=ALU.min,
-                op1=ALU.max,
+        def sigma_out(chunk, half, a):
+            i = chunk * CHUNK_TILES + a
+            columns = slice(half * BANK, (half + 1) * BANK)
+            bank = for_scalar([P, BANK], F32)
+            turn_back(bank, VALUE, chunk, half, a)
+            nc.scalar.activation(
+                out=sigma[:, i, columns], in_=bank[:], func=ACT.Sqrt, scale=-1.0, bias=var_eps[:]
             )
-            nc.sync.dma_start(out=k_var_rows[i * P : (i + 1) * P, :], in_=e[:, KEY, :])
 
-        def square_root(i):
-            e = var_out[i]
-            nc.scalar.activation(out=e[:, VALUE, :], in_=e[:, VALUE, :], func=ACT.Sqrt)
+        def scale_noise(i, h):
+            columns = slice(h * BANK, (h + 1) * BANK)
+            nc.gpsimd.tensor_tensor(
+                out=sigma[:, i, columns], in0=sigma[:, i, columns], in1=noise[:, i, columns], op=ALU.mult
+            )
 
-        def scale_noise(i, engine):
-            e = var_out[i]
-            engine.tensor_tensor(out=e[:, VALUE, :], in0=e[:, VALUE, :], in1=noise[:, i, :], op=ALU.mult)
+        def k_var_out(chunk, half, a, by_vector):
+            i = chunk * CHUNK_TILES + a
+            columns = slice(half * BANK, (half + 1) * BANK)
+            if half == 0:
+                k_var_tile = work.tile([P, C], F32, tag="k_var_tile", bufs=4)
+                k_var[i] = k_var_tile
+            if by_vector:
+                bank = for_vector([P, BANK], F32)
+                turn_back(bank, KEY, chunk, half, a)
+                nc.vector.tensor_scalar(
+                    out=k_var[i][:, columns],
+                    in0=bank[:],
+                    scalar1=-1.0,
+                    scalar2=VAR_EPS,
+                    op0=ALU.mult,
+                    op1=ALU.add,
+                )
+            else:
+                bank = for_scalar([P, BANK], F32)
+                turn_back(bank, KEY, chunk, half, a)
+                nc.scalar.activation(
+                    out=k_var[i][:, columns], in_=bank[:], func=ACT.Identity, scale=-1.0, bias=var_eps[:]
+                )
+            if half == HALVES - 1:
+                nc.sync.dma_start(out=k_var_rows[i * P : (i + 1) * P, :], in_=k_var[i][:])
 
-        def add_noise(i):
-            x = mean_in_v[i]
-            nc.vector.tensor_tensor(out=x[:], in0=x[:], in1=var_out[i][:, VALUE, :], op=ALU.add)
-            nc.sync.dma_start(out=v_sample_rows[i * P : (i + 1) * P, :], in_=x[:])
+        def sample(i, h):
+            columns = slice(h * BANK, (h + 1) * BANK)
+            nc.gpsimd.tensor_tensor(
+                out=sigma[:, i, columns], in0=sigma[:, i, columns], in1=v_mu[:, i, columns], op=ALU.add
+            )
+            if h == HALVES - 1:
+                nc.sync.dma_start(out=v_sample_rows[i * P : (i + 1) * P, :], in_=sigma[:, i, :])
 
-        quantise_context(0)
-        spread_to_sbuf(bias_rows, BK_ROW + HALVES, bias_all[:, KEY, VARIANCE:], nc.vector.tensor_copy)
-        spread_to_sbuf(bias_rows, BV_ROW + HALVES, bias_all[:, VALUE, VARIANCE:], nc.vector.tensor_copy)
-        spread_to_sbuf(bias_rows, BK_ROW, bias_all[:, KEY, :VARIANCE], nc.vector.tensor_copy)
-        spread_to_sbuf(bias_rows, BV_ROW, bias_all[:, VALUE, :VARIANCE], nc.vector.tensor_copy)
-        for i in range(1, PREP_AHEAD):
+        def q_sigmoid(weight, chunk, half):
+            return [
+                lambda j=j: sigmoid(weight, chunk, j)
+                for j in range(half * CHUNK_TILES, (half + 1) * CHUNK_TILES)
+            ]
+
+        def q_log(weight, chunk, half):
+            return [lambda: logarithm(weight, chunk, half)]
+
+        def q_tail(weight, chunk, half):
+            return [
+                lambda j=j: linear_tail(weight, chunk, j)
+                for j in range(half * CHUNK_TILES, (half + 1) * CHUNK_TILES)
+            ]
+
+        def q_sigma(chunk, half):
+            return [lambda a=a: sigma_out(chunk, half, a) for a in range(CHUNK_TILES)]
+
+        def q_k_var(chunk, half, by_vector):
+            return [lambda a=a: k_var_out(chunk, half, a, by_vector) for a in range(CHUNK_TILES)]
+
+        def q_project(*items):
+            return [lambda i=i, w=w, h=h: project_mean(i, w, h) for i, w in items for h in range(HALVES)]
+
+        def q_squares(*items):
+            return [lambda i=i, w=w: squares(i, w) for i, w in items]
+
+        def q_normalise(*items):
+            return [lambda i=i, w=w: normalise(i, w) for i, w in items]
+
+        def q_noise(i):
+            return [lambda h=h: scale_noise(i, h) for h in range(HALVES)]
+
+        def q_sample(i):
+            return [lambda h=h: sample(i, h) for h in range(HALVES)]
+
+        def q_prepare(first):
+            calls = [lambda: (negate_context(first), turn_context(first), negate_context(first + 1))]
+            for i in range(first, first + CHUNK_TILES):
+                calls.append(lambda i=i: prepare_step(i, first + CHUNK_TILES))
+            return calls
+
+        def prepare_step(i, end):
+            group_context(i)
+            if i + 1 < end:
+                turn_context(i + 1)
+            if i + 2 < end:
+                negate_context(i + 2)
             quantise_context(i)
-        project(0)
-        spread_to_sbuf(norm_rows, GAIN_K_ROW, gain_k[:], nc.scalar.copy)
-        spread_to_sbuf(norm_rows, SHIFT_K_ROW, shift_k[:], nc.scalar.copy)
-        spread(norm_rows, GAIN_V_ROW, gain_v)
-        spread(norm_rows, SHIFT_V_ROW, shift_v)
 
-        for r in range(ROUNDS):
-            first = r * GROUP
-            last_round = r == ROUNDS - 1
-            for i in range(first, first + GROUP):
-                if r > 0:
-                    add_noise(i - GROUP)
-                if i + 1 < TILES:
-                    project(i + 1)
-                exponential(i)
-                squares(i)
-                inverse_std(i)
-                if i > first:
-                    finish_k_mu(i - 1)
-                if i + PREP_AHEAD < TILES:
-                    quantise_context(i + PREP_AHEAD)
-            finish_k_mu(first + GROUP - 1)
-            for i in range(first, first + GROUP):
-                logarithm(i)
-                finish_v_mu(i)
-                linear_tail(i)
-            for i in range(first, first + GROUP):
-                square_root(i)
-                scale_noise(i, nc.vector)
-                if last_round:
-                    add_noise(i)
+        def weave(*quanta):
+            for step in range(max(len(q) for q in quanta)):
+                for q in quanta:
+                    if step < len(q):
+                        q[step]()
+
+        K, V = KEY, VALUE
+
+        nothing = []
+        pairs = (((0, V), (1, V)), ((2, V), (3, V)), ((0, K), (1, K)), ((4, V), (5, V)),
+                 ((6, V), (7, V)), ((2, K), (3, K)), ((4, K), (5, K)), ((6, K), (7, K)))
+        a, b, c, d, e, f, g, h = pairs
+
+        def first(pair):
+            return q_normalise(pair[0])
+
+        def second(pair):
+            return q_normalise(pair[1])
+
+        negate_context(0)
+        turn_context(0)
+        negate_context(1)
+        turn_var_bias()
+        spread_by_vector(bias_rows, HALVES * VALUE, bias_mean[:, VALUE, :])
+        for i in range(CHUNK_TILES):
+            prepare_step(i, CHUNK_TILES)
+        weave(q_sigmoid(V, 0, 0), q_project(*a))
+        spread_by_vector(bias_rows, HALVES * KEY, bias_mean[:, KEY, :])
+        spread(norm_rows, 2 * HALVES, gain_v)
+        spread(norm_rows, 3 * HALVES, shift_v)
+        spread_by_scalar(norm_rows, 0, gain_k[:])
+        spread_by_scalar(norm_rows, HALVES, shift_k[:])
+        slots = (
+            (q_squares(*a), q_project(*b), nothing),
+            (q_sigmoid(V, 0, 1), first(a), nothing),
+            (q_prepare(CHUNK_TILES), second(a), nothing),
+            (q_squares(*b), q_project(*c), nothing),
+            (q_sigmoid(V, 1, 0), first(b), nothing),
+            (q_sigmoid(V, 1, 1), second(b), nothing),
+            (q_log(V, 0, 0), q_project(*d), nothing),
+            (q_log(V, 0, 1), q_tail(V, 0, 0), nothing),
+            (q_log(V, 1, 0), q_tail(V, 0, 1), nothing),
+            (q_log(V, 1, 1), q_tail(V, 1, 0), nothing),
+            (q_squares(*c), q_tail(V, 1, 1), nothing),
+            (q_sigma(0, 0), first(c), nothing),
+            (q_sigma(0, 1), second(c), nothing),
+            (q_squares(*d), q_project(*e), q_noise(0)),
+            (q_sigma(1, 0), first(d), q_noise(1)),
+            (q_sigma(1, 1), second(d), q_noise(2)),
+            (q_squares(*e), q_project(*f), q_noise(3)),
+            (q_sigmoid(K, 0, 0), first(e), q_sample(0)),
+            (q_sigmoid(K, 0, 1), second(e), q_sample(1)),
+            (q_squares(*f), q_project(*g), q_sample(2)),
+            (q_sigmoid(K, 1, 0), first(f), q_sample(3)),
+            (q_sigmoid(K, 1, 1), second(f), q_noise(4)),
+            (q_squares(*g), q_project(*h), q_sample(4)),
+            (q_log(K, 0, 0), first(g), q_noise(5)),
+            (q_log(K, 0, 1), q_tail(K, 0, 0), q_sample(5)),
+            (q_log(K, 1, 0), q_tail(K, 0, 1), q_noise(6)),
+            (q_log(K, 1, 1), q_tail(K, 1, 0), q_sample(6)),
+            (q_squares(*h), q_tail(K, 1, 1), q_noise(7)),
+            (q_k_var(0, 0, False), second(g), q_sample(7)),
+            (q_k_var(0, 1, False), first(h), nothing),
+            (q_k_var(1, 0, False), second(h), nothing),
+            (q_k_var(1, 1, False)[:2], q_k_var(1, 1, True)[2:], nothing),
+        )
+        for slot in slots:
+            weave(*slot)

@@ -70,15 +70,14 @@ def tile_probcrossattention_pa_kernel(
         psum = stack.enter_context(tc.psum_pool(name="psum", bufs=1))
         stack.enter_context(tc.manual_schedule())
 
-        context_raw = keep.tile([P, TILES, C], BF16)
         noise = keep.tile([P, TILES, C], BF16)
         context_codes = keep.tile([P, PASSES, TOKENS], U32, align_bytes=64)
         context_scales = keep.tile([P, PASSES, TOKENS], U8, align_bytes=64)
         weight_codes = keep.tile([P, 2, PASSES, 2 * C], U32, align_bytes=64)
         weight_scales = keep.tile([P, 2 * C], U8, align_bytes=64)
         bias_mean = keep.tile([P, 2, C], BF16)
-        gain_k = keep.tile([P, C], BF16)
-        shift_k = keep.tile([P, C], BF16)
+        gain_v = keep.tile([P, C], BF16)
+        shift_v = keep.tile([P, C], BF16)
         bias_rows = keep.tile([P, BANK], BF16)
         norm_rows = keep.tile([P, BANK], BF16)
         var_bias_rows = keep.tile([P, P], BF16)
@@ -91,8 +90,8 @@ def tile_probcrossattention_pa_kernel(
         warm = keep.tile([P, 1], F32)
         v_mu = keep.tile([P, TILES, C], F32)
         sigma = keep.tile([P, TILES, C], F32)
-        gain_v = psum.tile([P, C], BF16)
-        shift_v = psum.tile([P, C], BF16)
+        gain_k = psum.tile([P, C], BF16)
+        shift_k = psum.tile([P, C], BF16)
 
         nc.vector.memset(var_bias_rows[:].bitcast(I32), 0)
         nc.vector.memset(bias_rows[:].bitcast(I32), 0)
@@ -105,8 +104,16 @@ def tile_probcrossattention_pa_kernel(
         make_identity(nc, identity_bf16[:])
         nc.scalar.activation(out=warm[:], in_=minus_half[:], func=ACT.Sigmoid)
 
+        context_raw = {}
+
+        def four_kib(shape, dtype):
+            four_kib_tile = work.tile(shape, dtype, tag="four_kib_tile", bufs=TILES)
+            return four_kib_tile
+
         def load_context(i):
-            nc.sync.dma_start(out=context_raw[:, i, :], in_=context_rows[:, i, :])
+            if i % 2 == 0:
+                context_raw[i // 2] = four_kib([P, 2, C], BF16)
+            nc.sync.dma_start(out=context_raw[i // 2][:, i % 2, :], in_=context_rows[:, i, :])
 
         def load_weight_section(weight, first_column):
             for g in range(PASSES):
@@ -128,20 +135,21 @@ def tile_probcrossattention_pa_kernel(
             rows = vector[first : first + count * width].rearrange("(j n) -> j n", n=width)
             nc.sync.dma_start(out=rows_tile[first_row : first_row + count, :], in_=rows)
 
-        for i in range(CHUNK_TILES):
-            load_context(i)
-        for weight in (KEY, VALUE):
+        load_context(0)
+        for weight in (VALUE, KEY):
             load_rows(bias_in[weight], MEAN, HALVES, BANK, bias_rows, HALVES * weight)
             load_rows(bias_in[weight], VARIANCE, CHANNEL_TILES, P, var_bias_rows, CHANNEL_TILES * weight)
+        for j, vector in enumerate((ln_k_g, ln_k_b, ln_v_g, ln_v_b)):
+            load_rows(vector, 0, HALVES, BANK, norm_rows, HALVES * j)
+        for i in range(1, CHUNK_TILES):
+            load_context(i)
         load_weight_scales(KEY)
         load_weight_scales(VALUE)
         load_weight_section(VALUE, MEAN)
         load_weight_section(VALUE, VARIANCE)
-        for j, vector in enumerate((ln_k_g, ln_k_b, ln_v_g, ln_v_b)):
-            load_rows(vector, 0, HALVES, BANK, norm_rows, HALVES * j)
-        load_weight_section(KEY, MEAN)
         for i in range(CHUNK_TILES, TILES):
             load_context(i)
+        load_weight_section(KEY, MEAN)
         for i in range(TILES):
             nc.sync.dma_start(out=noise[:, i, :], in_=noise_rows[:, i, :])
         load_weight_section(KEY, VARIANCE)
@@ -195,7 +203,7 @@ def tile_probcrossattention_pa_kernel(
 
         def negate_context(i):
             minus = work.tile([P, C], BF16, tag="minus", bufs=3)
-            nc.vector.tensor_scalar_mul(out=minus[:], in0=context_raw[:, i, :], scalar1=-1.0)
+            nc.vector.tensor_scalar_mul(out=minus[:], in0=context_raw[i // 2][:, i % 2, :], scalar1=-1.0)
             negated[i] = minus
 
         def turn_context(i):
@@ -261,8 +269,7 @@ def tile_probcrossattention_pa_kernel(
         def mean_input(i, weight):
             if weight == KEY:
                 if i not in k_mu:
-                    k_mu_tile = work.tile([P, C], F32, tag="k_mu_tile", bufs=4)
-                    k_mu[i] = k_mu_tile
+                    k_mu[i] = four_kib([P, C], F32)
                 return k_mu[i][:]
             return v_mu[:, i, :]
 
@@ -284,7 +291,7 @@ def tile_probcrossattention_pa_kernel(
             )
             if h == HALVES - 1:
                 neg_mean = work.tile([P, 1], F32, tag="neg_mean", bufs=8)
-                nc.vector.tensor_scalar(
+                nc.gpsimd.tensor_scalar(
                     out=neg_mean[:],
                     in0=half_sums[i, weight][:, 0:1],
                     scalar1=half_sums[i, weight][:, 1:2],
@@ -317,17 +324,20 @@ def tile_probcrossattention_pa_kernel(
             nc.gpsimd.tensor_tensor(out=rstd[:], in0=variance[:], in1=minus_half[:], op=ALU.pow)
             inv_std[i, weight] = rstd
 
-        def normalise(i, weight):
+        def centre_and_gain(i, weight):
             x = mean_input(i, weight)
-            gain, shift = ((gain_k, shift_k), (gain_v, shift_v))[weight]
             nc.vector.scalar_tensor_tensor(
                 out=x,
                 in0=x,
                 scalar=minus_mean[i, weight][:],
-                in1=gain[:],
+                in1=(gain_k, gain_v)[weight][:],
                 op0=ALU.add,
                 op1=ALU.mult,
             )
+
+        def scale_and_shift(i, weight):
+            x = mean_input(i, weight)
+            shift = (shift_k, shift_v)[weight]
             nc.vector.scalar_tensor_tensor(
                 out=x,
                 in0=x,
@@ -399,9 +409,7 @@ def tile_probcrossattention_pa_kernel(
         def k_var_out(chunk, half, a, by_vector):
             i = chunk * CHUNK_TILES + a
             columns = slice(half * BANK, (half + 1) * BANK)
-            if half == 0:
-                k_var_tile = work.tile([P, C], F32, tag="k_var_tile", bufs=4)
-                k_var[i] = k_var_tile
+            k_var[i] = v_mu[:, i, :]
             if by_vector:
                 bank = for_vector([P, BANK], F32)
                 turn_back(bank, KEY, chunk, half, a)
@@ -420,7 +428,7 @@ def tile_probcrossattention_pa_kernel(
                     out=k_var[i][:, columns], in_=bank[:], func=ACT.Identity, scale=-1.0, bias=var_eps[:]
                 )
             if half == HALVES - 1:
-                nc.sync.dma_start(out=k_var_rows[i * P : (i + 1) * P, :], in_=k_var[i][:])
+                nc.sync.dma_start(out=k_var_rows[i * P : (i + 1) * P, :], in_=k_var[i])
 
         def sample(i, h):
             columns = slice(h * BANK, (h + 1) * BANK)
@@ -430,48 +438,6 @@ def tile_probcrossattention_pa_kernel(
             if h == HALVES - 1:
                 nc.sync.dma_start(out=v_sample_rows[i * P : (i + 1) * P, :], in_=sigma[:, i, :])
 
-        def q_sigmoid(weight, chunk, half):
-            return [
-                lambda j=j: sigmoid(weight, chunk, j)
-                for j in range(half * CHUNK_TILES, (half + 1) * CHUNK_TILES)
-            ]
-
-        def q_log(weight, chunk, half):
-            return [lambda: logarithm(weight, chunk, half)]
-
-        def q_tail(weight, chunk, half):
-            return [
-                lambda j=j: linear_tail(weight, chunk, j)
-                for j in range(half * CHUNK_TILES, (half + 1) * CHUNK_TILES)
-            ]
-
-        def q_sigma(chunk, half):
-            return [lambda a=a: sigma_out(chunk, half, a) for a in range(CHUNK_TILES)]
-
-        def q_k_var(chunk, half, by_vector):
-            return [lambda a=a: k_var_out(chunk, half, a, by_vector) for a in range(CHUNK_TILES)]
-
-        def q_project(*items):
-            return [lambda i=i, w=w, h=h: project_mean(i, w, h) for i, w in items for h in range(HALVES)]
-
-        def q_squares(*items):
-            return [lambda i=i, w=w: squares(i, w) for i, w in items]
-
-        def q_normalise(*items):
-            return [lambda i=i, w=w: normalise(i, w) for i, w in items]
-
-        def q_noise(i):
-            return [lambda h=h: scale_noise(i, h) for h in range(HALVES)]
-
-        def q_sample(i):
-            return [lambda h=h: sample(i, h) for h in range(HALVES)]
-
-        def q_prepare(first):
-            calls = [lambda: (negate_context(first), turn_context(first), negate_context(first + 1))]
-            for i in range(first, first + CHUNK_TILES):
-                calls.append(lambda i=i: prepare_step(i, first + CHUNK_TILES))
-            return calls
-
         def prepare_step(i, end):
             group_context(i)
             if i + 1 < end:
@@ -480,71 +446,184 @@ def tile_probcrossattention_pa_kernel(
                 negate_context(i + 2)
             quantise_context(i)
 
-        def weave(*quanta):
-            for step in range(max(len(q) for q in quanta)):
-                for q in quanta:
-                    if step < len(q):
-                        q[step]()
+        def start_prepare(i):
+            negate_context(i)
+            turn_context(i)
+            negate_context(i + 1)
+
+        def s_prepare(chunk):
+            begin = chunk * CHUNK_TILES
+            return [(0, lambda: start_prepare(begin), (), None)] + [
+                (1, lambda i=i: prepare_step(i, begin + CHUNK_TILES), (), ("context", i))
+                for i in range(begin, begin + CHUNK_TILES)
+            ]
+
+        def s_sigmoid(weight, chunk):
+            return [(1, lambda j=j: sigmoid(weight, chunk, j), (), None) for j in range(CHANNEL_TILES)]
+
+        def s_log(weight, chunk, half):
+            return [(4, lambda: logarithm(weight, chunk, half), (), ("log", weight, chunk, half))]
+
+        def s_squares(i, weight):
+            return [(2, lambda: squares(i, weight), (("projected", i, weight),), ("squares", i, weight))]
+
+        def tails_of(weight, chunk, half):
+            return tuple(("tail", weight, chunk, half * CHUNK_TILES + q) for q in range(CHUNK_TILES))
+
+        def s_sigma(chunk, half):
+            return [
+                (1, lambda a=a: sigma_out(chunk, half, a), tails_of(VALUE, chunk, half), ("sigma", chunk * CHUNK_TILES + a, half))
+                for a in range(CHUNK_TILES)
+            ]
+
+        def k_var_calls(chunk, half, by_vector):
+            return [
+                (1, lambda a=a: k_var_out(chunk, half, a, by_vector), tails_of(KEY, chunk, half), None)
+                for a in range(CHUNK_TILES)
+            ]
+
+        def v_wait(units):
+            return [(units, lambda: None, (), None)]
+
+        def v_project(i, weight):
+            return [
+                (1, lambda h=h: project_mean(i, weight, h), (("context", i), ("bias", weight)), ("projected", i, weight) if h == HALVES - 1 else None)
+                for h in range(HALVES)
+            ]
+
+        def v_normalise(i, weight):
+            return [
+                (2, lambda: centre_and_gain(i, weight), (("squares", i, weight), ("norm", weight)), None),
+                (2, lambda: scale_and_shift(i, weight), (), ("normalised", i, weight)),
+            ]
+
+        def v_tail(weight, chunk, half):
+            return [
+                (1, lambda j=j: linear_tail(weight, chunk, j), (("log", weight, chunk, half),), ("tail", weight, chunk, j))
+                for j in range(half * CHUNK_TILES, (half + 1) * CHUNK_TILES)
+            ]
+
+        def g_noise(i):
+            return [(2, lambda h=h: scale_noise(i, h), (("sigma", i, h),), None) for h in range(HALVES)]
+
+        def g_sample(i):
+            return [(2, lambda h=h: sample(i, h), (("normalised", i, VALUE),), None) for h in range(HALVES)]
+
+        def merge(*streams):
+            issued = set()
+            position = [start for start, items in streams]
+            index = [0 for stream in streams]
+            while any(index[n] < len(stream[1]) for n, stream in enumerate(streams)):
+                ready = [
+                    n
+                    for n, stream in enumerate(streams)
+                    if index[n] < len(stream[1]) and all(need in issued for need in stream[1][index[n]][2])
+                ]
+                assert ready
+                n = min(ready, key=lambda n: position[n])
+                length, call, needs, gives = streams[n][1][index[n]]
+                call()
+                issued.add(gives)
+                position[n] += length
+                index[n] += 1
 
         K, V = KEY, VALUE
 
-        nothing = []
-        pairs = (((0, V), (1, V)), ((2, V), (3, V)), ((0, K), (1, K)), ((4, V), (5, V)),
-                 ((6, V), (7, V)), ((2, K), (3, K)), ((4, K), (5, K)), ((6, K), (7, K)))
-        a, b, c, d, e, f, g, h = pairs
+        items = [(i, V) for i in range(TILES)] + [(i, K) for i in range(TILES)]
 
-        def first(pair):
-            return q_normalise(pair[0])
+        def call_of(entries):
+            return [entry[1] for entry in entries]
 
-        def second(pair):
-            return q_normalise(pair[1])
+        def A(weight, first, count):
+            banks = s_sigmoid(weight, 0) + s_sigmoid(weight, 1)
+            return call_of(banks[first : first + count])
 
-        negate_context(0)
-        turn_context(0)
-        negate_context(1)
-        turn_var_bias()
+        def B(weight, chunk, half):
+            return call_of(s_log(weight, chunk, half))
+
+        def Q(*ms):
+            return [lambda m=m: squares(*items[m]) for m in ms]
+
+        def E(*tiles):
+            return [lambda i=i: prepare_step(i, TILES) for i in tiles]
+
+        def M(*ms):
+            return [lambda m=m, h=h: project_mean(items[m][0], items[m][1], h) for m in ms for h in range(HALVES)]
+
+        def s1(m):
+            return [lambda: centre_and_gain(*items[m])]
+
+        def s2(m):
+            return [lambda: scale_and_shift(*items[m])]
+
+        def T(weight, chunk, half):
+            return call_of(v_tail(weight, chunk, half))
+
+        def R(chunk, half):
+            return call_of(s_sigma(chunk, half))
+
+        def RK(chunk, half, by_vector):
+            return call_of(k_var_calls(chunk, half, by_vector))
+
+        def noise_half(first, h):
+            return [lambda i=i: scale_noise(i, h) for i in range(first, first + CHUNK_TILES)]
+
+        def samples(*tiles):
+            return [lambda i=i, h=h: sample(i, h) for i in tiles for h in range(HALVES)]
+
+        def weave(*columns):
+            order = sorted(
+                ((j + 0.5) / len(column), c, j) for c, column in enumerate(columns) for j in range(len(column))
+            )
+            for place, c, j in order:
+                columns[c][j]()
+
+        none = []
+
+        def RV(first, count):
+            banks = R(0, 0) + R(0, 1) + R(1, 0) + R(1, 1)
+            return banks[first : first + count]
+
+        start_prepare(0)
         spread_by_vector(bias_rows, HALVES * VALUE, bias_mean[:, VALUE, :])
-        for i in range(CHUNK_TILES):
-            prepare_step(i, CHUNK_TILES)
-        weave(q_sigmoid(V, 0, 0), q_project(*a))
-        spread_by_vector(bias_rows, HALVES * KEY, bias_mean[:, KEY, :])
-        spread(norm_rows, 2 * HALVES, gain_v)
-        spread(norm_rows, 3 * HALVES, shift_v)
-        spread_by_scalar(norm_rows, 0, gain_k[:])
-        spread_by_scalar(norm_rows, HALVES, shift_k[:])
-        slots = (
-            (q_squares(*a), q_project(*b), nothing),
-            (q_sigmoid(V, 0, 1), first(a), nothing),
-            (q_prepare(CHUNK_TILES), second(a), nothing),
-            (q_squares(*b), q_project(*c), nothing),
-            (q_sigmoid(V, 1, 0), first(b), nothing),
-            (q_sigmoid(V, 1, 1), second(b), nothing),
-            (q_log(V, 0, 0), q_project(*d), nothing),
-            (q_log(V, 0, 1), q_tail(V, 0, 0), nothing),
-            (q_log(V, 1, 0), q_tail(V, 0, 1), nothing),
-            (q_log(V, 1, 1), q_tail(V, 1, 0), nothing),
-            (q_squares(*c), q_tail(V, 1, 1), nothing),
-            (q_sigma(0, 0), first(c), nothing),
-            (q_sigma(0, 1), second(c), nothing),
-            (q_squares(*d), q_project(*e), q_noise(0)),
-            (q_sigma(1, 0), first(d), q_noise(1)),
-            (q_sigma(1, 1), second(d), q_noise(2)),
-            (q_squares(*e), q_project(*f), q_noise(3)),
-            (q_sigmoid(K, 0, 0), first(e), q_sample(0)),
-            (q_sigmoid(K, 0, 1), second(e), q_sample(1)),
-            (q_squares(*f), q_project(*g), q_sample(2)),
-            (q_sigmoid(K, 1, 0), first(f), q_sample(3)),
-            (q_sigmoid(K, 1, 1), second(f), q_noise(4)),
-            (q_squares(*g), q_project(*h), q_sample(4)),
-            (q_log(K, 0, 0), first(g), q_noise(5)),
-            (q_log(K, 0, 1), q_tail(K, 0, 0), q_sample(5)),
-            (q_log(K, 1, 0), q_tail(K, 0, 1), q_noise(6)),
-            (q_log(K, 1, 1), q_tail(K, 1, 0), q_sample(6)),
-            (q_squares(*h), q_tail(K, 1, 1), q_noise(7)),
-            (q_k_var(0, 0, False), second(g), q_sample(7)),
-            (q_k_var(0, 1, False), first(h), nothing),
-            (q_k_var(1, 0, False), second(h), nothing),
-            (q_k_var(1, 1, False)[:2], q_k_var(1, 1, True)[2:], nothing),
+        turn_var_bias()
+        prepare_step(0, CHUNK_TILES)
+        prepare_step(1, CHUNK_TILES)
+        weave(M(0))
+        prepare_step(2, CHUNK_TILES)
+        weave(M(1))
+        prepare_step(3, CHUNK_TILES)
+        spread_by_scalar(norm_rows, 2 * HALVES, gain_v[:])
+        spread_by_scalar(norm_rows, 3 * HALVES, shift_v[:])
+        start_prepare(CHUNK_TILES)
+        rows = (
+            (Q(0) + E(4, 5) + A(V, 0, 1), M(2) + s1(0), none),
+            (Q(1) + E(6, 7) + A(V, 1, 1), M(3) + s1(1) + s2(0), none),
+            (Q(2) + A(V, 2, 4), M(4) + s1(2) + s2(1), none),
+            (Q(3) + A(V, 6, 4), M(5) + s1(3) + s2(2), none),
+            (Q(4) + A(V, 10, 4), M(6) + s1(4) + s2(3), none),
+            (Q(5) + A(V, 14, 2) + [lambda: spread_by_scalar(bias_rows, HALVES * KEY, bias_mean[:, KEY, :])],
+             M(7) + s1(5) + s2(4), none),
+            (Q(6) + B(V, 0, 0), [lambda: spread(norm_rows, 0, gain_k), lambda: spread(norm_rows, HALVES, shift_k)]
+             + M(8) + s1(6) + s2(5), none),
+            (Q(7) + B(V, 0, 1), T(V, 0, 0) + s1(7), none),
+            (Q(8) + B(V, 1, 0), T(V, 0, 1) + s2(6), none),
+            (B(V, 1, 1), T(V, 1, 0) + s2(7), none),
+            (RV(0, 6), T(V, 1, 1) + M(9), none),
+            (Q(9) + RV(6, 4), M(10) + s1(8), noise_half(0, 0)[:3]),
+            (Q(10) + RV(10, 4), M(11) + s1(9) + s2(8), noise_half(0, 0)[3:] + noise_half(0, 1)[:2]),
+            (Q(11) + RV(14, 2), M(12) + s1(10) + s2(9), noise_half(0, 1)[2:] + samples(0)[:1]),
+            (Q(12) + A(K, 0, 4), M(13) + s1(11) + s2(10), samples(0)[1:] + samples(1)),
+            (Q(13) + A(K, 4, 4), M(14) + s1(12) + s2(11), samples(2) + samples(3)[:1]),
+            (Q(14) + A(K, 8, 4), M(15) + s1(13) + s2(12), samples(3)[1:] + noise_half(4, 0)[:2]),
+            (Q(15) + A(K, 12, 4), s1(14) + s2(13), noise_half(4, 0)[2:] + noise_half(4, 1)[:1]),
+            (B(K, 0, 0), s1(15) + s2(14) + s2(15), noise_half(4, 1)[1:]),
+            (B(K, 0, 1), T(K, 0, 0), samples(4)),
+            (B(K, 1, 0), T(K, 0, 1), samples(5)),
+            (B(K, 1, 1), T(K, 1, 0), samples(6)),
+            (RK(0, 0, False), T(K, 1, 1), samples(7)),
+            (RK(0, 1, False), RK(1, 0, True), none),
+            (RK(1, 1, False)[:2], RK(1, 1, True)[2:], none),
         )
-        for slot in slots:
-            weave(*slot)
+        for row in rows:
+            weave(*row)

@@ -76,8 +76,8 @@ def tile_probcrossattention_pa_kernel(
         weight_codes = keep.tile([P, 2, PASSES, 2 * C], U32, align_bytes=64)
         weight_scales = keep.tile([P, 2 * C], U8, align_bytes=64)
         bias_mean = keep.tile([P, 2, C], BF16)
-        gain_v = keep.tile([P, C], BF16)
-        shift_v = keep.tile([P, C], BF16)
+        gain_k = keep.tile([P, C], BF16)
+        shift_k = keep.tile([P, C], BF16)
         bias_rows = keep.tile([P, BANK], BF16)
         norm_rows = keep.tile([P, BANK], BF16)
         var_bias_rows = keep.tile([P, P], BF16)
@@ -90,8 +90,8 @@ def tile_probcrossattention_pa_kernel(
         warm = keep.tile([P, 1], F32)
         v_mu = keep.tile([P, TILES, C], F32)
         sigma = keep.tile([P, TILES, C], F32)
-        gain_k = psum.tile([P, C], BF16)
-        shift_k = psum.tile([P, C], BF16)
+        gain_v = psum.tile([P, C], BF16)
+        shift_v = psum.tile([P, C], BF16)
 
         nc.vector.memset(var_bias_rows[:].bitcast(I32), 0)
         nc.vector.memset(bias_rows[:].bitcast(I32), 0)
@@ -136,7 +136,7 @@ def tile_probcrossattention_pa_kernel(
             nc.sync.dma_start(out=rows_tile[first_row : first_row + count, :], in_=rows)
 
         load_context(0)
-        for weight in (VALUE, KEY):
+        for weight in (KEY, VALUE):
             load_rows(bias_in[weight], MEAN, HALVES, BANK, bias_rows, HALVES * weight)
             load_rows(bias_in[weight], VARIANCE, CHANNEL_TILES, P, var_bias_rows, CHANNEL_TILES * weight)
         for j, vector in enumerate((ln_k_g, ln_k_b, ln_v_g, ln_v_b)):
@@ -145,11 +145,11 @@ def tile_probcrossattention_pa_kernel(
             load_context(i)
         load_weight_scales(KEY)
         load_weight_scales(VALUE)
-        load_weight_section(VALUE, MEAN)
+        load_weight_section(KEY, MEAN)
         load_weight_section(VALUE, VARIANCE)
         for i in range(CHUNK_TILES, TILES):
             load_context(i)
-        load_weight_section(KEY, MEAN)
+        load_weight_section(VALUE, MEAN)
         for i in range(TILES):
             nc.sync.dma_start(out=noise[:, i, :], in_=noise_rows[:, i, :])
         load_weight_section(KEY, VARIANCE)
@@ -400,11 +400,19 @@ def tile_probcrossattention_pa_kernel(
                 out=sigma[:, i, columns], in_=bank[:], func=ACT.Sqrt, scale=-1.0, bias=var_eps[:]
             )
 
-        def scale_noise(i, h):
-            columns = slice(h * BANK, (h + 1) * BANK)
-            nc.gpsimd.tensor_tensor(
-                out=sigma[:, i, columns], in0=sigma[:, i, columns], in1=noise[:, i, columns], op=ALU.mult
-            )
+        def sigma_in_place(chunk, half):
+            part = log_sigmoid[VALUE, chunk][:, half * CHUNK_TILES : (half + 1) * CHUNK_TILES, :]
+            nc.scalar.activation(out=part, in_=part, func=ACT.Sqrt, scale=-1.0, bias=var_eps[:])
+
+        def noise_from_bank(chunk, half, a):
+            i = chunk * CHUNK_TILES + a
+            columns = slice(half * BANK, (half + 1) * BANK)
+            bank = for_vector([P, BANK], F32)
+            turn_back(bank, VALUE, chunk, half, a)
+            nc.vector.tensor_tensor(out=sigma[:, i, columns], in0=bank[:], in1=noise[:, i, columns], op=ALU.mult)
+
+        def scale_noise(i):
+            nc.gpsimd.tensor_tensor(out=sigma[:, i, :], in0=sigma[:, i, :], in1=noise[:, i, :], op=ALU.mult)
 
         def k_var_out(chunk, half, a, by_vector):
             i = chunk * CHUNK_TILES + a
@@ -427,16 +435,12 @@ def tile_probcrossattention_pa_kernel(
                 nc.scalar.activation(
                     out=k_var[i][:, columns], in_=bank[:], func=ACT.Identity, scale=-1.0, bias=var_eps[:]
                 )
-            if half == HALVES - 1:
-                nc.sync.dma_start(out=k_var_rows[i * P : (i + 1) * P, :], in_=k_var[i])
+            queue = nc.sync if by_vector else nc.scalar
+            queue.dma_start(out=k_var_rows[i * P : (i + 1) * P, columns], in_=k_var[i][:, columns])
 
-        def sample(i, h):
-            columns = slice(h * BANK, (h + 1) * BANK)
-            nc.gpsimd.tensor_tensor(
-                out=sigma[:, i, columns], in0=sigma[:, i, columns], in1=v_mu[:, i, columns], op=ALU.add
-            )
-            if h == HALVES - 1:
-                nc.sync.dma_start(out=v_sample_rows[i * P : (i + 1) * P, :], in_=sigma[:, i, :])
+        def sample(i):
+            nc.gpsimd.tensor_tensor(out=sigma[:, i, :], in0=sigma[:, i, :], in1=v_mu[:, i, :], op=ALU.add)
+            nc.sync.dma_start(out=v_sample_rows[i * P : (i + 1) * P, :], in_=sigma[:, i, :])
 
         def prepare_step(i, end):
             group_context(i)
@@ -504,10 +508,10 @@ def tile_probcrossattention_pa_kernel(
             ]
 
         def g_noise(i):
-            return [(2, lambda h=h: scale_noise(i, h), (("sigma", i, h),), None) for h in range(HALVES)]
+            return [(4, lambda: scale_noise(i), (), None)]
 
         def g_sample(i):
-            return [(2, lambda h=h: sample(i, h), (("normalised", i, VALUE),), None) for h in range(HALVES)]
+            return [(4, lambda: sample(i), (), None)]
 
         def merge(*streams):
             issued = set()
@@ -529,7 +533,7 @@ def tile_probcrossattention_pa_kernel(
 
         K, V = KEY, VALUE
 
-        items = [(i, V) for i in range(TILES)] + [(i, K) for i in range(TILES)]
+        items = [(i, K) for i in range(TILES)] + [(i, V) for i in range(TILES)]
 
         def call_of(entries):
             return [entry[1] for entry in entries]
@@ -565,11 +569,11 @@ def tile_probcrossattention_pa_kernel(
         def RK(chunk, half, by_vector):
             return call_of(k_var_calls(chunk, half, by_vector))
 
-        def noise_half(first, h):
-            return [lambda i=i: scale_noise(i, h) for i in range(first, first + CHUNK_TILES)]
+        def noises(*tiles):
+            return [lambda i=i: scale_noise(i) for i in tiles]
 
         def samples(*tiles):
-            return [lambda i=i, h=h: sample(i, h) for i in tiles for h in range(HALVES)]
+            return [lambda i=i: sample(i) for i in tiles]
 
         def weave(*columns):
             order = sorted(
@@ -580,12 +584,18 @@ def tile_probcrossattention_pa_kernel(
 
         none = []
 
+        def SQ(chunk, half):
+            return [lambda: sigma_in_place(chunk, half)]
+
+        def NB(chunk, half, first, count):
+            return [lambda a=a: noise_from_bank(chunk, half, a) for a in range(first, first + count)]
+
         def RV(first, count):
             banks = R(0, 0) + R(0, 1) + R(1, 0) + R(1, 1)
             return banks[first : first + count]
 
         start_prepare(0)
-        spread_by_vector(bias_rows, HALVES * VALUE, bias_mean[:, VALUE, :])
+        spread_by_vector(bias_rows, HALVES * KEY, bias_mean[:, KEY, :])
         turn_var_bias()
         prepare_step(0, CHUNK_TILES)
         prepare_step(1, CHUNK_TILES)
@@ -593,8 +603,8 @@ def tile_probcrossattention_pa_kernel(
         prepare_step(2, CHUNK_TILES)
         weave(M(1))
         prepare_step(3, CHUNK_TILES)
-        spread_by_scalar(norm_rows, 2 * HALVES, gain_v[:])
-        spread_by_scalar(norm_rows, 3 * HALVES, shift_v[:])
+        spread_by_scalar(norm_rows, 0, gain_k[:])
+        spread_by_scalar(norm_rows, HALVES, shift_k[:])
         start_prepare(CHUNK_TILES)
         rows = (
             (Q(0) + E(4, 5) + A(V, 0, 1), M(2) + s1(0), none),
@@ -602,27 +612,27 @@ def tile_probcrossattention_pa_kernel(
             (Q(2) + A(V, 2, 4), M(4) + s1(2) + s2(1), none),
             (Q(3) + A(V, 6, 4), M(5) + s1(3) + s2(2), none),
             (Q(4) + A(V, 10, 4), M(6) + s1(4) + s2(3), none),
-            (Q(5) + A(V, 14, 2) + [lambda: spread_by_scalar(bias_rows, HALVES * KEY, bias_mean[:, KEY, :])],
+            (Q(5) + A(V, 14, 2) + [lambda: spread_by_scalar(bias_rows, HALVES * VALUE, bias_mean[:, VALUE, :])],
              M(7) + s1(5) + s2(4), none),
-            (Q(6) + B(V, 0, 0), [lambda: spread(norm_rows, 0, gain_k), lambda: spread(norm_rows, HALVES, shift_k)]
+            (Q(6) + B(V, 0, 0), [lambda: spread(norm_rows, 2 * HALVES, gain_v), lambda: spread(norm_rows, 3 * HALVES, shift_v)]
              + M(8) + s1(6) + s2(5), none),
             (Q(7) + B(V, 0, 1), T(V, 0, 0) + s1(7), none),
             (Q(8) + B(V, 1, 0), T(V, 0, 1) + s2(6), none),
             (B(V, 1, 1), T(V, 1, 0) + s2(7), none),
             (RV(0, 6), T(V, 1, 1) + M(9), none),
-            (Q(9) + RV(6, 4), M(10) + s1(8), noise_half(0, 0)[:3]),
-            (Q(10) + RV(10, 4), M(11) + s1(9) + s2(8), noise_half(0, 0)[3:] + noise_half(0, 1)[:2]),
-            (Q(11) + RV(14, 2), M(12) + s1(10) + s2(9), noise_half(0, 1)[2:] + samples(0)[:1]),
-            (Q(12) + A(K, 0, 4), M(13) + s1(11) + s2(10), samples(0)[1:] + samples(1)),
-            (Q(13) + A(K, 4, 4), M(14) + s1(12) + s2(11), samples(2) + samples(3)[:1]),
-            (Q(14) + A(K, 8, 4), M(15) + s1(13) + s2(12), samples(3)[1:] + noise_half(4, 0)[:2]),
-            (Q(15) + A(K, 12, 4), s1(14) + s2(13), noise_half(4, 0)[2:] + noise_half(4, 1)[:1]),
-            (B(K, 0, 0), s1(15) + s2(14) + s2(15), noise_half(4, 1)[1:]),
-            (B(K, 0, 1), T(K, 0, 0), samples(4)),
-            (B(K, 1, 0), T(K, 0, 1), samples(5)),
-            (B(K, 1, 1), T(K, 1, 0), samples(6)),
-            (RK(0, 0, False), T(K, 1, 1), samples(7)),
-            (RK(0, 1, False), RK(1, 0, True), none),
+            (Q(9) + RV(6, 2) + SQ(1, 0), M(10) + s1(8), none),
+            (Q(10) + SQ(1, 1), M(11) + s1(9) + s2(8) + NB(1, 0, 0, 2), noises(0)),
+            (Q(11), M(12) + s1(10) + s2(9) + NB(1, 0, 2, 2), noises(1)),
+            (Q(12) + A(K, 0, 4), M(13) + s1(11) + s2(10) + NB(1, 1, 0, 2), noises(2)),
+            (Q(13) + A(K, 4, 4), M(14) + s1(12) + s2(11) + NB(1, 1, 2, 2), noises(3)),
+            (Q(14) + A(K, 8, 4), M(15) + s1(13) + s2(12), samples(0)),
+            (Q(15) + A(K, 12, 4), s1(14) + s2(13), samples(1)),
+            (B(K, 0, 0), s1(15) + s2(14) + s2(15), samples(2)),
+            (B(K, 0, 1), T(K, 0, 0), samples(3)),
+            (B(K, 1, 0), T(K, 0, 1), samples(4)),
+            (RK(0, 0, False) + B(K, 1, 1), T(K, 1, 0), samples(5)),
+            (RK(0, 1, False), T(K, 1, 1), samples(6)),
+            (RK(1, 0, False)[:2], RK(1, 0, True)[2:], samples(7)),
             (RK(1, 1, False)[:2], RK(1, 1, True)[2:], none),
         )
         for row in rows:

@@ -26,6 +26,7 @@ CHUNK_TILES = BANK // P
 CHANNEL_TILES = C // P
 VAR_EPS = 1e-6
 LN_EPS = 1e-5
+WARM_UP = 8
 LN_FLOOR = 2.0 ** -60
 
 FLOPS = 2 * TOKENS * C * 4 * C
@@ -88,11 +89,13 @@ def tile_probcrossattention_pa_kernel(
         ln_floor = keep.tile([P, 1], F32)
         minus_half = keep.tile([P, 1], F32)
         warm = keep.tile([P, 1], F32)
+        zeros = keep.tile([P, BANK], BF16)
         v_mu = keep.tile([P, TILES, C], F32)
         sigma = keep.tile([P, TILES, C], F32)
         gain_v = psum.tile([P, C], BF16)
         shift_v = psum.tile([P, C], BF16)
 
+        nc.vector.memset(zeros[:].bitcast(I32), 0)
         nc.vector.memset(var_bias_rows[:].bitcast(I32), 0)
         nc.vector.memset(bias_rows[:].bitcast(I32), 0)
         nc.vector.memset(weight_scales[:].bitcast(I32), 0)
@@ -103,6 +106,11 @@ def tile_probcrossattention_pa_kernel(
         make_identity(nc, identity_f32[:])
         make_identity(nc, identity_bf16[:])
         nc.scalar.activation(out=warm[:], in_=minus_half[:], func=ACT.Sigmoid)
+        idle_bank = psum.tile([P, BANK], F32, tag="bank_for_vector", bufs=3)
+        for repeat in range(WARM_UP):
+            nc.tensor.matmul(
+                out=idle_bank[:], lhsT=zeros[:, :P], rhs=zeros[:], start=True, stop=True
+            )
 
         context_raw = {}
 
@@ -355,7 +363,7 @@ def tile_probcrossattention_pa_kernel(
 
         def sigmoid(weight, chunk, j):
             if j == 0:
-                logs = work.tile([P, CHANNEL_TILES, BANK], F32, tag="logs", bufs=2)
+                logs = work.tile([P, CHANNEL_TILES, BANK], F32, tag="logs", bufs=3)
                 log_sigmoid[weight, chunk] = logs
             bank = for_scalar([P, BANK], F32)
             channels_by_tokens(bank, weight, chunk, j)
@@ -417,7 +425,8 @@ def tile_probcrossattention_pa_kernel(
         def k_var_out(chunk, half, a, by_vector):
             i = chunk * CHUNK_TILES + a
             columns = slice(half * BANK, (half + 1) * BANK)
-            k_var[i] = v_mu[:, i, :]
+            if i not in k_var:
+                k_var[i] = four_kib([P, C], F32)[:]
             if by_vector:
                 bank = for_vector([P, BANK], F32)
                 turn_back(bank, KEY, chunk, half, a)
@@ -577,10 +586,10 @@ def tile_probcrossattention_pa_kernel(
 
         def weave(*columns):
             order = sorted(
-                ((j + 0.5) / len(column), c, j) for c, column in enumerate(columns) for j in range(len(column))
+                ((j + (0.5 if c < 2 else 0.0)) / len(column), -c, j) for c, column in enumerate(columns) for j in range(len(column))
             )
             for place, c, j in order:
-                columns[c][j]()
+                columns[-c][j]()
 
         none = []
 
@@ -622,15 +631,14 @@ def tile_probcrossattention_pa_kernel(
             (RV(0, 6), T(V, 1, 1) + M(9), none),
             (Q(9) + RV(6, 2) + SQ(1, 0), M(10) + s1(8), none),
             (Q(10) + SQ(1, 1), M(11) + s1(9) + s2(8) + NB(1, 0, 0, 2), noises(0)),
-            (Q(11), M(12) + s1(10) + s2(9) + NB(1, 0, 2, 2), noises(1)),
-            (Q(12) + A(K, 0, 4), M(13) + s1(11) + s2(10) + NB(1, 1, 0, 2), noises(2)),
-            (Q(13) + A(K, 4, 4), M(14) + s1(12) + s2(11) + NB(1, 1, 2, 2), noises(3)),
-            (Q(14) + A(K, 8, 4), M(15) + s1(13) + s2(12), samples(0)),
-            (Q(15) + A(K, 12, 4), s1(14) + s2(13), samples(1)),
-            (B(K, 0, 0), s1(15) + s2(14) + s2(15), samples(2)),
-            (B(K, 0, 1), T(K, 0, 0), samples(3)),
-            (B(K, 1, 0), T(K, 0, 1), samples(4)),
-            (RK(0, 0, False) + B(K, 1, 1), T(K, 1, 0), samples(5)),
+            (Q(11) + A(K, 0, 4), M(12) + s1(10) + s2(9) + NB(1, 0, 2, 2), noises(1, 2)),
+            (Q(12) + A(K, 4, 4), M(13) + s1(11) + s2(10) + NB(1, 1, 0, 2), noises(3)),
+            (Q(13) + A(K, 8, 4), M(14) + s1(12) + s2(11) + NB(1, 1, 2, 2), samples(0, 1)),
+            (Q(14) + A(K, 12, 4), M(15) + s1(13) + s2(12), samples(2)),
+            (Q(15) + B(K, 0, 0), s1(14) + s2(13), samples(3)),
+            (B(K, 0, 1), T(K, 0, 0) + s1(15), samples(4)),
+            (B(K, 1, 0), T(K, 0, 1) + s2(14), samples(5)),
+            (RK(0, 0, False) + B(K, 1, 1), s2(15) + T(K, 1, 0), none),
             (RK(0, 1, False), T(K, 1, 1), samples(6)),
             (RK(1, 0, False)[:2], RK(1, 0, True)[2:], samples(7)),
             (RK(1, 1, False)[:2], RK(1, 1, True)[2:], none),

@@ -444,8 +444,7 @@ def tile_probcrossattention_pa_kernel(
                 nc.scalar.activation(
                     out=k_var[i][:, columns], in_=bank[:], func=ACT.Identity, scale=-1.0, bias=var_eps[:]
                 )
-            queue = nc.sync if by_vector else nc.scalar
-            queue.dma_start(out=k_var_rows[i * P : (i + 1) * P, columns], in_=k_var[i][:, columns])
+            nc.sync.dma_start(out=k_var_rows[i * P : (i + 1) * P, columns], in_=k_var[i][:, columns])
 
         def sample(i):
             nc.gpsimd.tensor_tensor(out=sigma[:, i, :], in0=sigma[:, i, :], in1=v_mu[:, i, :], op=ALU.add)

@@ -211,7 +211,17 @@ def tile_probcrossattention_pa_kernel(
 
         def negate_context(i):
             minus = work.tile([P, C], BF16, tag="minus", bufs=3)
-            nc.vector.tensor_scalar_mul(out=minus[:], in0=context_raw[i // 2][:, i % 2, :], scalar1=-1.0)
+            if i < CHUNK_TILES:
+                nc.vector.tensor_scalar_mul(out=minus[:], in0=context_raw[i // 2][:, i % 2, :], scalar1=-1.0)
+            else:
+                nc.gpsimd.tensor_scalar(
+                    out=minus[:],
+                    in0=context_raw[i // 2][:, i % 2, :],
+                    scalar1=-1.0,
+                    scalar2=0.0,
+                    op0=ALU.mult,
+                    op1=ALU.add,
+                )
             negated[i] = minus
 
         def turn_context(i):
@@ -297,17 +307,18 @@ def tile_probcrossattention_pa_kernel(
                 op1=ALU.add,
                 accum_out=half_sums[i, weight][:, h : h + 1],
             )
-            if h == HALVES - 1:
-                neg_mean = work.tile([P, 1], F32, tag="neg_mean", bufs=8)
-                nc.gpsimd.tensor_scalar(
-                    out=neg_mean[:],
-                    in0=half_sums[i, weight][:, 0:1],
-                    scalar1=half_sums[i, weight][:, 1:2],
-                    scalar2=-1.0 / C,
-                    op0=ALU.add,
-                    op1=ALU.mult,
-                )
-                minus_mean[i, weight] = neg_mean
+
+        def minus_mean_of(i, weight):
+            neg_mean = work.tile([P, 1], F32, tag="neg_mean", bufs=8)
+            nc.vector.tensor_scalar(
+                out=neg_mean[:],
+                in0=half_sums[i, weight][:, 0:1],
+                scalar1=half_sums[i, weight][:, 1:2],
+                scalar2=-1.0 / C,
+                op0=ALU.add,
+                op1=ALU.mult,
+            )
+            minus_mean[i, weight] = neg_mean
 
         def squares(i, weight):
             ssq = work.tile([P, 1], F32, tag="ssq", bufs=4)
@@ -319,6 +330,10 @@ def tile_probcrossattention_pa_kernel(
                 bias=minus_mean[i, weight][:],
                 accum_out=ssq[:],
             )
+            square_sum[i, weight] = ssq
+
+        def inverse_std(i, weight):
+            ssq = square_sum[i, weight]
             variance = work.tile([P, 1], F32, tag="variance", bufs=4)
             nc.gpsimd.tensor_scalar(
                 out=variance[:],
@@ -562,6 +577,12 @@ def tile_probcrossattention_pa_kernel(
         def M(*ms):
             return [lambda m=m, h=h: project_mean(items[m][0], items[m][1], h) for m in ms for h in range(HALVES)]
 
+        def NM(m):
+            return [lambda: minus_mean_of(*items[m])]
+
+        def IS(*ms):
+            return [lambda m=m: inverse_std(*items[m]) for m in ms]
+
         def s1(m):
             return [lambda: centre_and_gain(*items[m])]
 
@@ -585,7 +606,9 @@ def tile_probcrossattention_pa_kernel(
 
         def weave(*columns):
             order = sorted(
-                ((j + (0.5 if c < 2 else 0.0)) / len(column), -c, j) for c, column in enumerate(columns) for j in range(len(column))
+                (((j + 0.5) / len(column), j / len(column), 1.0)[max(c - 1, 0)], -c, j)
+                for c, column in enumerate(columns)
+                for j in range(len(column))
             )
             for place, c, j in order:
                 columns[-c][j]()
@@ -609,38 +632,39 @@ def tile_probcrossattention_pa_kernel(
         prepare_step(1, CHUNK_TILES)
         weave(M(0))
         prepare_step(2, CHUNK_TILES)
-        weave(M(1))
+        weave(M(1)[:1] + NM(0) + M(1)[1:])
         prepare_step(3, CHUNK_TILES)
+        weave(NM(1))
         spread_by_scalar(norm_rows, 0, gain_k[:])
         spread_by_scalar(norm_rows, HALVES, shift_k[:])
         start_prepare(CHUNK_TILES)
         rows = (
-            (Q(0) + E(4, 5) + A(V, 0, 1), M(2) + s1(0), none),
-            (Q(1) + E(6, 7) + A(V, 1, 1), M(3) + s1(1) + s2(0), none),
-            (Q(2) + A(V, 2, 4), M(4) + s1(2) + s2(1), none),
-            (Q(3) + A(V, 6, 4), M(5) + s1(3) + s2(2), none),
-            (Q(4) + A(V, 10, 4), M(6) + s1(4) + s2(3), none),
+            (Q(0) + E(4, 5) + A(V, 0, 1), M(2) + s1(0) + NM(2), none, IS(0)),
+            (Q(1) + E(6, 7) + A(V, 1, 1), M(3) + s1(1) + NM(3) + s2(0), none, IS(1)),
+            (Q(2) + A(V, 2, 4), M(4) + s1(2) + NM(4) + s2(1), none, IS(2)),
+            (Q(3) + A(V, 6, 4), M(5) + s1(3) + NM(5) + s2(2), none, IS(3)),
+            (Q(4) + A(V, 10, 4), M(6) + s1(4) + NM(6) + s2(3), none, IS(4)),
             (Q(5) + A(V, 14, 2) + [lambda: spread_by_scalar(bias_rows, HALVES * VALUE, bias_mean[:, VALUE, :])],
-             M(7) + s1(5) + s2(4), none),
+             M(7) + s1(5) + NM(7) + s2(4), none, IS(5)),
             (Q(6) + B(V, 0, 0), [lambda: spread(norm_rows, 2 * HALVES, gain_v), lambda: spread(norm_rows, 3 * HALVES, shift_v)]
-             + M(8) + s1(6) + s2(5), none),
-            (Q(7) + B(V, 0, 1), T(V, 0, 0) + s1(7), none),
-            (Q(8) + B(V, 1, 0), T(V, 0, 1) + s2(6), none),
-            (B(V, 1, 1), T(V, 1, 0) + s2(7), none),
-            (RV(0, 6), T(V, 1, 1) + M(9), none),
-            (Q(9) + RV(6, 2) + SQ(1, 0), M(10) + s1(8), none),
-            (Q(10) + SQ(1, 1), M(11) + s1(9) + s2(8) + NB(1, 0, 0, 2), noises(0)),
-            (Q(11) + A(K, 0, 4), M(12) + s1(10) + s2(9) + NB(1, 0, 2, 2), noises(1, 2)),
-            (Q(12) + A(K, 4, 4), M(13) + s1(11) + s2(10) + NB(1, 1, 0, 2), noises(3)),
-            (Q(13) + A(K, 8, 4), M(14) + s1(12) + s2(11) + NB(1, 1, 2, 2), samples(0, 1)),
-            (Q(14) + A(K, 12, 4), M(15) + s1(13) + s2(12), samples(2)),
-            (Q(15) + B(K, 0, 0), s1(14) + s2(13), samples(3)),
-            (B(K, 0, 1), T(K, 0, 0) + s1(15), samples(4)),
-            (B(K, 1, 0), T(K, 0, 1) + s2(14), samples(5)),
-            (RK(0, 0, False) + B(K, 1, 1), s2(15) + T(K, 1, 0), none),
-            (RK(0, 1, False), T(K, 1, 1), samples(6)),
-            (RK(1, 0, False)[:2], RK(1, 0, True)[2:], samples(7)),
-            (RK(1, 1, False)[:2], RK(1, 1, True)[2:], none),
+             + M(8) + s1(6) + NM(8) + s2(5), none, IS(6)),
+            (Q(7) + B(V, 0, 1), T(V, 0, 0) + s1(7), none, IS(7)),
+            (Q(8) + B(V, 1, 0), T(V, 0, 1) + s2(6), none, IS(8)),
+            (B(V, 1, 1), T(V, 1, 0) + s2(7), none, none),
+            (RV(0, 6), T(V, 1, 1) + M(9), none, none),
+            (RV(6, 2) + Q(9) + SQ(1, 0), NM(9) + M(10) + s1(8) + NM(10), none, IS(9)),
+            (Q(10) + SQ(1, 1), M(11) + s1(9) + NM(11) + s2(8) + NB(1, 0, 0, 2), noises(0), IS(10)),
+            (Q(11) + A(K, 0, 4), M(12) + s1(10) + NM(12) + s2(9) + NB(1, 0, 2, 2), noises(1), IS(11)),
+            (Q(12) + A(K, 4, 4), M(13) + s1(11) + NM(13) + s2(10), noises(2), IS(12)),
+            (Q(13) + A(K, 8, 4), M(14) + s1(12) + NM(14) + s2(11), noises(3), IS(13)),
+            (Q(14) + A(K, 12, 4), M(15) + s1(13) + NM(15) + s2(12), samples(0), IS(14)),
+            (Q(15) + B(K, 0, 0), s1(14) + s2(13) + NB(1, 1, 0, 4), samples(1), IS(15)),
+            (B(K, 0, 1), T(K, 0, 0) + s1(15), samples(2), none),
+            (B(K, 1, 0), T(K, 0, 1) + s2(14), samples(3), none),
+            (RK(0, 0, False) + B(K, 1, 1), s2(15) + T(K, 1, 0), samples(4), none),
+            (RK(0, 1, False), T(K, 1, 1), samples(5), none),
+            (RK(1, 0, False)[:2], RK(1, 0, True)[2:], samples(6), none),
+            (RK(1, 1, False)[:2], RK(1, 1, True)[2:], samples(7), none),
         )
         for row in rows:
             weave(*row)

@@ -143,18 +143,20 @@ def tile_probcrossattention_pa_kernel(
             rows = vector[first : first + count * width].rearrange("(j n) -> j n", n=width)
             nc.sync.dma_start(out=rows_tile[first_row : first_row + count, :], in_=rows)
 
+        norm_in = (ln_k_g, ln_k_b, ln_v_g, ln_v_b)
         load_context(0)
+        load_weight_scales(KEY)
         for weight in (KEY, VALUE):
             load_rows(bias_in[weight], MEAN, HALVES, BANK, bias_rows, HALVES * weight)
-            load_rows(bias_in[weight], VARIANCE, CHANNEL_TILES, P, var_bias_rows, CHANNEL_TILES * weight)
-        for j, vector in enumerate((ln_k_g, ln_k_b, ln_v_g, ln_v_b)):
-            load_rows(vector, 0, HALVES, BANK, norm_rows, HALVES * j)
+        load_weight_section(KEY, MEAN)
         for i in range(1, CHUNK_TILES):
             load_context(i)
-        load_weight_scales(KEY)
+        for weight in (KEY, VALUE):
+            load_rows(bias_in[weight], VARIANCE, CHANNEL_TILES, P, var_bias_rows, CHANNEL_TILES * weight)
         load_weight_scales(VALUE)
-        load_weight_section(KEY, MEAN)
         load_weight_section(VALUE, VARIANCE)
+        for j, vector in enumerate(norm_in):
+            load_rows(vector, 0, HALVES, BANK, norm_rows, HALVES * j)
         for i in range(CHUNK_TILES, TILES):
             load_context(i)
         load_weight_section(VALUE, MEAN)
@@ -627,7 +629,6 @@ def tile_probcrossattention_pa_kernel(
 
         start_prepare(0)
         spread_by_vector(bias_rows, HALVES * KEY, bias_mean[:, KEY, :])
-        turn_var_bias()
         prepare_step(0, CHUNK_TILES)
         prepare_step(1, CHUNK_TILES)
         weave(M(0))
@@ -635,6 +636,7 @@ def tile_probcrossattention_pa_kernel(
         weave(M(1)[:1] + NM(0) + M(1)[1:])
         prepare_step(3, CHUNK_TILES)
         weave(NM(1))
+        turn_var_bias()
         spread_by_scalar(norm_rows, 0, gain_k[:])
         spread_by_scalar(norm_rows, HALVES, shift_k[:])
         start_prepare(CHUNK_TILES)

@@ -425,8 +425,10 @@ def tile_probcrossattention_pa_kernel(
                 out=sigma[:, i, columns], in_=bank[:], func=ACT.Sqrt, scale=-1.0, bias=var_eps[:]
             )
 
-        def sigma_in_place(chunk, half):
-            part = log_sigmoid[VALUE, chunk][:, half * CHUNK_TILES : (half + 1) * CHUNK_TILES, :]
+        def sigma_in_place(chunk, half, first=0, count=CHUNK_TILES):
+            part = log_sigmoid[VALUE, chunk][
+                :, half * CHUNK_TILES : (half + 1) * CHUNK_TILES, first * P : (first + count) * P
+            ]
             nc.scalar.activation(out=part, in_=part, func=ACT.Sqrt, scale=-1.0, bias=var_eps[:])
 
         def noise_from_bank(chunk, half, a):
@@ -617,8 +619,11 @@ def tile_probcrossattention_pa_kernel(
 
         none = []
 
-        def SQ(chunk, half):
-            return [lambda: sigma_in_place(chunk, half)]
+        def SQ(chunk, half, first=0, count=CHUNK_TILES):
+            return [lambda: sigma_in_place(chunk, half, first, count)]
+
+        def RS(chunk, half, first, count):
+            return R(chunk, half)[first : first + count]
 
         def NB(chunk, half, first, count):
             return [lambda a=a: noise_from_bank(chunk, half, a) for a in range(first, first + count)]
@@ -654,19 +659,19 @@ def tile_probcrossattention_pa_kernel(
             (Q(8) + B(V, 1, 0), T(V, 0, 1) + s2(6), none, IS(8)),
             (B(V, 1, 1), T(V, 1, 0) + s2(7), none, none),
             (RV(0, 6), T(V, 1, 1) + M(9), none, none),
-            (RV(6, 2) + Q(9) + SQ(1, 0), NM(9) + M(10) + s1(8) + NM(10), none, IS(9)),
-            (Q(10) + SQ(1, 1), M(11) + s1(9) + NM(11) + s2(8) + NB(1, 0, 0, 2), noises(0), IS(10)),
-            (Q(11) + A(K, 0, 4), M(12) + s1(10) + NM(12) + s2(9) + NB(1, 0, 2, 2), noises(1), IS(11)),
-            (Q(12) + A(K, 4, 4), M(13) + s1(11) + NM(13) + s2(10), noises(2), IS(12)),
-            (Q(13) + A(K, 8, 4), M(14) + s1(12) + NM(14) + s2(11), noises(3), IS(13)),
-            (Q(14) + A(K, 12, 4), M(15) + s1(13) + NM(15) + s2(12), samples(0), IS(14)),
-            (Q(15) + B(K, 0, 0), s1(14) + s2(13) + NB(1, 1, 0, 4), samples(1), IS(15)),
-            (B(K, 0, 1), T(K, 0, 0) + s1(15), samples(2), none),
-            (B(K, 1, 0), T(K, 0, 1) + s2(14), samples(3), none),
-            (RK(0, 0, False) + B(K, 1, 1), s2(15) + T(K, 1, 0), samples(4), none),
-            (RK(0, 1, False), T(K, 1, 1), samples(5), none),
-            (RK(1, 0, False)[:2], RK(1, 0, True)[2:], samples(6), none),
-            (RK(1, 1, False)[:2], RK(1, 1, True)[2:], samples(7), none),
+            (RV(6, 2) + Q(9) + SQ(1, 0), NM(9) + M(10) + s1(8) + NM(10), noises(0), IS(9)),
+            (Q(10) + SQ(1, 1), M(11) + s1(9) + NM(11) + s2(8) + NB(1, 0, 0, 2), noises(1), IS(10)),
+            (Q(11) + A(K, 0, 4), M(12) + s1(10) + NM(12) + s2(9) + NB(1, 0, 2, 2), noises(2), IS(11)),
+            (Q(12) + A(K, 4, 4), M(13) + s1(11) + NM(13) + s2(10), noises(3), IS(12)),
+            (Q(13) + A(K, 8, 4), M(14) + s1(12) + NM(14) + s2(11), samples(0), IS(13)),
+            (Q(14) + A(K, 12, 4), M(15) + s1(13) + NM(15) + s2(12), samples(1), IS(14)),
+            (Q(15) + B(K, 0, 0), s1(14) + s2(13) + NB(1, 1, 0, 4), samples(2), IS(15)),
+            (B(K, 0, 1), T(K, 0, 0) + s1(15), samples(3), none),
+            (B(K, 1, 0), T(K, 0, 1) + s2(14), samples(4), none),
+            (RK(0, 0, False) + B(K, 1, 1), s2(15) + T(K, 1, 0), samples(5), none),
+            (RK(0, 1, False), T(K, 1, 1), samples(6), none),
+            (RK(1, 0, False)[:2], RK(1, 0, True)[2:], samples(7), none),
+            (RK(1, 1, False)[:2], RK(1, 1, True)[2:], none, none),
         )
         for row in rows:
             weave(*row)

@@ -26,6 +26,7 @@ CHUNK_TILES = BANK // P
 CHANNEL_TILES = C // P
 VAR_EPS = 1e-6
 LN_EPS = 1e-5
+RUN = 2
 WARM_UP = 8
 LN_FLOOR = 2.0 ** -60
 
@@ -610,7 +611,7 @@ def tile_probcrossattention_pa_kernel(
 
         def weave(*columns):
             order = sorted(
-                (((j + 0.5) / len(column), j / len(column), 1.0)[max(c - 1, 0)], -c, j)
+                (((j // RUN + 0.5) / ((len(column) + RUN - 1) // RUN), j / len(column), 1.0)[max(c - 1, 0)], -c, j)
                 for c, column in enumerate(columns)
                 for j in range(len(column))
             )

@@ -27,7 +27,6 @@ CHANNEL_TILES = C // P
 VAR_EPS = 1e-6
 LN_EPS = 1e-5
 RUN = 2
-WARM_UP = 8
 LN_FLOOR = 2.0 ** -60
 
 FLOPS = 2 * TOKENS * C * 4 * C
@@ -90,13 +89,11 @@ def tile_probcrossattention_pa_kernel(
         ln_floor = keep.tile([P, 1], F32)
         minus_half = keep.tile([P, 1], F32)
         warm = keep.tile([P, 1], F32)
-        zeros = keep.tile([P, BANK], BF16)
         v_mu = keep.tile([P, TILES, C], F32)
         sigma = keep.tile([P, TILES, C], F32)
         gain_v = psum.tile([P, C], BF16)
         shift_v = psum.tile([P, C], BF16)
 
-        nc.vector.memset(zeros[:].bitcast(I32), 0)
         nc.vector.memset(var_bias_rows[:].bitcast(I32), 0)
         nc.vector.memset(bias_rows[:].bitcast(I32), 0)
         nc.vector.memset(weight_scales[:].bitcast(I32), 0)
@@ -107,11 +104,6 @@ def tile_probcrossattention_pa_kernel(
         make_identity(nc, identity_f32[:])
         make_identity(nc, identity_bf16[:])
         nc.scalar.activation(out=warm[:], in_=minus_half[:], func=ACT.Sigmoid)
-        idle_bank = psum.tile([P, BANK], F32, tag="bank_for_vector", bufs=3)
-        for repeat in range(WARM_UP):
-            nc.tensor.matmul(
-                out=idle_bank[:], lhsT=zeros[:, :P], rhs=zeros[:], start=True, stop=True
-            )
 
         context_raw = {}
 

@@ -75,35 +75,35 @@ def tile_probcrossattention_pa_kernel(
         context_codes = keep.tile([P, PASSES, TOKENS], U32, align_bytes=64)
         context_scales = keep.tile([P, PASSES, TOKENS], U8, align_bytes=64)
         weight_codes = keep.tile([P, 2, PASSES, 2 * C], U32, align_bytes=64)
-        weight_scales = keep.tile([P, 2 * C], U8, align_bytes=64)
+        scales_k = keep.tile([P, 2 * C], U8, align_bytes=64)
+        scales_v = keep.tile([P, 2 * C], U8, align_bytes=64)
+        weight_scales = (scales_k, scales_v)
         bias_mean = keep.tile([P, 2, C], BF16)
         gain_k = keep.tile([P, C], BF16)
         shift_k = keep.tile([P, C], BF16)
-        bias_rows = keep.tile([P, BANK], BF16)
+        gain_v = keep.tile([P, C], BF16)
+        bias_rows = keep.tile([P, P], BF16)
         norm_rows = keep.tile([P, BANK], BF16)
-        var_bias_rows = keep.tile([P, P], BF16)
-        neg_var_bias = keep.tile([P, 2 * CHANNEL_TILES], F32)
+        neg_var_bias = keep.tile([P, 4 * CHANNEL_TILES], F32)
         identity_f32 = keep.tile([P, P], F32)
         identity_bf16 = keep.tile([P, P], BF16)
         var_eps = keep.tile([P, 1], F32)
         ln_floor = keep.tile([P, 1], F32)
-        minus_half = keep.tile([P, 1], F32)
+        minus_half = keep.tile([P, 2], F32)
         warm = keep.tile([P, 1], F32)
         v_mu = keep.tile([P, TILES, C], F32)
-        sigma = keep.tile([P, TILES, C], F32)
-        gain_v = psum.tile([P, C], BF16)
-        shift_v = psum.tile([P, C], BF16)
+        sigma = None
 
-        nc.vector.memset(var_bias_rows[:].bitcast(I32), 0)
         nc.vector.memset(bias_rows[:].bitcast(I32), 0)
-        nc.vector.memset(weight_scales[:].bitcast(I32), 0)
+        nc.vector.memset(scales_v[:].bitcast(I32), 0)
+        nc.vector.memset(scales_k[:].bitcast(I32), 0)
         nc.vector.memset(norm_rows[:].bitcast(I32), 0)
         nc.vector.memset(var_eps[:], VAR_EPS)
         nc.vector.memset(ln_floor[:], LN_FLOOR)
         nc.vector.memset(minus_half[:], -0.5)
         make_identity(nc, identity_f32[:])
         make_identity(nc, identity_bf16[:])
-        nc.scalar.activation(out=warm[:], in_=minus_half[:], func=ACT.Sigmoid)
+        nc.scalar.activation(out=warm[:], in_=var_eps[:], func=ACT.Sigmoid)
 
         context_raw = {}
 
@@ -116,19 +116,24 @@ def tile_probcrossattention_pa_kernel(
                 context_raw[i // 2] = four_kib([P, 2, C], BF16)
             nc.sync.dma_start(out=context_raw[i // 2][:, i % 2, :], in_=context_rows[:, i, :])
 
-        def load_weight_section(weight, first_column):
+        def load_weight_half(weight, first_column):
+            columns = slice(first_column, first_column + BANK)
             for g in range(PASSES):
                 packed = words_in[weight][g].rearrange("p n t -> p (n t)")
                 nc.sync.dma_start(
-                    out=weight_codes[:, weight, g, first_column : first_column + C].bitcast(I32),
-                    in_=packed[:, PACK * first_column : PACK * (first_column + C)].bitcast(I32),
+                    out=weight_codes[:, weight, g, columns].bitcast(I32),
+                    in_=packed[:, PACK * first_column : PACK * (first_column + BANK)].bitcast(I32),
                 )
+
+        def load_weight_section(weight, first_column):
+            load_weight_half(weight, first_column)
+            load_weight_half(weight, first_column + BANK)
 
         def load_weight_scales(weight):
             for quadrant in range(4):
-                first_row = 32 * quadrant + 8 * weight
+                first_row = 32 * quadrant
                 nc.sync.dma_start(
-                    out=weight_scales[first_row : first_row + 8, :].bitcast(I32),
+                    out=weight_scales[weight][first_row : first_row + 8, :].bitcast(I32),
                     in_=scales_in[weight][:, 4 * quadrant : 4 * quadrant + 4, :].bitcast(I32),
                 )
 
@@ -137,25 +142,28 @@ def tile_probcrossattention_pa_kernel(
             nc.sync.dma_start(out=rows_tile[first_row : first_row + count, :], in_=rows)
 
         norm_in = (ln_k_g, ln_k_b, ln_v_g, ln_v_b)
+        def load_bias(weight):
+            load_rows(bias_in[weight], MEAN, 2 * CHANNEL_TILES, P, bias_rows, 2 * CHANNEL_TILES * weight)
+
         load_context(0)
-        load_weight_scales(KEY)
-        for weight in (KEY, VALUE):
-            load_rows(bias_in[weight], MEAN, HALVES, BANK, bias_rows, HALVES * weight)
-        load_weight_section(KEY, MEAN)
-        for i in range(1, CHUNK_TILES):
-            load_context(i)
-        for weight in (KEY, VALUE):
-            load_rows(bias_in[weight], VARIANCE, CHANNEL_TILES, P, var_bias_rows, CHANNEL_TILES * weight)
-        load_weight_scales(VALUE)
-        load_weight_section(VALUE, VARIANCE)
+        load_bias(KEY)
+        load_bias(VALUE)
         for j, vector in enumerate(norm_in):
             load_rows(vector, 0, HALVES, BANK, norm_rows, HALVES * j)
+        for i in range(1, CHUNK_TILES):
+            load_context(i)
+        load_weight_scales(VALUE)
+        load_weight_half(VALUE, VARIANCE)
+        load_weight_scales(KEY)
+        load_weight_half(KEY, MEAN)
+        load_weight_half(VALUE, VARIANCE + BANK)
+        load_weight_half(KEY, MEAN + BANK)
         for i in range(CHUNK_TILES, TILES):
             load_context(i)
+        load_weight_section(KEY, VARIANCE)
         load_weight_section(VALUE, MEAN)
         for i in range(TILES):
             nc.sync.dma_start(out=noise[:, i, :], in_=noise_rows[:, i, :])
-        load_weight_section(KEY, VARIANCE)
 
         negated = {}
         turned = {}
@@ -167,6 +175,8 @@ def tile_probcrossattention_pa_kernel(
         half_sums = {}
         log_sigmoid = {}
         k_var = {}
+        gain = {}
+        shift = {}
 
         def for_scalar(shape, dtype):
             bank_for_scalar = psum.tile(shape, dtype, tag="bank_for_scalar", bufs=3)
@@ -177,10 +187,11 @@ def tile_probcrossattention_pa_kernel(
             return bank_for_vector
 
         def spread(rows_tile, first_row, target):
-            for h in range(HALVES):
+            width = rows_tile.shape[1]
+            for h in range(C // width):
                 j = first_row + h
                 nc.tensor.matmul(
-                    out=target[:, h * BANK : (h + 1) * BANK],
+                    out=target[:, h * width : (h + 1) * width],
                     lhsT=identity_bf16[:, j : j + 1].to_broadcast([P, P]),
                     rhs=rows_tile[:],
                     start=True,
@@ -197,11 +208,14 @@ def tile_probcrossattention_pa_kernel(
             spread(rows_tile, first_row, bank)
             nc.scalar.copy(out=target, in_=bank[:])
 
+        def spread_bias(weight):
+            spread_by_vector(bias_rows, 2 * CHANNEL_TILES * weight, bias_mean[:, weight, :])
+
         def turn_var_bias():
             bank = for_vector([P, C], BF16)
-            nc.tensor.transpose(bank[:, :P], var_bias_rows[:], identity_bf16[:])
+            nc.tensor.transpose(bank[:, :P], bias_rows[:], identity_bf16[:])
             nc.vector.tensor_scalar_mul(
-                out=neg_var_bias[:], in0=bank[:, : 2 * CHANNEL_TILES], scalar1=-1.0
+                out=neg_var_bias[:], in0=bank[:, : 4 * CHANNEL_TILES], scalar1=-1.0
             )
 
         def negate_context(i):
@@ -249,7 +263,7 @@ def tile_probcrossattention_pa_kernel(
                 )
 
         def plane(weight, g, columns):
-            return weight_scales[4 * (PASSES * weight + g) : P, columns]
+            return weight_scales[weight][4 * g : P, columns]
 
         def tokens_by_channels(bank, i, weight, first_column):
             tokens = slice(i * P, (i + 1) * P)
@@ -304,7 +318,7 @@ def tile_probcrossattention_pa_kernel(
             )
 
         def minus_mean_of(i, weight):
-            neg_mean = work.tile([P, 1], F32, tag="neg_mean", bufs=8)
+            neg_mean = work.tile([P, 1], F32, tag="neg_mean", bufs=16)
             nc.vector.tensor_scalar(
                 out=neg_mean[:],
                 in0=half_sums[i, weight][:, 0:1],
@@ -316,31 +330,33 @@ def tile_probcrossattention_pa_kernel(
             minus_mean[i, weight] = neg_mean
 
         def squares(i, weight):
-            ssq = work.tile([P, 1], F32, tag="ssq", bufs=4)
+            pair, column = divmod(i, 2)
+            if column == 0:
+                pair_sums = work.tile([P, 2], F32, tag="pair_sums", bufs=4)
+                square_sum[pair, weight] = pair_sums
             unread = work.tile([P, C], BF16, tag="unread", bufs=1)
             nc.scalar.activation(
                 out=unread[:],
                 in_=mean_input(i, weight),
                 func=ACT.Square,
                 bias=minus_mean[i, weight][:],
-                accum_out=ssq[:],
+                accum_out=square_sum[pair, weight][:, column : column + 1],
             )
-            square_sum[i, weight] = ssq
 
-        def inverse_std(i, weight):
-            ssq = square_sum[i, weight]
-            variance = work.tile([P, 1], F32, tag="variance", bufs=4)
+        def inverse_std(pair, weight):
+            variance = work.tile([P, 2], F32, tag="variance", bufs=4)
             nc.gpsimd.tensor_scalar(
                 out=variance[:],
-                in0=ssq[:],
+                in0=square_sum[pair, weight][:],
                 scalar1=1.0 / C,
                 scalar2=LN_EPS,
                 op0=ALU.mult,
                 op1=ALU.add,
             )
-            rstd = work.tile([P, 1], F32, tag="rstd", bufs=8)
+            rstd = work.tile([P, 2], F32, tag="rstd", bufs=8)
             nc.gpsimd.tensor_tensor(out=rstd[:], in0=variance[:], in1=minus_half[:], op=ALU.pow)
-            inv_std[i, weight] = rstd
+            for column in range(2):
+                inv_std[2 * pair + column, weight] = rstd[:, column : column + 1]
 
         def centre_and_gain(i, weight):
             x = mean_input(i, weight)
@@ -348,19 +364,52 @@ def tile_probcrossattention_pa_kernel(
                 out=x,
                 in0=x,
                 scalar=minus_mean[i, weight][:],
-                in1=(gain_k, gain_v)[weight][:],
+                in1=gain[weight][:],
                 op0=ALU.add,
                 op1=ALU.mult,
             )
 
+        def spread_gain_v():
+            bank = for_vector([P, C], BF16)
+            spread(norm_rows, 2 * HALVES, bank)
+            nc.vector.tensor_copy(out=gain_v[:], in_=bank[:])
+
+        def spread_norm(weight):
+            gain_bank = psum.tile([P, C], BF16, tag="gain_bank", bufs=1)
+            shift_bank = psum.tile([P, C], BF16, tag="shift_bank", bufs=1)
+            spread(norm_rows, 2 * HALVES * weight, gain_bank)
+            spread(norm_rows, 2 * HALVES * weight + HALVES, shift_bank)
+            gain[weight] = gain_bank
+            shift[weight] = shift_bank
+
+        def centre_and_gain_on_gpsimd(i):
+            x = v_mu[:, i, :]
+            nc.gpsimd.tensor_scalar(
+                out=x, in0=x, scalar1=minus_mean[i, VALUE][:], scalar2=1.0, op0=ALU.add, op1=ALU.mult
+            )
+            nc.gpsimd.tensor_tensor(out=x, in0=x, in1=gain_v[:], op=ALU.mult)
+
+        def normalise_on_gpsimd(i):
+            x = k_mu[i][:]
+            nc.gpsimd.tensor_scalar(
+                out=x,
+                in0=x,
+                scalar1=minus_mean[i, KEY][:],
+                scalar2=inv_std[i, KEY],
+                op0=ALU.add,
+                op1=ALU.mult,
+            )
+            nc.gpsimd.tensor_tensor(out=x, in0=x, in1=gain_k[:], op=ALU.mult)
+            nc.gpsimd.tensor_tensor(out=x, in0=x, in1=shift_k[:], op=ALU.add)
+            nc.sync.dma_start(out=k_mu_rows[i * P : (i + 1) * P, :], in_=x)
+
         def scale_and_shift(i, weight):
             x = mean_input(i, weight)
-            shift = (shift_k, shift_v)[weight]
             nc.vector.scalar_tensor_tensor(
                 out=x,
                 in0=x,
-                scalar=inv_std[i, weight][:],
-                in1=shift[:],
+                scalar=inv_std[i, weight],
+                in1=shift[weight][:],
                 op0=ALU.mult,
                 op1=ALU.add,
             )
@@ -368,12 +417,12 @@ def tile_probcrossattention_pa_kernel(
                 nc.sync.dma_start(out=k_mu_rows[i * P : (i + 1) * P, :], in_=x)
 
         def bias_column(weight, j):
-            column = CHANNEL_TILES * weight + j
+            column = 2 * CHANNEL_TILES * weight + CHANNEL_TILES + j
             return neg_var_bias[:, column : column + 1]
 
         def sigmoid(weight, chunk, j):
             if j == 0:
-                logs = work.tile([P, CHANNEL_TILES, BANK], F32, tag="logs", bufs=3)
+                logs = work.tile([P, CHANNEL_TILES, BANK], F32, tag="logs", bufs=4)
                 log_sigmoid[weight, chunk] = logs
             bank = for_scalar([P, BANK], F32)
             channels_by_tokens(bank, weight, chunk, j)
@@ -434,6 +483,52 @@ def tile_probcrossattention_pa_kernel(
         def scale_noise(i):
             nc.gpsimd.tensor_tensor(out=sigma[:, i, :], in0=sigma[:, i, :], in1=noise[:, i, :], op=ALU.mult)
 
+        def times_noise(chunk, j):
+            if j % 4:
+                bank = psum.tile([P, 2, BANK], BF16, tag="shift_bank", bufs=1)
+            else:
+                bank = psum.tile([P, 2, BANK], BF16, tag="gain_bank", bufs=1)
+            for q in range(2):
+                for a in range(CHUNK_TILES):
+                    nc.tensor.transpose(
+                        bank[:, q, a * P : (a + 1) * P],
+                        noise[:, chunk * CHUNK_TILES + a, (j + q) * P : (j + q + 1) * P],
+                        identity_bf16[:],
+                    )
+            part = log_sigmoid[VALUE, chunk][:, j : j + 2, :]
+            nc.vector.tensor_tensor(out=part, in0=part, in1=bank[:], op=ALU.mult)
+
+        def scale_and_add(i, half):
+            columns = slice(half * BANK, (half + 1) * BANK)
+            chunk, a = divmod(i, CHUNK_TILES)
+            bank = for_vector([P, BANK], F32)
+            j = 3 * HALVES + half
+            nc.tensor.matmul(
+                out=bank[:],
+                lhsT=identity_bf16[:, j : j + 1].to_broadcast([P, P]),
+                rhs=norm_rows[:],
+                start=True,
+                stop=False,
+            )
+            for q in range(CHUNK_TILES):
+                nc.tensor.matmul(
+                    out=bank[:, q * P : (q + 1) * P],
+                    lhsT=log_sigmoid[VALUE, chunk][:, half * CHUNK_TILES + q, a * P : (a + 1) * P],
+                    rhs=identity_f32[:],
+                    is_transpose=True,
+                    start=False,
+                    stop=(q == CHUNK_TILES - 1),
+                )
+            nc.vector.scalar_tensor_tensor(
+                out=v_mu[:, i, columns],
+                in0=v_mu[:, i, columns],
+                scalar=inv_std[i, VALUE],
+                in1=bank[:],
+                op0=ALU.mult,
+                op1=ALU.add,
+            )
+            nc.sync.dma_start(out=v_sample_rows[i * P : (i + 1) * P, columns], in_=v_mu[:, i, columns])
+
         def k_var_out(chunk, half, a, by_vector):
             i = chunk * CHUNK_TILES + a
             columns = slice(half * BANK, (half + 1) * BANK)
@@ -460,7 +555,14 @@ def tile_probcrossattention_pa_kernel(
 
         def sample(i):
             nc.gpsimd.tensor_tensor(out=sigma[:, i, :], in0=sigma[:, i, :], in1=v_mu[:, i, :], op=ALU.add)
+
+        def store_sample(i):
             nc.sync.dma_start(out=v_sample_rows[i * P : (i + 1) * P, :], in_=sigma[:, i, :])
+
+        def start_prepare(i):
+            negate_context(i)
+            turn_context(i)
+            negate_context(i + 1)
 
         def prepare_step(i, end):
             group_context(i)
@@ -470,100 +572,17 @@ def tile_probcrossattention_pa_kernel(
                 negate_context(i + 2)
             quantise_context(i)
 
-        def start_prepare(i):
-            negate_context(i)
-            turn_context(i)
-            negate_context(i + 1)
-
-        def s_prepare(chunk):
-            begin = chunk * CHUNK_TILES
-            return [(0, lambda: start_prepare(begin), (), None)] + [
-                (1, lambda i=i: prepare_step(i, begin + CHUNK_TILES), (), ("context", i))
-                for i in range(begin, begin + CHUNK_TILES)
-            ]
-
-        def s_sigmoid(weight, chunk):
-            return [(1, lambda j=j: sigmoid(weight, chunk, j), (), None) for j in range(CHANNEL_TILES)]
-
-        def s_log(weight, chunk, half):
-            return [(4, lambda: logarithm(weight, chunk, half), (), ("log", weight, chunk, half))]
-
-        def s_squares(i, weight):
-            return [(2, lambda: squares(i, weight), (("projected", i, weight),), ("squares", i, weight))]
-
-        def tails_of(weight, chunk, half):
-            return tuple(("tail", weight, chunk, half * CHUNK_TILES + q) for q in range(CHUNK_TILES))
-
-        def s_sigma(chunk, half):
-            return [
-                (1, lambda a=a: sigma_out(chunk, half, a), tails_of(VALUE, chunk, half), ("sigma", chunk * CHUNK_TILES + a, half))
-                for a in range(CHUNK_TILES)
-            ]
-
-        def k_var_calls(chunk, half, by_vector):
-            return [
-                (1, lambda a=a: k_var_out(chunk, half, a, by_vector), tails_of(KEY, chunk, half), None)
-                for a in range(CHUNK_TILES)
-            ]
-
-        def v_wait(units):
-            return [(units, lambda: None, (), None)]
-
-        def v_project(i, weight):
-            return [
-                (1, lambda h=h: project_mean(i, weight, h), (("context", i), ("bias", weight)), ("projected", i, weight) if h == HALVES - 1 else None)
-                for h in range(HALVES)
-            ]
-
-        def v_normalise(i, weight):
-            return [
-                (2, lambda: centre_and_gain(i, weight), (("squares", i, weight), ("norm", weight)), None),
-                (2, lambda: scale_and_shift(i, weight), (), ("normalised", i, weight)),
-            ]
-
-        def v_tail(weight, chunk, half):
-            return [
-                (1, lambda j=j: linear_tail(weight, chunk, j), (("log", weight, chunk, half),), ("tail", weight, chunk, j))
-                for j in range(half * CHUNK_TILES, (half + 1) * CHUNK_TILES)
-            ]
-
-        def g_noise(i):
-            return [(4, lambda: scale_noise(i), (), None)]
-
-        def g_sample(i):
-            return [(4, lambda: sample(i), (), None)]
-
-        def merge(*streams):
-            issued = set()
-            position = [start for start, items in streams]
-            index = [0 for stream in streams]
-            while any(index[n] < len(stream[1]) for n, stream in enumerate(streams)):
-                ready = [
-                    n
-                    for n, stream in enumerate(streams)
-                    if index[n] < len(stream[1]) and all(need in issued for need in stream[1][index[n]][2])
-                ]
-                assert ready
-                n = min(ready, key=lambda n: position[n])
-                length, call, needs, gives = streams[n][1][index[n]]
-                call()
-                issued.add(gives)
-                position[n] += length
-                index[n] += 1
-
         K, V = KEY, VALUE
 
         items = [(i, K) for i in range(TILES)] + [(i, V) for i in range(TILES)]
+        none = []
 
-        def call_of(entries):
-            return [entry[1] for entry in entries]
-
-        def A(weight, first, count):
-            banks = s_sigmoid(weight, 0) + s_sigmoid(weight, 1)
-            return call_of(banks[first : first + count])
+        def A(first, count):
+            banks = [(w, chunk, j) for w in (V, K) for chunk in range(CHUNKS) for j in range(CHANNEL_TILES)]
+            return [lambda b=b: sigmoid(*b) for b in banks[first : first + count]]
 
         def B(weight, chunk, half):
-            return call_of(s_log(weight, chunk, half))
+            return [lambda: logarithm(weight, chunk, half)]
 
         def Q(*ms):
             return [lambda m=m: squares(*items[m]) for m in ms]
@@ -578,28 +597,49 @@ def tile_probcrossattention_pa_kernel(
             return [lambda: minus_mean_of(*items[m])]
 
         def IS(*ms):
-            return [lambda m=m: inverse_std(*items[m]) for m in ms]
+            return [lambda m=m: inverse_std(items[m][0] // 2, items[m][1]) for m in ms]
 
-        def s1(m):
-            return [lambda: centre_and_gain(*items[m])]
+        def s1(*ms):
+            return [lambda m=m: centre_and_gain(*items[m]) for m in ms]
 
-        def s2(m):
-            return [lambda: scale_and_shift(*items[m])]
+        def G1(*ms):
+            return [lambda m=m: centre_and_gain_on_gpsimd(m - TILES) for m in ms]
 
-        def T(weight, chunk, half):
-            return call_of(v_tail(weight, chunk, half))
+        def MH(m, h):
+            return [lambda: project_mean(items[m][0], items[m][1], h)]
 
-        def R(chunk, half):
-            return call_of(s_sigma(chunk, half))
+        def GN(*ms):
+            return [lambda m=m: normalise_on_gpsimd(m) for m in ms]
 
-        def RK(chunk, half, by_vector):
-            return call_of(k_var_calls(chunk, half, by_vector))
+        def F(*ms):
+            return [lambda m=m: scale_and_shift(*items[m]) for m in ms]
 
-        def noises(*tiles):
-            return [lambda i=i: scale_noise(i) for i in tiles]
+        def T(weight, chunk, half, first=0, count=CHUNK_TILES):
+            return [lambda j=j: linear_tail(weight, chunk, half * CHUNK_TILES + j) for j in range(first, first + count)]
 
-        def samples(*tiles):
+        def SQ(chunk, half):
+            return [lambda: sigma_in_place(chunk, half)]
+
+        def NB(chunk, half, first=0, count=CHUNK_TILES):
+            return [lambda a=a: noise_from_bank(chunk, half, a) for a in range(first, first + count)]
+
+        def NT(chunk, half):
+            return [lambda j=j: times_noise(chunk, half * CHUNK_TILES + j) for j in range(0, CHUNK_TILES, 2)]
+
+        def SAH(h, *tiles):
+            return [lambda i=i: scale_and_add(i, h) for i in tiles]
+
+        def SA(*tiles):
+            return [lambda i=i, h=h: scale_and_add(i, h) for i in tiles for h in range(HALVES)]
+
+        def SD(*tiles):
+            return [lambda i=i: store_sample(i) for i in tiles]
+
+        def S(*tiles):
             return [lambda i=i: sample(i) for i in tiles]
+
+        def RK(chunk, half, by_vector, first=0, count=CHUNK_TILES):
+            return [lambda a=a: k_var_out(chunk, half, a, by_vector) for a in range(first, first + count)]
 
         def weave(*columns):
             order = sorted(
@@ -610,61 +650,50 @@ def tile_probcrossattention_pa_kernel(
             for place, c, j in order:
                 columns[-c][j]()
 
-        none = []
+        def copy_k(target, banks, weight=K):
+            return [lambda: nc.vector.tensor_copy(out=target[:], in_=banks[weight][:])]
 
-        def SQ(chunk, half, first=0, count=CHUNK_TILES):
-            return [lambda: sigma_in_place(chunk, half, first, count)]
-
-        def RS(chunk, half, first, count):
-            return R(chunk, half)[first : first + count]
-
-        def NB(chunk, half, first, count):
-            return [lambda a=a: noise_from_bank(chunk, half, a) for a in range(first, first + count)]
-
-        def RV(first, count):
-            banks = R(0, 0) + R(0, 1) + R(1, 0) + R(1, 1)
-            return banks[first : first + count]
+        def by_scalar(rows_tile, first_row, target):
+            return [lambda: spread_by_scalar(rows_tile, first_row, target)]
 
         start_prepare(0)
-        spread_by_vector(bias_rows, HALVES * KEY, bias_mean[:, KEY, :])
+        turn_var_bias()
         prepare_step(0, CHUNK_TILES)
         prepare_step(1, CHUNK_TILES)
-        weave(M(0))
         prepare_step(2, CHUNK_TILES)
-        weave(M(1)[:1] + NM(0) + M(1)[1:])
         prepare_step(3, CHUNK_TILES)
-        weave(NM(1))
-        turn_var_bias()
-        spread_by_scalar(norm_rows, 0, gain_k[:])
-        spread_by_scalar(norm_rows, HALVES, shift_k[:])
-        start_prepare(CHUNK_TILES)
+        spread_bias(K)
+        spread_norm(K)
         rows = (
-            (Q(0) + E(4, 5) + A(V, 0, 1), M(2) + s1(0) + NM(2), none, IS(0)),
-            (Q(1) + E(6, 7) + A(V, 1, 1), M(3) + s1(1) + NM(3) + s2(0), none, IS(1)),
-            (Q(2) + A(V, 2, 4), M(4) + s1(2) + NM(4) + s2(1), none, IS(2)),
-            (Q(3) + A(V, 6, 4), M(5) + s1(3) + NM(5) + s2(2), none, IS(3)),
-            (Q(4) + A(V, 10, 4), M(6) + s1(4) + NM(6) + s2(3), none, IS(4)),
-            (Q(5) + A(V, 14, 2) + [lambda: spread_by_scalar(bias_rows, HALVES * VALUE, bias_mean[:, VALUE, :])],
-             M(7) + s1(5) + NM(7) + s2(4), none, IS(5)),
-            (Q(6) + B(V, 0, 0), [lambda: spread(norm_rows, 2 * HALVES, gain_v), lambda: spread(norm_rows, 3 * HALVES, shift_v)]
-             + M(8) + s1(6) + NM(8) + s2(5), none, IS(6)),
-            (Q(7) + B(V, 0, 1), T(V, 0, 0) + s1(7), none, IS(7)),
-            (Q(8) + B(V, 1, 0), T(V, 0, 1) + s2(6), none, IS(8)),
-            (B(V, 1, 1), T(V, 1, 0) + s2(7), none, none),
-            (RV(0, 6), T(V, 1, 1) + M(9), none, none),
-            (RV(6, 2) + Q(9) + SQ(1, 0), NM(9) + M(10) + s1(8) + NM(10), noises(0), IS(9)),
-            (Q(10) + SQ(1, 1), M(11) + s1(9) + NM(11) + s2(8) + NB(1, 0, 0, 2), noises(1), IS(10)),
-            (Q(11) + A(K, 0, 4), M(12) + s1(10) + NM(12) + s2(9) + NB(1, 0, 2, 2), noises(2), IS(11)),
-            (Q(12) + A(K, 4, 4), M(13) + s1(11) + NM(13) + s2(10), noises(3), IS(12)),
-            (Q(13) + A(K, 8, 4), M(14) + s1(12) + NM(14) + s2(11), samples(0), IS(13)),
-            (Q(14) + A(K, 12, 4), M(15) + s1(13) + NM(15) + s2(12), samples(1), IS(14)),
-            (Q(15) + B(K, 0, 0), s1(14) + s2(13) + NB(1, 1, 0, 4), samples(2), IS(15)),
-            (B(K, 0, 1), T(K, 0, 0) + s1(15), samples(3), none),
-            (B(K, 1, 0), T(K, 0, 1) + s2(14), samples(4), none),
-            (RK(0, 0, False) + B(K, 1, 1), s2(15) + T(K, 1, 0), samples(5), none),
-            (RK(0, 1, False), T(K, 1, 1), samples(6), none),
-            (RK(1, 0, False)[:2], RK(1, 0, True)[2:], samples(7), none),
-            (RK(1, 1, False)[:2], RK(1, 1, True)[2:], none, none),
+            (A(0, 4), MH(0, 0) + MH(1, 0), none, none),
+            (A(4, 4), MH(0, 1) + NM(0) + MH(1, 1) + copy_k(gain_k, gain) + NM(1), none, none),
+            (Q(0) + [lambda: start_prepare(CHUNK_TILES)] + E(4), M(2) + copy_k(shift_k, shift) + NM(2), none, none),
+            (Q(1) + E(5, 6), M(3) + NM(3), none, IS(0)),
+            (Q(2) + E(7) + Q(3), M(4) + NM(4) + s1(0), none, IS(2)),
+            (Q(4) + A(8, 3), M(5) + F(0) + NM(5), GN(3), none),
+            (Q(5) + A(11, 3), M(6) + s1(1) + NM(6), none, IS(4)),
+            (Q(6) + A(14, 3), M(7) + F(1) + [lambda: spread_bias(V)] + NM(7), GN(5), none),
+            (Q(7) + A(17, 3), M(8) + s1(2) + NM(8), none, IS(6)),
+            (Q(8) + A(20, 3), M(9) + F(2) + NM(9), none, none),
+            (Q(9) + A(23, 3), M(10) + s1(4) + NM(10), GN(6), IS(8)),
+            (Q(10) + A(26, 3), M(11) + F(4) + NM(11), GN(7), none),
+            (Q(11) + A(29, 3), M(12) + [spread_gain_v] + NM(12), none, IS(10)),
+            (Q(12) + B(V, 0, 0), M(13) + NM(13) + M(14) + NM(14) + M(15) + NM(15), G1(8), none),
+            (Q(13) + B(V, 0, 1), T(V, 0, 0), G1(9), IS(12)),
+            (B(V, 1, 0), T(V, 0, 1), G1(10), none),
+            (B(V, 1, 1), T(V, 1, 0), none, none),
+            (B(K, 0, 0), T(V, 1, 1), G1(11), none),
+            (B(K, 0, 1), T(K, 0, 0), none, none),
+            (B(K, 1, 0), T(K, 0, 1), G1(12), none),
+            (B(K, 1, 1), T(K, 1, 0), none, none),
+            (SQ(0, 0), T(K, 1, 1), G1(13), none),
+            (SQ(0, 1) + Q(14), NT(0, 0), none, none),
+            (SQ(1, 0) + Q(15), NT(0, 1) + SAH(0, 0, 1), none, IS(14)),
+            (SQ(1, 1) + RK(0, 0, False)[:2], SAH(1, 0, 1) + SA(2), G1(14), none),
+            (RK(0, 0, False)[2:] + RK(0, 1, False), NT(1, 0) + SA(3), G1(15), none),
+            (RK(1, 0, False), NT(1, 1) + SA(4), none, none),
+            (RK(1, 1, False)[:3], SA(5, 6), none, none),
+            (RK(1, 1, False)[3:], SA(7), none, none),
         )
         for row in rows:
             weave(*row)

@@ -490,10 +490,12 @@ def tile_probcrossattention_pa_kernel(
                 bank = psum.tile([P, 2, BANK], BF16, tag="gain_bank", bufs=1)
             for q in range(2):
                 for a in range(CHUNK_TILES):
-                    nc.tensor.transpose(
-                        bank[:, q, a * P : (a + 1) * P],
-                        noise[:, chunk * CHUNK_TILES + a, (j + q) * P : (j + q + 1) * P],
-                        identity_bf16[:],
+                    nc.tensor.matmul(
+                        out=bank[:, q, a * P : (a + 1) * P],
+                        lhsT=noise[:, chunk * CHUNK_TILES + a, (j + q) * P : (j + q + 1) * P],
+                        rhs=identity_bf16[:],
+                        start=True,
+                        stop=True,
                     )
             part = log_sigmoid[VALUE, chunk][:, j : j + 2, :]
             nc.vector.tensor_tensor(out=part, in0=part, in1=bank[:], op=ALU.mult)

@@ -145,19 +145,18 @@ def tile_probcrossattention_pa_kernel(
         def load_bias(weight):
             load_rows(bias_in[weight], MEAN, 2 * CHANNEL_TILES, P, bias_rows, 2 * CHANNEL_TILES * weight)
 
-        load_context(0)
+        for i in range(CHUNK_TILES):
+            load_context(i)
         load_bias(KEY)
         load_bias(VALUE)
         for j, vector in enumerate(norm_in):
             load_rows(vector, 0, HALVES, BANK, norm_rows, HALVES * j)
-        for i in range(1, CHUNK_TILES):
-            load_context(i)
         load_weight_scales(VALUE)
         load_weight_half(VALUE, VARIANCE)
         load_weight_scales(KEY)
         load_weight_half(KEY, MEAN)
-        load_weight_half(VALUE, VARIANCE + BANK)
         load_weight_half(KEY, MEAN + BANK)
+        load_weight_half(VALUE, VARIANCE + BANK)
         for i in range(CHUNK_TILES, TILES):
             load_context(i)
         load_weight_section(KEY, VARIANCE)
@@ -529,7 +528,8 @@ def tile_probcrossattention_pa_kernel(
                 op0=ALU.mult,
                 op1=ALU.add,
             )
-            nc.sync.dma_start(out=v_sample_rows[i * P : (i + 1) * P, columns], in_=v_mu[:, i, columns])
+            if half == HALVES - 1:
+                nc.sync.dma_start(out=v_sample_rows[i * P : (i + 1) * P, :], in_=v_mu[:, i, :])
 
         def k_var_out(chunk, half, a, by_vector):
             i = chunk * CHUNK_TILES + a
@@ -553,7 +553,8 @@ def tile_probcrossattention_pa_kernel(
                 nc.scalar.activation(
                     out=k_var[i][:, columns], in_=bank[:], func=ACT.Identity, scale=-1.0, bias=var_eps[:]
                 )
-            nc.sync.dma_start(out=k_var_rows[i * P : (i + 1) * P, columns], in_=k_var[i][:, columns])
+            if half == HALVES - 1:
+                nc.sync.dma_start(out=k_var_rows[i * P : (i + 1) * P, :], in_=k_var[i])
 
         def sample(i):
             nc.gpsimd.tensor_tensor(out=sigma[:, i, :], in0=sigma[:, i, :], in1=v_mu[:, i, :], op=ALU.add)
@@ -640,6 +641,13 @@ def tile_probcrossattention_pa_kernel(
         def S(*tiles):
             return [lambda i=i: sample(i) for i in tiles]
 
+        def RT(by_vector, *tiles):
+            return [
+                lambda i=i, h=h: k_var_out(i // CHUNK_TILES, h, i % CHUNK_TILES, by_vector)
+                for i in tiles
+                for h in range(HALVES)
+            ]
+
         def RK(chunk, half, by_vector, first=0, count=CHUNK_TILES):
             return [lambda a=a: k_var_out(chunk, half, a, by_vector) for a in range(first, first + count)]
 
@@ -659,13 +667,13 @@ def tile_probcrossattention_pa_kernel(
             return [lambda: spread_by_scalar(rows_tile, first_row, target)]
 
         start_prepare(0)
-        turn_var_bias()
         prepare_step(0, CHUNK_TILES)
+        turn_var_bias()
         prepare_step(1, CHUNK_TILES)
         prepare_step(2, CHUNK_TILES)
+        spread_norm(K)
         prepare_step(3, CHUNK_TILES)
         spread_bias(K)
-        spread_norm(K)
         rows = (
             (A(0, 4), MH(0, 0) + MH(1, 0), none, none),
             (A(4, 4), MH(0, 1) + NM(0) + MH(1, 1) + copy_k(gain_k, gain) + NM(1), none, none),
@@ -690,12 +698,12 @@ def tile_probcrossattention_pa_kernel(
             (B(K, 1, 1), T(K, 1, 0), none, none),
             (SQ(0, 0), T(K, 1, 1), G1(13), none),
             (SQ(0, 1) + Q(14), NT(0, 0), none, none),
-            (SQ(1, 0) + Q(15), NT(0, 1) + SAH(0, 0, 1), none, IS(14)),
-            (SQ(1, 1) + RK(0, 0, False)[:2], SAH(1, 0, 1) + SA(2), G1(14), none),
-            (RK(0, 0, False)[2:] + RK(0, 1, False), NT(1, 0) + SA(3), G1(15), none),
-            (RK(1, 0, False), NT(1, 1) + SA(4), none, none),
-            (RK(1, 1, False)[:3], SA(5, 6), none, none),
-            (RK(1, 1, False)[3:], SA(7), none, none),
+            (SQ(1, 0) + Q(15), NT(0, 1) + SA(0), none, IS(14)),
+            (SQ(1, 1) + RT(False, 0), NT(1, 0) + SA(1), G1(14), none),
+            (RT(False, 1, 2), NT(1, 1) + SA(2), G1(15), none),
+            (RT(False, 3, 4), SA(3, 4), none, none),
+            (RT(False, 5, 6), SA(5, 6), none, none),
+            (RT(False, 7), SA(7), none, none),
         )
         for row in rows:
             weave(*row)

@@ -89,11 +89,13 @@ def tile_probcrossattention_pa_kernel(
         identity_bf16 = keep.tile([P, P], BF16)
         var_eps = keep.tile([P, 1], F32)
         ln_floor = keep.tile([P, 1], F32)
+        zeros = keep.tile([P, BANK], BF16)
         minus_half = keep.tile([P, 2], F32)
         warm = keep.tile([P, 1], F32)
         v_mu = keep.tile([P, TILES, C], F32)
         sigma = None
 
+        nc.vector.memset(zeros[:].bitcast(I32), 0)
         nc.vector.memset(bias_rows[:].bitcast(I32), 0)
         nc.vector.memset(scales_v[:].bitcast(I32), 0)
         nc.vector.memset(scales_k[:].bitcast(I32), 0)
@@ -176,6 +178,7 @@ def tile_probcrossattention_pa_kernel(
         k_var = {}
         gain = {}
         shift = {}
+        sample_banks = {}
 
         def for_scalar(shape, dtype):
             bank_for_scalar = psum.tile(shape, dtype, tag="bank_for_scalar", bufs=3)
@@ -499,32 +502,41 @@ def tile_probcrossattention_pa_kernel(
             part = log_sigmoid[VALUE, chunk][:, j : j + 2, :]
             nc.vector.tensor_tensor(out=part, in0=part, in1=bank[:], op=ALU.mult)
 
+        def add_samples(i):
+            chunk, a = divmod(i, CHUNK_TILES)
+            banks = []
+            for half in range(HALVES):
+                bank = for_vector([P, BANK], F32)
+                j = 3 * HALVES + half
+                nc.tensor.matmul(
+                    out=bank[:],
+                    lhsT=identity_bf16[:, j : j + 1].to_broadcast([P, P]),
+                    rhs=norm_rows[:],
+                    start=True,
+                    stop=False,
+                )
+                banks.append(bank)
+            for half in range(HALVES):
+                for q in range(CHUNK_TILES):
+                    nc.tensor.matmul(
+                        out=banks[half][:, q * P : (q + 1) * P],
+                        lhsT=log_sigmoid[VALUE, chunk][:, half * CHUNK_TILES + q, a * P : (a + 1) * P],
+                        rhs=identity_f32[:],
+                        is_transpose=True,
+                        start=False,
+                        stop=(q == CHUNK_TILES - 1),
+                    )
+            sample_banks[i] = banks
+
         def scale_and_add(i, half):
             columns = slice(half * BANK, (half + 1) * BANK)
-            chunk, a = divmod(i, CHUNK_TILES)
-            bank = for_vector([P, BANK], F32)
-            j = 3 * HALVES + half
-            nc.tensor.matmul(
-                out=bank[:],
-                lhsT=identity_bf16[:, j : j + 1].to_broadcast([P, P]),
-                rhs=norm_rows[:],
-                start=True,
-                stop=False,
-            )
-            for q in range(CHUNK_TILES):
-                nc.tensor.matmul(
-                    out=bank[:, q * P : (q + 1) * P],
-                    lhsT=log_sigmoid[VALUE, chunk][:, half * CHUNK_TILES + q, a * P : (a + 1) * P],
-                    rhs=identity_f32[:],
-                    is_transpose=True,
-                    start=False,
-                    stop=(q == CHUNK_TILES - 1),
-                )
+            if half == 0:
+                add_samples(i)
             nc.vector.scalar_tensor_tensor(
                 out=v_mu[:, i, columns],
                 in0=v_mu[:, i, columns],
                 scalar=inv_std[i, VALUE],
-                in1=bank[:],
+                in1=sample_banks[i][half][:],
                 op0=ALU.mult,
                 op1=ALU.add,
             )
@@ -666,6 +678,9 @@ def tile_probcrossattention_pa_kernel(
         def by_scalar(rows_tile, first_row, target):
             return [lambda: spread_by_scalar(rows_tile, first_row, target)]
 
+        warm_bank = psum.tile([P, BANK], F32, tag="bank_for_vector", bufs=3)
+        for turn in range(4):
+            nc.tensor.matmul(out=warm_bank[:], lhsT=zeros[:, :P], rhs=zeros[:], start=True, stop=True)
         start_prepare(0)
         prepare_step(0, CHUNK_TILES)
         turn_var_bias()

@@ -178,7 +178,7 @@ def tile_probcrossattention_pa_kernel(
         k_var = {}
         gain = {}
         shift = {}
-        sample_banks = {}
+        k_var_banks = {}
 
         def for_scalar(shape, dtype):
             bank_for_scalar = psum.tile(shape, dtype, tag="bank_for_scalar", bufs=3)
@@ -502,77 +502,68 @@ def tile_probcrossattention_pa_kernel(
             part = log_sigmoid[VALUE, chunk][:, j : j + 2, :]
             nc.vector.tensor_tensor(out=part, in0=part, in1=bank[:], op=ALU.mult)
 
-        def add_samples(i):
-            chunk, a = divmod(i, CHUNK_TILES)
-            banks = []
-            for half in range(HALVES):
-                bank = for_vector([P, BANK], F32)
-                j = 3 * HALVES + half
-                nc.tensor.matmul(
-                    out=bank[:],
-                    lhsT=identity_bf16[:, j : j + 1].to_broadcast([P, P]),
-                    rhs=norm_rows[:],
-                    start=True,
-                    stop=False,
-                )
-                banks.append(bank)
-            for half in range(HALVES):
-                for q in range(CHUNK_TILES):
-                    nc.tensor.matmul(
-                        out=banks[half][:, q * P : (q + 1) * P],
-                        lhsT=log_sigmoid[VALUE, chunk][:, half * CHUNK_TILES + q, a * P : (a + 1) * P],
-                        rhs=identity_f32[:],
-                        is_transpose=True,
-                        start=False,
-                        stop=(q == CHUNK_TILES - 1),
-                    )
-            sample_banks[i] = banks
-
         def scale_and_add(i, half):
             columns = slice(half * BANK, (half + 1) * BANK)
-            if half == 0:
-                add_samples(i)
+            chunk, a = divmod(i, CHUNK_TILES)
+            bank = for_vector([P, BANK], F32)
+            j = 3 * HALVES + half
+            nc.tensor.matmul(
+                out=bank[:],
+                lhsT=identity_bf16[:, j : j + 1].to_broadcast([P, P]),
+                rhs=norm_rows[:],
+                start=True,
+                stop=False,
+            )
+            for q in range(CHUNK_TILES):
+                nc.tensor.matmul(
+                    out=bank[:, q * P : (q + 1) * P],
+                    lhsT=log_sigmoid[VALUE, chunk][:, half * CHUNK_TILES + q, a * P : (a + 1) * P],
+                    rhs=identity_f32[:],
+                    is_transpose=True,
+                    start=False,
+                    stop=(q == CHUNK_TILES - 1),
+                )
             nc.vector.scalar_tensor_tensor(
                 out=v_mu[:, i, columns],
                 in0=v_mu[:, i, columns],
                 scalar=inv_std[i, VALUE],
-                in1=sample_banks[i][half][:],
+                in1=bank[:],
                 op0=ALU.mult,
                 op1=ALU.add,
             )
-            if half == HALVES - 1:
-                nc.sync.dma_start(out=v_sample_rows[i * P : (i + 1) * P, :], in_=v_mu[:, i, :])
+            nc.sync.dma_start(out=v_sample_rows[i * P : (i + 1) * P, columns], in_=v_mu[:, i, columns])
 
-        def k_var_out(chunk, half, a, by_vector):
-            i = chunk * CHUNK_TILES + a
-            columns = slice(half * BANK, (half + 1) * BANK)
-            if i not in k_var:
-                k_var[i] = four_kib([P, C], F32)[:]
-            if by_vector:
-                bank = for_vector([P, BANK], F32)
-                turn_back(bank, KEY, chunk, half, a)
-                nc.vector.tensor_scalar(
-                    out=k_var[i][:, columns],
-                    in0=bank[:],
-                    scalar1=-1.0,
-                    scalar2=VAR_EPS,
-                    op0=ALU.mult,
-                    op1=ALU.add,
-                )
-            else:
+        def turn_k_var(i):
+            chunk, a = divmod(i, CHUNK_TILES)
+            banks = []
+            for half in range(HALVES):
                 bank = for_scalar([P, BANK], F32)
                 turn_back(bank, KEY, chunk, half, a)
-                nc.scalar.activation(
-                    out=k_var[i][:, columns], in_=bank[:], func=ACT.Identity, scale=-1.0, bias=var_eps[:]
-                )
+                banks.append(bank)
+            k_var_banks[i] = banks
+
+        def k_var_by_vector(i, half):
+            columns = slice(half * BANK, (half + 1) * BANK)
+            if half == 0:
+                k_var[i] = four_kib([P, C], F32)
+            bank = for_vector([P, BANK], F32)
+            chunk, a = divmod(i, CHUNK_TILES)
+            turn_back(bank, KEY, chunk, half, a)
+            nc.vector.tensor_scalar(
+                out=k_var[i][:, columns], in0=bank[:], scalar1=-1.0, scalar2=VAR_EPS, op0=ALU.mult, op1=ALU.add
+            )
             if half == HALVES - 1:
-                nc.sync.dma_start(out=k_var_rows[i * P : (i + 1) * P, :], in_=k_var[i])
+                nc.sync.dma_start(out=k_var_rows[i * P : (i + 1) * P, :], in_=k_var[i][:])
 
-        def sample(i):
-            nc.gpsimd.tensor_tensor(out=sigma[:, i, :], in0=sigma[:, i, :], in1=v_mu[:, i, :], op=ALU.add)
-
-        def store_sample(i):
-            nc.sync.dma_start(out=v_sample_rows[i * P : (i + 1) * P, :], in_=sigma[:, i, :])
+        def k_var_out(i, half):
+            columns = slice(half * BANK, (half + 1) * BANK)
+            if half == 0:
+                k_var[i] = four_kib([P, C], F32)
+            nc.scalar.activation(
+                out=k_var[i][:, columns], in_=k_var_banks[i][half][:], func=ACT.Identity, scale=-1.0, bias=var_eps[:]
+            )
+            if half == HALVES - 1:
+                nc.sync.dma_start(out=k_var_rows[i * P : (i + 1) * P, :], in_=k_var[i][:])
 
         def start_prepare(i):
             negate_context(i)
@@ -647,21 +638,21 @@ def tile_probcrossattention_pa_kernel(
         def SA(*tiles):
             return [lambda i=i, h=h: scale_and_add(i, h) for i in tiles for h in range(HALVES)]
 
-        def SD(*tiles):
-            return [lambda i=i: store_sample(i) for i in tiles]
+        def RV(i):
+            return [lambda h=h: k_var_by_vector(i, h) for h in range(HALVES)]
 
-        def S(*tiles):
-            return [lambda i=i: sample(i) for i in tiles]
+        def TK(i):
+            return [lambda: turn_k_var(i)]
 
-        def RT(by_vector, *tiles):
+        def RO(i):
+            return [lambda h=h: k_var_out(i, h) for h in range(HALVES)]
+
+        def RT(*tiles):
             return [
-                lambda i=i, h=h: k_var_out(i // CHUNK_TILES, h, i % CHUNK_TILES, by_vector)
+                lambda i=i, h=h: (turn_k_var(i) if h == 0 else None, k_var_out(i, h))
                 for i in tiles
                 for h in range(HALVES)
             ]
-
-        def RK(chunk, half, by_vector, first=0, count=CHUNK_TILES):
-            return [lambda a=a: k_var_out(chunk, half, a, by_vector) for a in range(first, first + count)]
 
         def weave(*columns):
             order = sorted(
@@ -703,22 +694,21 @@ def tile_probcrossattention_pa_kernel(
             (Q(9) + A(23, 3), M(10) + s1(4) + NM(10), GN(6), IS(8)),
             (Q(10) + A(26, 3), M(11) + F(4) + NM(11), GN(7), none),
             (Q(11) + A(29, 3), M(12) + [spread_gain_v] + NM(12), none, IS(10)),
-            (Q(12) + B(V, 0, 0), M(13) + NM(13) + M(14) + NM(14) + M(15) + NM(15), G1(8), none),
-            (Q(13) + B(V, 0, 1), T(V, 0, 0), G1(9), IS(12)),
-            (B(V, 1, 0), T(V, 0, 1), G1(10), none),
-            (B(V, 1, 1), T(V, 1, 0), none, none),
-            (B(K, 0, 0), T(V, 1, 1), G1(11), none),
-            (B(K, 0, 1), T(K, 0, 0), none, none),
-            (B(K, 1, 0), T(K, 0, 1), G1(12), none),
-            (B(K, 1, 1), T(K, 1, 0), none, none),
-            (SQ(0, 0), T(K, 1, 1), G1(13), none),
-            (SQ(0, 1) + Q(14), NT(0, 0), none, none),
-            (SQ(1, 0) + Q(15), NT(0, 1) + SA(0), none, IS(14)),
-            (SQ(1, 1) + RT(False, 0), NT(1, 0) + SA(1), G1(14), none),
-            (RT(False, 1, 2), NT(1, 1) + SA(2), G1(15), none),
-            (RT(False, 3, 4), SA(3, 4), none, none),
-            (RT(False, 5, 6), SA(5, 6), none, none),
-            (RT(False, 7), SA(7), none, none),
+            (Q(12) + B(K, 0, 0), M(13) + NM(13) + M(14) + NM(14), G1(8), none),
+            (Q(13) + B(K, 0, 1), T(K, 0, 0) + M(15) + NM(15), G1(9), none),
+            (B(V, 0, 0), T(K, 0, 1), G1(10), IS(12)),
+            (B(V, 0, 1), T(V, 0, 0), none, none),
+            (B(V, 1, 0), T(V, 0, 1) + TK(1) + RV(0), G1(11), none),
+            (B(K, 1, 0) + RO(1), T(V, 1, 0), none, none),
+            (B(K, 1, 1), T(K, 1, 0) + RV(2), G1(12), none),
+            (B(V, 1, 1), T(K, 1, 1), G1(13), none),
+            (SQ(0, 0) + Q(14), T(V, 1, 1) + TK(3), none, none),
+            (RO(3) + SQ(0, 1) + Q(15), NT(0, 0), none, IS(14)),
+            (SQ(1, 0) + RT(4), NT(0, 1) + SAH(0, 0, 1), G1(14), none),
+            (SQ(1, 1) + RT(5), NT(1, 0) + SAH(1, 0, 1), G1(15), none),
+            (RT(6), NT(1, 1) + SA(2, 3), none, none),
+            (RT(7), SA(4, 5), none, none),
+            (none, SA(6, 7), none, none),
         )
         for row in rows:
             weave(*row)

@@ -188,6 +188,19 @@ def tile_probcrossattention_pa_kernel(
             bank_for_vector = psum.tile(shape, dtype, tag="bank_for_vector", bufs=3)
             return bank_for_vector
 
+        late_banks = []
+
+        def for_vector_late(shape, dtype):
+            place = len(late_banks) % 5
+            if place == 3:
+                late_bank = psum.tile(shape, dtype, tag="gain_bank", bufs=1)
+            elif place == 4:
+                late_bank = psum.tile(shape, dtype, tag="shift_bank", bufs=1)
+            else:
+                late_bank = for_vector(shape, dtype)
+            late_banks.append(late_bank)
+            return late_bank
+
         def spread(rows_tile, first_row, target):
             width = rows_tile.shape[1]
             for h in range(C // width):
@@ -441,7 +454,7 @@ def tile_probcrossattention_pa_kernel(
 
         def linear_tail(weight, chunk, j):
             part = log_sigmoid[weight, chunk][:, j, :]
-            bank = for_vector([P, BANK], F32)
+            bank = for_vector_late([P, BANK], F32)
             channels_by_tokens(bank, weight, chunk, j)
             nc.vector.scalar_tensor_tensor(
                 out=part,
@@ -486,10 +499,7 @@ def tile_probcrossattention_pa_kernel(
             nc.gpsimd.tensor_tensor(out=sigma[:, i, :], in0=sigma[:, i, :], in1=noise[:, i, :], op=ALU.mult)
 
         def times_noise(chunk, j):
-            if j % 4:
-                bank = psum.tile([P, 2, BANK], BF16, tag="shift_bank", bufs=1)
-            else:
-                bank = psum.tile([P, 2, BANK], BF16, tag="gain_bank", bufs=1)
+            bank = for_vector_late([P, 2, BANK], BF16)
             for q in range(2):
                 for a in range(CHUNK_TILES):
                     nc.tensor.matmul(
@@ -505,7 +515,7 @@ def tile_probcrossattention_pa_kernel(
         def scale_and_add(i, half):
             columns = slice(half * BANK, (half + 1) * BANK)
             chunk, a = divmod(i, CHUNK_TILES)
-            bank = for_vector([P, BANK], F32)
+            bank = for_vector_late([P, BANK], F32)
             j = 3 * HALVES + half
             nc.tensor.matmul(
                 out=bank[:],
@@ -546,7 +556,7 @@ def tile_probcrossattention_pa_kernel(
             columns = slice(half * BANK, (half + 1) * BANK)
             if half == 0:
                 k_var[i] = four_kib([P, C], F32)
-            bank = for_vector([P, BANK], F32)
+            bank = for_vector_late([P, BANK], F32)
             chunk, a = divmod(i, CHUNK_TILES)
             turn_back(bank, KEY, chunk, half, a)
             nc.vector.tensor_scalar(
@@ -682,31 +692,30 @@ def tile_probcrossattention_pa_kernel(
         spread_bias(K)
         rows = (
             (A(0, 4), MH(0, 0) + MH(1, 0), none, none),
-            (A(4, 4), MH(0, 1) + NM(0) + MH(1, 1) + copy_k(gain_k, gain) + NM(1), none, none),
+            (A(4, 4), MH(0, 1) + MH(1, 1) + NM(0) + copy_k(gain_k, gain) + NM(1), none, none),
             (Q(0) + [lambda: start_prepare(CHUNK_TILES)] + E(4), M(2) + copy_k(shift_k, shift) + NM(2), none, none),
             (Q(1) + E(5, 6), M(3) + NM(3), none, IS(0)),
-            (Q(2) + E(7) + Q(3), M(4) + NM(4) + s1(0), none, IS(2)),
+            (Q(2) + E(7) + Q(3), M(4) + s1(0) + NM(4), none, IS(2)),
             (Q(4) + A(8, 3), M(5) + F(0) + NM(5), GN(3), none),
             (Q(5) + A(11, 3), M(6) + s1(1) + NM(6), none, IS(4)),
             (Q(6) + A(14, 3), M(7) + F(1) + [lambda: spread_bias(V)] + NM(7), GN(5), none),
             (Q(7) + A(17, 3), M(8) + s1(2) + NM(8), none, IS(6)),
-            (Q(8) + A(20, 3), M(9) + F(2) + NM(9), none, none),
+            (Q(8) + A(20, 3), M(9) + F(2) + [spread_gain_v] + NM(9), none, none),
             (Q(9) + A(23, 3), M(10) + s1(4) + NM(10), GN(6), IS(8)),
-            (Q(10) + A(26, 3), M(11) + F(4) + NM(11), GN(7), none),
-            (Q(11) + A(29, 3), M(12) + [spread_gain_v] + NM(12), none, IS(10)),
-            (Q(12) + B(K, 0, 0), M(13) + NM(13) + M(14) + NM(14), G1(8), none),
-            (Q(13) + B(K, 0, 1), T(K, 0, 0) + M(15) + NM(15), G1(9), none),
-            (B(V, 0, 0), T(K, 0, 1), G1(10), IS(12)),
-            (B(V, 0, 1), T(V, 0, 0), none, none),
+            (A(26, 6), M(11) + F(4) + NM(11), GN(7), none),
+            (B(K, 0, 0), M(12) + M(13)[:1] + NM(12) + M(13)[1:] + M(14)[:1] + NM(13) + M(14)[1:], G1(8), none),
+            (B(K, 0, 1) + Q(10), NM(14) + T(K, 0, 0)[:2] + M(15) + T(K, 0, 0)[2:] + NM(15), G1(9), none),
+            (B(V, 0, 0) + Q(11), T(K, 0, 1), G1(10), IS(10)),
+            (B(V, 0, 1) + Q(12), T(V, 0, 0), none, none),
             (B(V, 1, 0), T(V, 0, 1) + TK(1) + RV(0), G1(11), none),
             (B(K, 1, 0) + RO(1), T(V, 1, 0), none, none),
             (B(K, 1, 1), T(K, 1, 0) + RV(2), G1(12), none),
-            (B(V, 1, 1), T(K, 1, 1), G1(13), none),
-            (SQ(0, 0) + Q(14), T(V, 1, 1) + TK(3), none, none),
-            (RO(3) + SQ(0, 1) + Q(15), NT(0, 0), none, IS(14)),
-            (SQ(1, 0) + RT(4), NT(0, 1) + SAH(0, 0, 1), G1(14), none),
-            (SQ(1, 1) + RT(5), NT(1, 0) + SAH(1, 0, 1), G1(15), none),
-            (RT(6), NT(1, 1) + SA(2, 3), none, none),
+            (B(V, 1, 1), T(K, 1, 1) + RV(3), none, none),
+            (SQ(0, 0) + Q(13), T(V, 1, 1), none, none),
+            (SQ(0, 1) + Q(14), NT(0, 0), G1(13), IS(12)),
+            (SQ(1, 0) + Q(15), NT(0, 1) + SAH(0, 0, 1), G1(14), IS(14)),
+            (SQ(1, 1) + RT(4), NT(1, 0) + SAH(1, 0, 1), G1(15), none),
+            (RT(5, 6), NT(1, 1) + SA(2, 3), none, none),
             (RT(7), SA(4, 5), none, none),
             (none, SA(6, 7), none, none),
         )

@@ -347,7 +347,7 @@ def tile_probcrossattention_pa_kernel(
         def squares(i, weight):
             pair, column = divmod(i, 2)
             if column == 0:
-                pair_sums = work.tile([P, 2], F32, tag="pair_sums", bufs=4)
+                pair_sums = work.tile([P, 2], F32, tag="pair_sums", bufs=8)
                 square_sum[pair, weight] = pair_sums
             unread = work.tile([P, C], BF16, tag="unread", bufs=1)
             nc.scalar.activation(
@@ -497,6 +497,10 @@ def tile_probcrossattention_pa_kernel(
 
         def scale_noise(i):
             nc.gpsimd.tensor_tensor(out=sigma[:, i, :], in0=sigma[:, i, :], in1=noise[:, i, :], op=ALU.mult)
+
+        def keep_warm():
+            bank = for_vector_late([P, BANK], F32)
+            nc.tensor.matmul(out=bank[:], lhsT=zeros[:, :P], rhs=zeros[:], start=True, stop=True)
 
         def times_noise(chunk, j):
             bank = for_vector_late([P, 2, BANK], BF16)
@@ -712,10 +716,10 @@ def tile_probcrossattention_pa_kernel(
             (B(K, 1, 1), T(K, 1, 0) + RV(2), G1(12), none),
             (B(V, 1, 1), T(K, 1, 1) + RV(3), none, none),
             (SQ(0, 0) + Q(13), T(V, 1, 1), none, none),
-            (SQ(0, 1) + Q(14), NT(0, 0), G1(13), IS(12)),
+            (SQ(0, 1) + Q(14), NT(0, 0) + RV(4), G1(13), IS(12)),
             (SQ(1, 0) + Q(15), NT(0, 1) + SAH(0, 0, 1), G1(14), IS(14)),
-            (SQ(1, 1) + RT(4), NT(1, 0) + SAH(1, 0, 1), G1(15), none),
-            (RT(5, 6), NT(1, 1) + SA(2, 3), none, none),
+            (SQ(1, 1) + RT(5), NT(1, 0) + SAH(1, 0, 1), G1(15), none),
+            (RT(6), NT(1, 1) + SA(2, 3), none, none),
             (RT(7), SA(4, 5), none, none),
             (none, SA(6, 7), none, none),
         )

@@ -715,12 +715,12 @@ def tile_probcrossattention_pa_kernel(
             (B(K, 1, 0) + RO(1), T(V, 1, 0), none, none),
             (B(K, 1, 1), T(K, 1, 0) + RV(2), G1(12), none),
             (B(V, 1, 1), T(K, 1, 1) + RV(3), none, none),
-            (SQ(0, 0) + Q(13), T(V, 1, 1), none, none),
-            (SQ(0, 1) + Q(14), NT(0, 0) + RV(4), G1(13), IS(12)),
+            (SQ(0, 0) + Q(13), T(V, 1, 1) + RV(4), none, none),
+            (SQ(0, 1) + Q(14), NT(0, 0) + RV(5), G1(13), IS(12)),
             (SQ(1, 0) + Q(15), NT(0, 1) + SAH(0, 0, 1), G1(14), IS(14)),
-            (SQ(1, 1) + RT(5), NT(1, 0) + SAH(1, 0, 1), G1(15), none),
-            (RT(6), NT(1, 1) + SA(2, 3), none, none),
-            (RT(7), SA(4, 5), none, none),
+            (SQ(1, 1) + RT(6), NT(1, 0) + SAH(1, 0, 1), G1(15), none),
+            (RT(7), SA(2) + NT(1, 1) + SA(3), none, none),
+            (none, SA(4, 5), none, none),
             (none, SA(6, 7), none, none),
         )
         for row in rows:

@@ -155,10 +155,10 @@ def tile_probcrossattention_pa_kernel(
             load_rows(vector, 0, HALVES, BANK, norm_rows, HALVES * j)
         load_weight_scales(VALUE)
         load_weight_half(VALUE, VARIANCE)
+        load_weight_half(VALUE, VARIANCE + BANK)
         load_weight_scales(KEY)
         load_weight_half(KEY, MEAN)
         load_weight_half(KEY, MEAN + BANK)
-        load_weight_half(VALUE, VARIANCE + BANK)
         for i in range(CHUNK_TILES, TILES):
             load_context(i)
         load_weight_section(KEY, VARIANCE)
@@ -695,18 +695,18 @@ def tile_probcrossattention_pa_kernel(
         prepare_step(3, CHUNK_TILES)
         spread_bias(K)
         rows = (
-            (A(0, 4), MH(0, 0) + MH(1, 0), none, none),
-            (A(4, 4), MH(0, 1) + MH(1, 1) + NM(0) + copy_k(gain_k, gain) + NM(1), none, none),
-            (Q(0) + [lambda: start_prepare(CHUNK_TILES)] + E(4), M(2) + copy_k(shift_k, shift) + NM(2), none, none),
+            (A(0, 8), copy_k(gain_k, gain) + copy_k(shift_k, shift), none, none),
+            (none, MH(0, 0) + MH(0, 1) + MH(1, 0) + NM(0) + MH(1, 1) + NM(1), none, none),
+            (Q(0) + [lambda: start_prepare(CHUNK_TILES)] + E(4), M(2) + NM(2), none, none),
             (Q(1) + E(5, 6), M(3) + NM(3), none, IS(0)),
-            (Q(2) + E(7) + Q(3), M(4) + s1(0) + NM(4), none, IS(2)),
-            (Q(4) + A(8, 3), M(5) + F(0) + NM(5), GN(3), none),
-            (Q(5) + A(11, 3), M(6) + s1(1) + NM(6), none, IS(4)),
-            (Q(6) + A(14, 3), M(7) + F(1) + [lambda: spread_bias(V)] + NM(7), GN(5), none),
-            (Q(7) + A(17, 3), M(8) + s1(2) + NM(8), none, IS(6)),
-            (Q(8) + A(20, 3), M(9) + F(2) + [spread_gain_v] + NM(9), none, none),
-            (Q(9) + A(23, 3), M(10) + s1(4) + NM(10), GN(6), IS(8)),
-            (A(26, 6), M(11) + F(4) + NM(11), GN(7), none),
+            (Q(2) + E(7) + Q(3), M(4) + NM(4), none, IS(2)),
+            (Q(4) + A(8, 3), M(5) + s1(0) + NM(5), GN(3), none),
+            (Q(5) + A(11, 3), M(6) + F(0) + NM(6), none, IS(4)),
+            (Q(6) + A(14, 3), M(7) + s1(1) + [lambda: spread_bias(V)] + NM(7), GN(5), none),
+            (Q(7) + A(17, 3), M(8) + F(1) + NM(8), none, IS(6)),
+            (Q(8) + A(20, 3), M(9) + s1(2) + [spread_gain_v] + NM(9), none, none),
+            (Q(9) + A(23, 3), M(10) + F(2) + NM(10), GN(6), IS(8)),
+            (A(26, 6), M(11) + s1(4) + NM(11) + F(4), GN(7), none),
             (B(K, 0, 0), M(12) + M(13)[:1] + NM(12) + M(13)[1:] + M(14)[:1] + NM(13) + M(14)[1:], G1(8), none),
             (B(K, 0, 1) + Q(10), NM(14) + T(K, 0, 0)[:2] + M(15) + T(K, 0, 0)[2:] + NM(15), G1(9), none),
             (B(V, 0, 0) + Q(11), T(K, 0, 1), G1(10), IS(10)),

from contextlib import ExitStack

import concourse.mybir as mybir
from concourse.masks import make_identity

F32 = mybir.dt.float32
BF16 = mybir.dt.bfloat16
I32 = mybir.dt.int32
U32 = mybir.dt.uint32
U8 = mybir.dt.uint8
FP8X4 = mybir.dt.float8_e4m3fn_x4
ALU = mybir.AluOpType
ACT = mybir.ActivationFunctionType

P = 128
PACK = 4
K_PASS = P * PACK
TOKENS = 1024
C = 1024
PASSES = C // K_PASS
TILES = TOKENS // P
BANK = 512
HALVES = C // BANK
CHUNKS = TOKENS // BANK
CHUNK_TILES = BANK // P
CHANNEL_TILES = C // P
VAR_EPS = 1e-6
LN_EPS = 1e-5
RUN = 2
LN_FLOOR = 2.0 ** -60

FLOPS = 2 * TOKENS * C * 4 * C

KEY = 0
VALUE = 1
MEAN = 0
VARIANCE = C


def tile_probcrossattention_pa_kernel(
    tc,
    context,
    eps_noise,
    Wk_words,
    Wk_scales,
    bk,
    Wv_words,
    Wv_scales,
    bv,
    ln_k_g,
    ln_k_b,
    ln_v_g,
    ln_v_b,
    out_0,
    out_1,
    out_2,
):
    nc = tc.nc
    context_rows = context.flatten_outer_dims().rearrange("(i p) c -> p i c", p=P)
    noise_rows = eps_noise.flatten_outer_dims().rearrange("(i p) c -> p i c", p=P)
    k_mu_rows = out_0.flatten_outer_dims()
    k_var_rows = out_1.flatten_outer_dims()
    v_sample_rows = out_2.flatten_outer_dims()
    words_in = (Wk_words, Wv_words)
    scales_in = (Wk_scales, Wv_scales)
    bias_in = (bk, bv)

    with ExitStack() as stack:
        keep = stack.enter_context(tc.tile_pool(name="keep", bufs=1))
        work = stack.enter_context(tc.tile_pool(name="work", bufs=2))
        psum = stack.enter_context(tc.psum_pool(name="psum", bufs=1))
        stack.enter_context(tc.manual_schedule())

        noise = keep.tile([P, TILES, C], BF16)
        context_codes = keep.tile([P, PASSES, TOKENS], U32, align_bytes=64)
        context_scales = keep.tile([P, PASSES, TOKENS], U8, align_bytes=64)
        weight_codes = keep.tile([P, 2, PASSES, 2 * C], U32, align_bytes=64)
        scales_k = keep.tile([P, 2 * C], U8, align_bytes=64)
        scales_v = keep.tile([P, 2 * C], U8, align_bytes=64)
        weight_scales = (scales_k, scales_v)
        bias_mean = keep.tile([P, 2, C], BF16)
        gain_k = keep.tile([P, C], BF16)
        shift_k = keep.tile([P, C], BF16)
        gain_v = keep.tile([P, C], BF16)
        bias_rows = keep.tile([P, P], BF16)
        norm_rows = keep.tile([P, BANK], BF16)
        neg_var_bias = keep.tile([P, 4 * CHANNEL_TILES], F32)
        identity_f32 = keep.tile([P, P], F32)
        identity_bf16 = keep.tile([P, P], BF16)
        var_eps = keep.tile([P, 1], F32)
        ln_floor = keep.tile([P, 1], F32)
        zeros = keep.tile([P, BANK], BF16)
        minus_half = keep.tile([P, 2], F32)
        warm = keep.tile([P, 1], F32)
        v_mu = keep.tile([P, TILES, C], F32)
        sigma = None

        nc.vector.memset(zeros[:].bitcast(I32), 0)
        nc.vector.memset(bias_rows[:].bitcast(I32), 0)
        nc.vector.memset(scales_v[:].bitcast(I32), 0)
        nc.vector.memset(scales_k[:].bitcast(I32), 0)
        nc.vector.memset(norm_rows[:].bitcast(I32), 0)
        nc.vector.memset(var_eps[:], VAR_EPS)
        nc.vector.memset(ln_floor[:], LN_FLOOR)
        nc.vector.memset(minus_half[:], -0.5)
        make_identity(nc, identity_f32[:])
        make_identity(nc, identity_bf16[:])
        nc.scalar.activation(out=warm[:], in_=var_eps[:], func=ACT.Sigmoid)

        context_raw = {}

        def four_kib(shape, dtype):
            four_kib_tile = work.tile(shape, dtype, tag="four_kib_tile", bufs=TILES)
            return four_kib_tile

        def load_context(i):
            if i % 2 == 0:
                context_raw[i // 2] = four_kib([P, 2, C], BF16)
            nc.sync.dma_start(out=context_raw[i // 2][:, i % 2, :], in_=context_rows[:, i, :])

        def load_weight_half(weight, first_column):
            columns = slice(first_column, first_column + BANK)
            for g in range(PASSES):
                packed = words_in[weight][g].rearrange("p n t -> p (n t)")
                nc.sync.dma_start(
                    out=weight_codes[:, weight, g, columns].bitcast(I32),
                    in_=packed[:, PACK * first_column : PACK * (first_column + BANK)].bitcast(I32),
                )

        def load_weight_section(weight, first_column):
            load_weight_half(weight, first_column)
            load_weight_half(weight, first_column + BANK)

        def load_weight_scales(weight):
            for quadrant in range(4):
                first_row = 32 * quadrant
                nc.sync.dma_start(
                    out=weight_scales[weight][first_row : first_row + 8, :].bitcast(I32),
                    in_=scales_in[weight][:, 4 * quadrant : 4 * quadrant + 4, :].bitcast(I32),
                )

        def load_rows(vector, first, count, width, rows_tile, first_row):
            rows = vector[first : first + count * width].rearrange("(j n) -> j n", n=width)
            nc.sync.dma_start(out=rows_tile[first_row : first_row + count, :], in_=rows)

        norm_in = (ln_k_g, ln_k_b, ln_v_g, ln_v_b)
        def load_bias(weight):
            load_rows(bias_in[weight], MEAN, 2 * CHANNEL_TILES, P, bias_rows, 2 * CHANNEL_TILES * weight)

        for i in range(CHUNK_TILES):
            load_context(i)
        load_bias(KEY)
        load_bias(VALUE)
        for j, vector in enumerate(norm_in):
            load_rows(vector, 0, HALVES, BANK, norm_rows, HALVES * j)
        load_weight_scales(VALUE)
        load_weight_half(VALUE, VARIANCE)
        load_weight_half(VALUE, VARIANCE + BANK)
        load_weight_scales(KEY)
        load_weight_half(KEY, MEAN)
        load_weight_half(KEY, MEAN + BANK)
        for i in range(CHUNK_TILES, TILES):
            load_context(i)
        load_weight_section(KEY, VARIANCE)
        load_weight_section(VALUE, MEAN)
        for i in range(TILES):
            nc.sync.dma_start(out=noise[:, i, :], in_=noise_rows[:, i, :])

        negated = {}
        turned = {}
        grouped = {}
        k_mu = {}
        minus_mean = {}
        inv_std = {}
        square_sum = {}
        half_sums = {}
        log_sigmoid = {}
        k_var = {}
        gain = {}
        shift = {}
        k_var_banks = {}

        def for_scalar(shape, dtype):
            bank_for_scalar = psum.tile(shape, dtype, tag="bank_for_scalar", bufs=3)
            return bank_for_scalar

        def for_vector(shape, dtype):
            bank_for_vector = psum.tile(shape, dtype, tag="bank_for_vector", bufs=3)
            return bank_for_vector

        late_banks = []

        def for_vector_late(shape, dtype):
            place = len(late_banks) % 5
            if place == 3:
                late_bank = psum.tile(shape, dtype, tag="gain_bank", bufs=1)
            elif place == 4:
                late_bank = psum.tile(shape, dtype, tag="shift_bank", bufs=1)
            else:
                late_bank = for_vector(shape, dtype)
            late_banks.append(late_bank)
            return late_bank

        def spread(rows_tile, first_row, target):
            width = rows_tile.shape[1]
            for h in range(C // width):
                j = first_row + h
                nc.tensor.matmul(
                    out=target[:, h * width : (h + 1) * width],
                    lhsT=identity_bf16[:, j : j + 1].to_broadcast([P, P]),
                    rhs=rows_tile[:],
                    start=True,
                    stop=True,
                )

        def spread_by_vector(rows_tile, first_row, target):
            bank = for_vector([P, C], BF16)
            spread(rows_tile, first_row, bank)
            nc.vector.tensor_copy(out=target, in_=bank[:])

        def spread_by_scalar(rows_tile, first_row, target):
            bank = for_scalar([P, C], BF16)
            spread(rows_tile, first_row, bank)
            nc.scalar.copy(out=target, in_=bank[:])

        def spread_bias(weight):
            spread_by_vector(bias_rows, 2 * CHANNEL_TILES * weight, bias_mean[:, weight, :])

        def turn_var_bias():
            bank = for_vector([P, C], BF16)
            nc.tensor.transpose(bank[:, :P], bias_rows[:], identity_bf16[:])
            nc.vector.tensor_scalar_mul(
                out=neg_var_bias[:], in0=bank[:, : 4 * CHANNEL_TILES], scalar1=-1.0
            )

        def negate_context(i):
            minus = work.tile([P, C], BF16, tag="minus", bufs=3)
            if i < CHUNK_TILES:
                nc.vector.tensor_scalar_mul(out=minus[:], in0=context_raw[i // 2][:, i % 2, :], scalar1=-1.0)
            else:
                nc.gpsimd.tensor_scalar(
                    out=minus[:],
                    in0=context_raw[i // 2][:, i % 2, :],
                    scalar1=-1.0,
                    scalar2=0.0,
                    op0=ALU.mult,
                    op1=ALU.add,
                )
            negated[i] = minus

        def turn_context(i):
            words = negated[i][:].bitcast(F32)
            bank = for_scalar([P, PASSES * 2, P], F32)
            for g in range(PASSES):
                for u in range(2):
                    nc.tensor.transpose(
                        bank[:, 2 * g + u, :],
                        words[:, 256 * g + u : 256 * (g + 1) : 2],
                        identity_f32[:],
                    )
            turned[i] = bank

        def group_context(i):
            side_by_side = work.tile([P, PASSES * P * PACK], BF16, tag="side_by_side", bufs=3, align_bytes=64)
            nc.scalar.copy(
                out=side_by_side[:].bitcast(F32).rearrange("p (g r u) -> p g r u", g=PASSES, u=2),
                in_=turned[i][:].rearrange("p (g u) r -> p g r u", u=2),
            )
            grouped[i] = side_by_side

        def quantise_context(i):
            tokens = slice(i * P, (i + 1) * P)
            for g in range(PASSES):
                nc.vector.quantize_mx(
                    out=context_codes[:, g, tokens].bitcast(FP8X4),
                    scales=context_scales[:, g, tokens],
                    in_=grouped[i][:, g * K_PASS : (g + 1) * K_PASS],
                )

        def plane(weight, g, columns):
            return weight_scales[weight][4 * g : P, columns]

        def tokens_by_channels(bank, i, weight, first_column):
            tokens = slice(i * P, (i + 1) * P)
            columns = slice(first_column, first_column + BANK)
            for g in range(PASSES):
                nc.tensor.matmul_mx(
                    out=bank[:],
                    lhsT=context_codes[:, g, tokens].bitcast(FP8X4),
                    lhsT_scale=context_scales[:, g, tokens],
                    rhs=weight_codes[:, weight, g, columns].bitcast(FP8X4),
                    rhs_scale=plane(weight, g, columns),
                    start=(g == 0),
                    stop=(g == PASSES - 1),
                )

        def channels_by_tokens(bank, weight, chunk, j):
            tokens = slice(chunk * BANK, (chunk + 1) * BANK)
            columns = slice(VARIANCE + j * P, VARIANCE + (j + 1) * P)
            for g in range(PASSES):
                nc.tensor.matmul_mx(
                    out=bank[:],
                    lhsT=weight_codes[:, weight, g, columns].bitcast(FP8X4),
                    lhsT_scale=plane(weight, g, columns),
                    rhs=context_codes[:, g, tokens].bitcast(FP8X4),
                    rhs_scale=context_scales[:, g, tokens],
                    start=(g == 0),
                    stop=(g == PASSES - 1),
                )

        def mean_input(i, weight):
            if weight == KEY:
                if i not in k_mu:
                    k_mu[i] = four_kib([P, C], F32)
                return k_mu[i][:]
            return v_mu[:, i, :]

        def project_mean(i, weight, h):
            x = mean_input(i, weight)
            if h == 0:
                sums = work.tile([P, HALVES], F32, tag="sums", bufs=4)
                half_sums[i, weight] = sums
            bank = for_vector([P, BANK], F32)
            tokens_by_channels(bank, i, weight, MEAN + h * BANK)
            nc.vector.scalar_tensor_tensor(
                out=x[:, h * BANK : (h + 1) * BANK],
                in0=bank[:],
                scalar=-1.0,
                in1=bias_mean[:, weight, h * BANK : (h + 1) * BANK],
                op0=ALU.mult,
                op1=ALU.add,
                accum_out=half_sums[i, weight][:, h : h + 1],
            )

        def minus_mean_of(i, weight):
            neg_mean = work.tile([P, 1], F32, tag="neg_mean", bufs=16)
            nc.vector.tensor_scalar(
                out=neg_mean[:],
                in0=half_sums[i, weight][:, 0:1],
                scalar1=half_sums[i, weight][:, 1:2],
                scalar2=-1.0 / C,
                op0=ALU.add,
                op1=ALU.mult,
            )
            minus_mean[i, weight] = neg_mean

        def squares(i, weight):
            pair, column = divmod(i, 2)
            if column == 0:
                pair_sums = work.tile([P, 2], F32, tag="pair_sums", bufs=8)
                square_sum[pair, weight] = pair_sums
            unread = work.tile([P, C], BF16, tag="unread", bufs=1)
            nc.scalar.activation(
                out=unread[:],
                in_=mean_input(i, weight),
                func=ACT.Square,
                bias=minus_mean[i, weight][:],
                accum_out=square_sum[pair, weight][:, column : column + 1],
            )

        def inverse_std(pair, weight):
            variance = work.tile([P, 2], F32, tag="variance", bufs=4)
            nc.gpsimd.tensor_scalar(
                out=variance[:],
                in0=square_sum[pair, weight][:],
                scalar1=1.0 / C,
                scalar2=LN_EPS,
                op0=ALU.mult,
                op1=ALU.add,
            )
            rstd = work.tile([P, 2], F32, tag="rstd", bufs=8)
            nc.gpsimd.tensor_tensor(out=rstd[:], in0=variance[:], in1=minus_half[:], op=ALU.pow)
            for column in range(2):
                inv_std[2 * pair + column, weight] = rstd[:, column : column + 1]

        def centre_and_gain(i, weight):
            x = mean_input(i, weight)
            nc.vector.scalar_tensor_tensor(
                out=x,
                in0=x,
                scalar=minus_mean[i, weight][:],
                in1=gain[weight][:],
                op0=ALU.add,
                op1=ALU.mult,
            )

        def spread_gain_v():
            bank = for_vector([P, C], BF16)
            spread(norm_rows, 2 * HALVES, bank)
            nc.vector.tensor_copy(out=gain_v[:], in_=bank[:])

        def spread_norm(weight):
            gain_bank = psum.tile([P, C], BF16, tag="gain_bank", bufs=1)
            shift_bank = psum.tile([P, C], BF16, tag="shift_bank", bufs=1)
            spread(norm_rows, 2 * HALVES * weight, gain_bank)
            spread(norm_rows, 2 * HALVES * weight + HALVES, shift_bank)
            gain[weight] = gain_bank
            shift[weight] = shift_bank

        def centre_and_gain_on_gpsimd(i):
            x = v_mu[:, i, :]
            nc.gpsimd.tensor_scalar(
                out=x, in0=x, scalar1=minus_mean[i, VALUE][:], scalar2=1.0, op0=ALU.add, op1=ALU.mult
            )
            nc.gpsimd.tensor_tensor(out=x, in0=x, in1=gain_v[:], op=ALU.mult)

        def normalise_on_gpsimd(i):
            x = k_mu[i][:]
            nc.gpsimd.tensor_scalar(
                out=x,
                in0=x,
                scalar1=minus_mean[i, KEY][:],
                scalar2=inv_std[i, KEY],
                op0=ALU.add,
                op1=ALU.mult,
            )
            nc.gpsimd.tensor_tensor(out=x, in0=x, in1=gain_k[:], op=ALU.mult)
            nc.gpsimd.tensor_tensor(out=x, in0=x, in1=shift_k[:], op=ALU.add)
            nc.sync.dma_start(out=k_mu_rows[i * P : (i + 1) * P, :], in_=x)

        def scale_and_shift(i, weight):
            x = mean_input(i, weight)
            nc.vector.scalar_tensor_tensor(
                out=x,
                in0=x,
                scalar=inv_std[i, weight],
                in1=shift[weight][:],
                op0=ALU.mult,
                op1=ALU.add,
            )
            if weight == KEY:
                nc.sync.dma_start(out=k_mu_rows[i * P : (i + 1) * P, :], in_=x)

        def bias_column(weight, j):
            column = 2 * CHANNEL_TILES * weight + CHANNEL_TILES + j
            return neg_var_bias[:, column : column + 1]

        def sigmoid(weight, chunk, j):
            if j == 0:
                logs = work.tile([P, CHANNEL_TILES, BANK], F32, tag="logs", bufs=4)
                log_sigmoid[weight, chunk] = logs
            bank = for_scalar([P, BANK], F32)
            channels_by_tokens(bank, weight, chunk, j)
            nc.scalar.activation(
                out=log_sigmoid[weight, chunk][:, j, :],
                in_=bank[:],
                func=ACT.Sigmoid,
                bias=bias_column(weight, j),
            )

        def logarithm(weight, chunk, half):
            part = log_sigmoid[weight, chunk][:, half * CHUNK_TILES : (half + 1) * CHUNK_TILES, :]
            nc.scalar.activation(out=part, in_=part, func=ACT.Ln, bias=ln_floor[:])

        def linear_tail(weight, chunk, j):
            part = log_sigmoid[weight, chunk][:, j, :]
            bank = for_vector_late([P, BANK], F32)
            channels_by_tokens(bank, weight, chunk, j)
            nc.vector.scalar_tensor_tensor(
                out=part,
                in0=bank[:],
                scalar=bias_column(weight, j),
                in1=part,
                op0=ALU.add,
                op1=ALU.min,
            )

        def turn_back(bank, weight, chunk, half, a):
            for q in range(CHUNK_TILES):
                nc.tensor.transpose(
                    bank[:, q * P : (q + 1) * P],
                    log_sigmoid[weight, chunk][:, half * CHUNK_TILES + q, a * P : (a + 1) * P],
                    identity_f32[:],
                )

        def sigma_out(chunk, half, a):
            i = chunk * CHUNK_TILES + a
            columns = slice(half * BANK, (half + 1) * BANK)
            bank = for_scalar([P, BANK], F32)
            turn_back(bank, VALUE, chunk, half, a)
            nc.scalar.activation(
                out=sigma[:, i, columns], in_=bank[:], func=ACT.Sqrt, scale=-1.0, bias=var_eps[:]
            )

        def sigma_in_place(chunk, half, first=0, count=CHUNK_TILES):
            part = log_sigmoid[VALUE, chunk][
                :, half * CHUNK_TILES : (half + 1) * CHUNK_TILES, first * P : (first + count) * P
            ]
            nc.scalar.activation(out=part, in_=part, func=ACT.Sqrt, scale=-1.0, bias=var_eps[:])

        def noise_from_bank(chunk, half, a):
            i = chunk * CHUNK_TILES + a
            columns = slice(half * BANK, (half + 1) * BANK)
            bank = for_vector([P, BANK], F32)
            turn_back(bank, VALUE, chunk, half, a)
            nc.vector.tensor_tensor(out=sigma[:, i, columns], in0=bank[:], in1=noise[:, i, columns], op=ALU.mult)

        def scale_noise(i):
            nc.gpsimd.tensor_tensor(out=sigma[:, i, :], in0=sigma[:, i, :], in1=noise[:, i, :], op=ALU.mult)

        def keep_warm():
            bank = for_vector_late([P, BANK], F32)
            nc.tensor.matmul(out=bank[:], lhsT=zeros[:, :P], rhs=zeros[:], start=True, stop=True)

        def times_noise(chunk, j):
            bank = for_vector_late([P, 2, BANK], BF16)
            for q in range(2):
                for a in range(CHUNK_TILES):
                    nc.tensor.matmul(
                        out=bank[:, q, a * P : (a + 1) * P],
                        lhsT=noise[:, chunk * CHUNK_TILES + a, (j + q) * P : (j + q + 1) * P],
                        rhs=identity_bf16[:],
                        start=True,
                        stop=True,
                    )
            part = log_sigmoid[VALUE, chunk][:, j : j + 2, :]
            nc.vector.tensor_tensor(out=part, in0=part, in1=bank[:], op=ALU.mult)

        def scale_and_add(i, half):
            columns = slice(half * BANK, (half + 1) * BANK)
            chunk, a = divmod(i, CHUNK_TILES)
            bank = for_vector_late([P, BANK], F32)
            j = 3 * HALVES + half
            nc.tensor.matmul(
                out=bank[:],
                lhsT=identity_bf16[:, j : j + 1].to_broadcast([P, P]),
                rhs=norm_rows[:],
                start=True,
                stop=False,
            )
            for q in range(CHUNK_TILES):
                nc.tensor.matmul(
                    out=bank[:, q * P : (q + 1) * P],
                    lhsT=log_sigmoid[VALUE, chunk][:, half * CHUNK_TILES + q, a * P : (a + 1) * P],
                    rhs=identity_f32[:],
                    is_transpose=True,
                    start=False,
                    stop=(q == CHUNK_TILES - 1),
                )
            nc.vector.scalar_tensor_tensor(
                out=v_mu[:, i, columns],
                in0=v_mu[:, i, columns],
                scalar=inv_std[i, VALUE],
                in1=bank[:],
                op0=ALU.mult,
                op1=ALU.add,
            )
            nc.sync.dma_start(out=v_sample_rows[i * P : (i + 1) * P, columns], in_=v_mu[:, i, columns])

        def turn_k_var(i):
            chunk, a = divmod(i, CHUNK_TILES)
            banks = []
            for half in range(HALVES):
                bank = for_scalar([P, BANK], F32)
                turn_back(bank, KEY, chunk, half, a)
                banks.append(bank)
            k_var_banks[i] = banks

        def k_var_by_vector(i, half):
            columns = slice(half * BANK, (half + 1) * BANK)
            if half == 0:
                k_var[i] = four_kib([P, C], F32)
            bank = for_vector_late([P, BANK], F32)
            chunk, a = divmod(i, CHUNK_TILES)
            turn_back(bank, KEY, chunk, half, a)
            nc.vector.tensor_scalar(
                out=k_var[i][:, columns], in0=bank[:], scalar1=-1.0, scalar2=VAR_EPS, op0=ALU.mult, op1=ALU.add
            )
            if half == HALVES - 1:
                nc.sync.dma_start(out=k_var_rows[i * P : (i + 1) * P, :], in_=k_var[i][:])

        def k_var_out(i, half):
            columns = slice(half * BANK, (half + 1) * BANK)
            if half == 0:
                k_var[i] = four_kib([P, C], F32)
            nc.scalar.activation(
                out=k_var[i][:, columns], in_=k_var_banks[i][half][:], func=ACT.Identity, scale=-1.0, bias=var_eps[:]
            )
            if half == HALVES - 1:
                nc.sync.dma_start(out=k_var_rows[i * P : (i + 1) * P, :], in_=k_var[i][:])

        def start_prepare(i):
            negate_context(i)
            turn_context(i)
            negate_context(i + 1)

        def prepare_step(i, end):
            group_context(i)
            if i + 1 < end:
                turn_context(i + 1)
            if i + 2 < end:
                negate_context(i + 2)
            quantise_context(i)

        K, V = KEY, VALUE

        items = [(i, K) for i in range(TILES)] + [(i, V) for i in range(TILES)]
        none = []

        def A(first, count):
            banks = [(w, chunk, j) for w in (V, K) for chunk in range(CHUNKS) for j in range(CHANNEL_TILES)]
            return [lambda b=b: sigmoid(*b) for b in banks[first : first + count]]

        def B(weight, chunk, half):
            return [lambda: logarithm(weight, chunk, half)]

        def Q(*ms):
            return [lambda m=m: squares(*items[m]) for m in ms]

        def E(*tiles):
            return [lambda i=i: prepare_step(i, TILES) for i in tiles]

        def M(*ms):
            return [lambda m=m, h=h: project_mean(items[m][0], items[m][1], h) for m in ms for h in range(HALVES)]

        def NM(m):
            return [lambda: minus_mean_of(*items[m])]

        def IS(*ms):
            return [lambda m=m: inverse_std(items[m][0] // 2, items[m][1]) for m in ms]

        def s1(*ms):
            return [lambda m=m: centre_and_gain(*items[m]) for m in ms]

        def G1(*ms):
            return [lambda m=m: centre_and_gain_on_gpsimd(m - TILES) for m in ms]

        def MH(m, h):
            return [lambda: project_mean(items[m][0], items[m][1], h)]

        def GN(*ms):
            return [lambda m=m: normalise_on_gpsimd(m) for m in ms]

        def F(*ms):
            return [lambda m=m: scale_and_shift(*items[m]) for m in ms]

        def T(weight, chunk, half, first=0, count=CHUNK_TILES):
            return [lambda j=j: linear_tail(weight, chunk, half * CHUNK_TILES + j) for j in range(first, first + count)]

        def SQ(chunk, half):
            return [lambda: sigma_in_place(chunk, half)]

        def NB(chunk, half, first=0, count=CHUNK_TILES):
            return [lambda a=a: noise_from_bank(chunk, half, a) for a in range(first, first + count)]

        def NT(chunk, half):
            return [lambda j=j: times_noise(chunk, half * CHUNK_TILES + j) for j in range(0, CHUNK_TILES, 2)]

        def SAH(h, *tiles):
            return [lambda i=i: scale_and_add(i, h) for i in tiles]

        def SA(*tiles):
            return [lambda i=i, h=h: scale_and_add(i, h) for i in tiles for h in range(HALVES)]

        def RV(i):
            return [lambda h=h: k_var_by_vector(i, h) for h in range(HALVES)]

        def TK(i):
            return [lambda: turn_k_var(i)]

        def RO(i):
            return [lambda h=h: k_var_out(i, h) for h in range(HALVES)]

        def RT(*tiles):
            return [
                lambda i=i, h=h: (turn_k_var(i) if h == 0 else None, k_var_out(i, h))
                for i in tiles
                for h in range(HALVES)
            ]

        def weave(*columns):
            order = sorted(
                (((j // RUN + 0.5) / ((len(column) + RUN - 1) // RUN), j / len(column), 1.0)[max(c - 1, 0)], -c, j)
                for c, column in enumerate(columns)
                for j in range(len(column))
            )
            for place, c, j in order:
                columns[-c][j]()

        def copy_k(target, banks, weight=K):
            return [lambda: nc.vector.tensor_copy(out=target[:], in_=banks[weight][:])]

        def by_scalar(rows_tile, first_row, target):
            return [lambda: spread_by_scalar(rows_tile, first_row, target)]

        warm_bank = psum.tile([P, BANK], F32, tag="bank_for_vector", bufs=3)
        for turn in range(4):
            nc.tensor.matmul(out=warm_bank[:], lhsT=zeros[:, :P], rhs=zeros[:], start=True, stop=True)
        start_prepare(0)
        prepare_step(0, CHUNK_TILES)
        turn_var_bias()
        prepare_step(1, CHUNK_TILES)
        prepare_step(2, CHUNK_TILES)
        spread_norm(K)
        prepare_step(3, CHUNK_TILES)
        spread_bias(K)
        rows = (
            (A(0, 8), copy_k(gain_k, gain) + copy_k(shift_k, shift), none, none),
            (none, MH(0, 0) + MH(0, 1) + MH(1, 0) + NM(0) + MH(1, 1) + NM(1), none, none),
            (Q(0) + [lambda: start_prepare(CHUNK_TILES)] + E(4), M(2) + NM(2), none, none),
            (Q(1) + E(5, 6), M(3) + NM(3), none, IS(0)),
            (Q(2) + E(7) + Q(3), M(4) + NM(4), none, IS(2)),
            (Q(4) + A(8, 3), M(5) + s1(0) + NM(5), GN(3), none),
            (Q(5) + A(11, 3), M(6) + F(0) + NM(6), none, IS(4)),
            (Q(6) + A(14, 3), M(7) + s1(1) + [lambda: spread_bias(V)] + NM(7), GN(5), none),
            (Q(7) + A(17, 3), M(8) + F(1) + NM(8), none, IS(6)),
            (Q(8) + A(20, 3), M(9) + s1(2) + [spread_gain_v] + NM(9), none, none),
            (Q(9) + A(23, 3), M(10) + F(2) + NM(10), GN(6), IS(8)),
            (A(26, 6), M(11) + s1(4) + NM(11) + F(4), GN(7), none),
            (B(K, 0, 0), M(12) + M(13)[:1] + NM(12) + M(13)[1:] + M(14)[:1] + NM(13) + M(14)[1:], G1(8), none),
            (B(K, 0, 1) + Q(10), NM(14) + T(K, 0, 0)[:2] + M(15) + T(K, 0, 0)[2:] + NM(15), G1(9), none),
            (B(V, 0, 0) + Q(11), T(K, 0, 1), G1(10), IS(10)),
            (B(V, 0, 1) + Q(12), T(V, 0, 0), none, none),
            (B(V, 1, 0), T(V, 0, 1) + TK(1) + RV(0), G1(11), none),
            (B(K, 1, 0) + RO(1), T(V, 1, 0), none, none),
            (B(K, 1, 1), T(K, 1, 0) + RV(2), G1(12), none),
            (B(V, 1, 1), T(K, 1, 1) + RV(3), none, none),
            (SQ(0, 0) + Q(13), T(V, 1, 1) + RV(4), none, none),
            (SQ(0, 1) + Q(14), NT(0, 0) + RV(5), G1(13), IS(12)),
            (SQ(1, 0) + Q(15), NT(0, 1) + SAH(0, 0, 1), G1(14), IS(14)),
            (SQ(1, 1) + RT(6), NT(1, 0) + SAH(1, 0, 1), G1(15), none),
            (RT(7), SA(2) + NT(1, 1) + SA(3), none, none),
            (none, SA(4, 5), none, none),
            (none, SA(6, 7), none, none),
        )
        for row in rows:
            weave(*row)
